import numpy as np
import ml_dtypes


def mxq(x, axis, fmt="e4m3"):
    dtype, down = {"e4m3": (ml_dtypes.float8_e4m3fn, 7), "e5m2": (ml_dtypes.float8_e5m2, 14)}[fmt]
    v = np.moveaxis(np.asarray(x, np.float32).astype(ml_dtypes.bfloat16).astype(np.float64), axis, -1)
    blocks = v.reshape(v.shape[:-1] + (-1, 32))
    amax = np.abs(blocks).max(-1, keepdims=True)
    byte = np.maximum(np.where(amax > 0, np.frexp(amax)[1] - 1 + 127, 0) - down, 1)
    scale = np.exp2(byte - 127.0)
    codes = (blocks / scale).astype(np.float32).astype(dtype).astype(np.float64)
    return np.moveaxis((codes * scale).reshape(v.shape), -1, axis)


WIDE = False


def mx_kscale(k):
    if not WIDE:
        return np.ones(k)
    levels = np.array([10, -10, 5, -5, 0])
    a = np.random.permutation(np.resize(levels, k // 512 * 4)).reshape(k // 512, 4)
    idx = np.arange(k)
    return np.exp2(a[idx // 512, idx % 128 // 32])


BF16 = ml_dtypes.bfloat16


def bf(x):
    return np.asarray(x, np.float32).astype(BF16)


def f64(x):
    return np.asarray(x).astype(np.float64)


E2M1 = np.array([0.0, 0.5, 1.0, 1.5, 2.0, 3.0, 4.0, 6.0, -0.0, -0.5, -1.0, -1.5, -2.0, -3.0, -4.0, -6.0])


def pack_weight(w, fmt):
    k, n = w.shape
    w = f64(bf(w)).reshape(k // 32, 32, n)
    amax = np.abs(w).max(1)
    if fmt == "e4m3":
        byte = np.frexp(amax)[1] - 1 + 127 - 7
    else:
        mant, ex = np.frexp(amax / 6.0)
        byte = np.where(mant > 0.5, ex, ex - 1) + 127
    byte = np.clip(np.where(amax > 0, byte, 1), 1, 254)
    scaled = (w * np.exp2(127.0 - byte)[:, None, :]).reshape(k, n).astype(np.float32)
    by_word = np.ascontiguousarray(scaled.reshape(k // 512, 128, 4, n).transpose(0, 1, 3, 2))
    if fmt == "e4m3":
        words = by_word.astype(ml_dtypes.float8_e4m3fn).view(np.uint8)
    else:
        c = by_word.astype(ml_dtypes.float4_e2m1fn).view(np.uint8) & 0xF
        words = c[..., 0::2] | (c[..., 1::2] << 4)
    return np.ascontiguousarray(words), np.ascontiguousarray(byte.astype(np.uint8).reshape(k // 512, 16, n))


def unpack_weight(words, scales, fmt):
    g, p, n, _ = words.shape
    if fmt == "e4m3":
        vals = np.ascontiguousarray(words).view(ml_dtypes.float8_e4m3fn).astype(np.float64)
    else:
        nib = np.empty((g, p, n, 4), np.uint8)
        nib[..., 0::2] = words & 0xF
        nib[..., 1::2] = words >> 4
        vals = E2M1[nib]
    vals = vals * np.repeat(np.exp2(scales.astype(np.float64) - 127.0), 8, axis=1)[..., None]
    return vals.transpose(0, 1, 3, 2).reshape(g * 512, n)


B, T, HID, H, D, QB = 4, 1024, 1024, 4, 128, 512
LN_EPS = 1e-5
FMT = "e4m3"


def layer_norm(u):
    mu = u.mean(-1, keepdims=True)
    var = ((u - mu) ** 2).mean(-1, keepdims=True)
    return (u - mu) * (1.0 / np.sqrt(var + LN_EPS))


def feature_map(u, gamma, beta):
    return layer_norm(u * gamma + beta)


def setup_inputs():
    s = mx_kscale(HID)
    hidden_states = bf(np.random.standard_normal((B, T, HID)) * s)
    wq = np.random.standard_normal((H * D, HID)) / np.sqrt(HID) / s
    wk = np.random.standard_normal((H * D, HID)) / np.sqrt(HID) / s
    gamma = bf(1.0 + 0.1 * np.random.standard_normal(D))
    beta = bf(0.1 * np.random.standard_normal(D))
    wq_words, wq_scales = pack_weight(np.ascontiguousarray(wq.T), FMT)
    wk_words, wk_scales = pack_weight(np.ascontiguousarray(wk.T), FMT)
    return {"hidden_states": hidden_states,
            "Wq_words": wq_words,
            "Wq_scales": wq_scales,
            "Wk_words": wk_words,
            "Wk_scales": wk_scales,
            "gamma": gamma,
            "beta": beta}


def reference(hidden_states, Wq_words, Wq_scales, Wk_words, Wk_scales, gamma, beta):
    g, b = f64(gamma), f64(beta)
    xq = mxq(f64(hidden_states), 2, "e4m3")
    q = (xq @ unpack_weight(Wq_words, Wq_scales, FMT)).reshape(B, T, H, D)
    k = (xq @ unpack_weight(Wk_words, Wk_scales, FMT)).reshape(B, T, H, D)
    q_feat = feature_map(q, g, b) * (D ** -0.5)
    k_feat = feature_map(k, g, b)
    return q_feat, k_feat

@@ -1,0 +1,204 @@
+from contextlib import ExitStack
+
+import concourse.bass as bass
+import concourse.mybir as mybir
+import concourse.tile as tile
+from concourse.masks import make_identity
+
+BF16 = mybir.dt.bfloat16
+F32 = mybir.dt.float32
+I32 = mybir.dt.int32
+U32 = mybir.dt.uint32
+U8 = mybir.dt.uint8
+FP8X4 = mybir.dt.float8_e4m3fn_x4
+ALU = mybir.AluOpType
+ACT = mybir.ActivationFunctionType
+
+P = 128
+TOKENS = 4 * 1024
+HID = 1024
+K_PASS = 512
+PASSES = HID // K_PASS
+HEADS = 4
+D = 128
+COLS = HEADS * D
+LN_EPS = 1e-5
+N_TILES = TOKENS // P
+
+FLOPS = 2 * TOKENS * HID * 2 * COLS
+
+
+def tile_rebasedlinearattention_pa_t_kernel(
+    tc, hidden_states, Wq_words, Wq_scales, Wk_words, Wk_scales, gamma, beta, out_0, out_1
+):
+    nc = tc.nc
+    x_rows = hidden_states.rearrange("b t k -> (b t) k")
+    out_rows = [o.rearrange("b t h d -> (b t) (h d)") for o in (out_0, out_1)]
+
+    with ExitStack() as ctx:
+        const = ctx.enter_context(tc.tile_pool(name="const", bufs=1))
+        x_pool = ctx.enter_context(tc.tile_pool(name="x", bufs=N_TILES))
+        stage = ctx.enter_context(tc.tile_pool(name="stage", bufs=3))
+        z_pool = ctx.enter_context(tc.tile_pool(name="z", bufs=6))
+        feat_pool = ctx.enter_context(tc.tile_pool(name="feat", bufs=3))
+        small = ctx.enter_context(tc.tile_pool(name="small", bufs=4))
+        psum_x = ctx.enter_context(tc.psum_pool(name="psum_x", bufs=2))
+        psum_o = ctx.enter_context(tc.psum_pool(name="psum_o", bufs=6))
+
+        ident = const.tile([P, P], F32)
+        make_identity(nc, ident[:])
+
+        w_planes = const.tile([P, 2, PASSES, COLS], U8, align_bytes=64)
+        nc.vector.memset(w_planes[:].rearrange("p w g n -> p (w g n)").bitcast(I32), 0)
+        w_codes = const.tile([P, 2, PASSES, COLS], U32, align_bytes=64)
+        eps = const.tile([P, 2], F32)
+        nc.vector.memset(eps[:, 0:1], D * LN_EPS)
+        nc.vector.memset(eps[:, 1:2], LN_EPS)
+
+        x_tiles = []
+        for t in range(N_TILES):
+            x_sb = x_pool.tile([P, HID], BF16, name="x_sb")
+            x_tiles.append(x_sb)
+
+        nc.sync.dma_start(out=x_tiles[0][:], in_=x_rows[0:P, :])
+        for w, words in enumerate((Wq_words, Wk_words)):
+            nc.sync.dma_start(
+                out=w_codes[:, w].bitcast(I32),
+                in_=words.rearrange("g p n t -> p g (n t)").bitcast(I32),
+            )
+        for w, scales in enumerate((Wq_scales, Wk_scales)):
+            for quad in range(4):
+                nc.sync.dma_start(
+                    out=w_planes[32 * quad : 32 * quad + 4, w].bitcast(I32),
+                    in_=scales[:, 4 * quad : 4 * quad + 4, :].rearrange("g r n -> r g n").bitcast(I32),
+                )
+        gb_bf = const.tile([P, 2, D], BF16)
+        nc.sync.dma_start(out=gb_bf[:, 0, :], in_=gamma.partition_broadcast(P))
+        nc.sync.dma_start(out=gb_bf[:, 1, :], in_=beta.partition_broadcast(P))
+        gb = const.tile([P, 2, D], F32)
+        nc.vector.tensor_copy(out=gb[:], in_=gb_bf[:])
+        for t in range(1, N_TILES):
+            nc.sync.dma_start(out=x_tiles[t][:], in_=x_rows[t * P : (t + 1) * P, :])
+
+        gamma_heads = gb[:, 0, :].unsqueeze(1).to_broadcast([P, HEADS, D])
+        beta_heads = gb[:, 1, :].unsqueeze(1).to_broadcast([P, 2 * HEADS, D])
+
+        xt, grouped, x_codes, x_planes, acc, z = {}, {}, {}, {}, {}, {}
+        stats, std, rstd, shift = {}, {}, {}, {}
+
+        def transpose_x(t):
+            x_words = x_tiles[t][:].bitcast(F32)
+            xt[t] = psum_x.tile([P, PASSES * 2, P], F32, name="xt")
+            for g in range(PASSES):
+                for u in range(2):
+                    nc.tensor.transpose(
+                        xt[t][:, 2 * g + u, :],
+                        x_words[:, 256 * g + u : 256 * (g + 1) : 2],
+                        ident[:],
+                    )
+
+        def copy_x(t):
+            grouped[t] = stage.tile([P, PASSES, P, 4], BF16, align_bytes=64, name="grouped")
+            grouped_words = (
+                grouped[t][:]
+                .rearrange("p g r t -> p (g r t)")
+                .bitcast(F32)
+                .rearrange("p (g r u) -> p g r u", g=PASSES, u=2)
+            )
+            nc.scalar.copy(out=grouped_words, in_=xt[t][:].rearrange("p (g u) r -> p g r u", u=2))
+
+        def quantise_x(t):
+            x_codes[t] = stage.tile([P, PASSES, P], U32, align_bytes=64, name="x_codes")
+            x_planes[t] = stage.tile([P, PASSES, P], U8, align_bytes=64, name="x_planes")
+            nc.vector.quantize_mx(
+                out=x_codes[t][:].rearrange("p g r -> p (g r)").bitcast(FP8X4),
+                scales=x_planes[t][:].rearrange("p g r -> p (g r)"),
+                in_=grouped[t][:].rearrange("p g r t -> p (g r t)"),
+            )
+
+        def project(t):
+            for w in range(2):
+                acc[t, w] = psum_o.tile([P, COLS], F32, name="acc")
+                for g in range(PASSES):
+                    nc.tensor.matmul_mx(
+                        out=acc[t, w][:],
+                        lhsT=x_codes[t][:, g, :].bitcast(FP8X4),
+                        lhsT_scale=x_planes[t][:, g, :],
+                        rhs=w_codes[:, w, g, :].bitcast(FP8X4),
+                        rhs_scale=w_planes[:, w, g, :],
+                        start=(g == 0),
+                        stop=(g == PASSES - 1),
+                    )
+
+        def times_gamma(t):
+            z[t] = z_pool.tile([P, 2 * HEADS, D], F32, name="z")
+            for w in range(2):
+                nc.vector.tensor_tensor(
+                    out=z[t][:, w * HEADS : (w + 1) * HEADS, :],
+                    in0=acc[t, w][:].rearrange("p (h d) -> p h d", h=HEADS),
+                    in1=gamma_heads,
+                    op=ALU.mult,
+                )
+
+        def plus_beta(t):
+            nc.gpsimd.tensor_tensor(out=z[t][:], in0=z[t][:], in1=beta_heads, op=ALU.add)
+
+        def moments(t):
+            stats[t] = small.tile([P, HEADS, 6], F32, name="stats")
+            for a in range(HEADS):
+                nc.vector.bn_stats(
+                    out=stats[t][:, a, :],
+                    in_=z[t][:, 2 * a : 2 * a + 2, :].rearrange("p h d -> p d h"),
+                )
+
+        def root(t):
+            by_head = stats[t][:].rearrange("p a (h s) -> p (a h) s", s=3)
+            std[t] = small.tile([P, 2 * HEADS], F32, name="std")
+            nc.scalar.activation(
+                out=std[t][:, 0:HEADS], in_=by_head[:, 0:HEADS, 2], func=ACT.Sqrt,
+                bias=eps[:, 0:1], scale=1.0,
+            )
+            nc.scalar.activation(
+                out=std[t][:, HEADS:], in_=by_head[:, HEADS:, 2], func=ACT.Sqrt,
+                bias=eps[:, 1:2], scale=1.0 / D,
+            )
+
+        def scale_and_shift(t):
+            by_head = stats[t][:].rearrange("p a (h s) -> p (a h) s", s=3)
+            rstd[t] = small.tile([P, 2 * HEADS], F32, name="rstd")
+            nc.vector.reciprocal(out=rstd[t][:], in_=std[t][:])
+            shift[t] = small.tile([P, 2 * HEADS], F32, name="shift")
+            nc.vector.scalar_tensor_tensor(
+                out=shift[t][:], in0=by_head[:, :, 1], scalar=-1.0, in1=rstd[t][:],
+                op0=ALU.mult, op1=ALU.mult,
+            )
+
+        def normalise_and_store(t):
+            feat = feat_pool.tile([P, 2 * HEADS, D], F32, name="feat")
+            for h in range(2 * HEADS):
+                nc.scalar.activation(
+                    out=feat[:, h, :], in_=z[t][:, h, :], func=ACT.Identity,
+                    bias=shift[t][:, h : h + 1], scale=rstd[t][:, h : h + 1],
+                )
+            for w in range(2):
+                nc.scalar.dma_start(
+                    out=out_rows[w][t * P : (t + 1) * P, :],
+                    in_=feat[:, w * HEADS : (w + 1) * HEADS, :].rearrange("p h d -> p (h d)"),
+                )
+
+        def run(stage_of_tile, t):
+            if 0 <= t < N_TILES:
+                stage_of_tile(t)
+
+        with tc.manual_schedule():
+            for i in range(-4, N_TILES + 4):
+                run(times_gamma, i)
+                run(plus_beta, i)
+                run(quantise_x, i + 2)
+                run(moments, i - 2)
+                run(scale_and_shift, i - 3)
+                run(project, i + 1)
+                run(transpose_x, i + 4)
+                run(copy_x, i + 3)
+                run(normalise_and_store, i - 4)
+                run(root, i - 2)

@@ -1,8 +1,6 @@
 from contextlib import ExitStack
 
-import concourse.bass as bass
 import concourse.mybir as mybir
-import concourse.tile as tile
 from concourse.masks import make_identity
 
 BF16 = mybir.dt.bfloat16
@@ -24,6 +22,9 @@ D = 128
 COLS = HEADS * D
 LN_EPS = 1e-5
 N_TILES = TOKENS // P
+BLOCK = 512
+TILES_PER_BLOCK = BLOCK // P
+N_STEPS = N_TILES
 
 FLOPS = 2 * TOKENS * HID * 2 * COLS
 
@@ -38,12 +39,13 @@ def tile_rebasedlinearattention_pa_t_kernel(
     with ExitStack() as ctx:
         const = ctx.enter_context(tc.tile_pool(name="const", bufs=1))
         x_pool = ctx.enter_context(tc.tile_pool(name="x", bufs=N_TILES))
-        stage = ctx.enter_context(tc.tile_pool(name="stage", bufs=3))
-        z_pool = ctx.enter_context(tc.tile_pool(name="z", bufs=6))
-        feat_pool = ctx.enter_context(tc.tile_pool(name="feat", bufs=3))
+        stage = ctx.enter_context(tc.tile_pool(name="stage", bufs=2))
+        u_pool = ctx.enter_context(tc.tile_pool(name="u", bufs=3))
+        feat_pool = ctx.enter_context(tc.tile_pool(name="feat", bufs=8))
         small = ctx.enter_context(tc.tile_pool(name="small", bufs=4))
         psum_x = ctx.enter_context(tc.psum_pool(name="psum_x", bufs=2))
-        psum_o = ctx.enter_context(tc.psum_pool(name="psum_o", bufs=6))
+        psum_v = ctx.enter_context(tc.psum_pool(name="psum_v", bufs=2))
+        psum_u = ctx.enter_context(tc.psum_pool(name="psum_u", bufs=4))
 
         ident = const.tile([P, P], F32)
         make_identity(nc, ident[:])
@@ -54,13 +56,18 @@ def tile_rebasedlinearattention_pa_t_kernel(
         eps = const.tile([P, 2], F32)
         nc.vector.memset(eps[:, 0:1], D * LN_EPS)
         nc.vector.memset(eps[:, 1:2], LN_EPS)
+        gb_rows = const.tile([P, P], BF16)
+        nc.vector.memset(gb_rows[:], 0.0)
 
         x_tiles = []
         for t in range(N_TILES):
             x_sb = x_pool.tile([P, HID], BF16, name="x_sb")
             x_tiles.append(x_sb)
 
-        nc.sync.dma_start(out=x_tiles[0][:], in_=x_rows[0:P, :])
+        for t in range(TILES_PER_BLOCK):
+            nc.sync.dma_start(out=x_tiles[t][:], in_=x_rows[t * P : (t + 1) * P, :])
+        nc.sync.dma_start(out=gb_rows[0:1, :], in_=gamma.rearrange("(o d) -> o d", o=1))
+        nc.sync.dma_start(out=gb_rows[1:2, :], in_=beta.rearrange("(o d) -> o d", o=1))
         for w, words in enumerate((Wq_words, Wk_words)):
             nc.sync.dma_start(
                 out=w_codes[:, w].bitcast(I32),
@@ -72,18 +79,17 @@ def tile_rebasedlinearattention_pa_t_kernel(
                     out=w_planes[32 * quad : 32 * quad + 4, w].bitcast(I32),
                     in_=scales[:, 4 * quad : 4 * quad + 4, :].rearrange("g r n -> r g n").bitcast(I32),
                 )
-        gb_bf = const.tile([P, 2, D], BF16)
-        nc.sync.dma_start(out=gb_bf[:, 0, :], in_=gamma.partition_broadcast(P))
-        nc.sync.dma_start(out=gb_bf[:, 1, :], in_=beta.partition_broadcast(P))
-        gb = const.tile([P, 2, D], F32)
-        nc.vector.tensor_copy(out=gb[:], in_=gb_bf[:])
-        for t in range(1, N_TILES):
+        for t in range(TILES_PER_BLOCK, N_TILES):
             nc.sync.dma_start(out=x_tiles[t][:], in_=x_rows[t * P : (t + 1) * P, :])
 
-        gamma_heads = gb[:, 0, :].unsqueeze(1).to_broadcast([P, HEADS, D])
-        beta_heads = gb[:, 1, :].unsqueeze(1).to_broadcast([P, 2 * HEADS, D])
+        gb_square = const.tile([P, P], F32)
+        nc.vector.tensor_copy(out=gb_square[:], in_=gb_rows[:])
+        gb_t = psum_x.tile([P, PASSES * 2, P], F32, name="xt")
+        nc.tensor.transpose(gb_t[:, 0, :], gb_square[:], ident[:])
+        gb = const.tile([P, 2], F32)
+        nc.vector.tensor_copy(out=gb[:], in_=gb_t[:, 0, 0:2])
 
-        xt, grouped, x_codes, x_planes, acc, z = {}, {}, {}, {}, {}, {}
+        xt, grouped, x_codes, x_planes, vt, u_t, ub = {}, {}, {}, {}, {}, {}, {}
         stats, std, rstd, shift = {}, {}, {}, {}
 
         def transpose_x(t):
@@ -98,107 +104,130 @@ def tile_rebasedlinearattention_pa_t_kernel(
                     )
 
         def copy_x(t):
-            grouped[t] = stage.tile([P, PASSES, P, 4], BF16, align_bytes=64, name="grouped")
+            b, j = divmod(t, TILES_PER_BLOCK)
+            if j == 0:
+                grouped[b] = stage.tile([P, PASSES, BLOCK, 4], BF16, align_bytes=64, name="grouped")
             grouped_words = (
-                grouped[t][:]
+                grouped[b][:]
                 .rearrange("p g r t -> p (g r t)")
                 .bitcast(F32)
                 .rearrange("p (g r u) -> p g r u", g=PASSES, u=2)
             )
-            nc.scalar.copy(out=grouped_words, in_=xt[t][:].rearrange("p (g u) r -> p g r u", u=2))
-
-        def quantise_x(t):
-            x_codes[t] = stage.tile([P, PASSES, P], U32, align_bytes=64, name="x_codes")
-            x_planes[t] = stage.tile([P, PASSES, P], U8, align_bytes=64, name="x_planes")
-            nc.vector.quantize_mx(
-                out=x_codes[t][:].rearrange("p g r -> p (g r)").bitcast(FP8X4),
-                scales=x_planes[t][:].rearrange("p g r -> p (g r)"),
-                in_=grouped[t][:].rearrange("p g r t -> p (g r t)"),
+            nc.vector.tensor_copy(
+                out=grouped_words[:, :, j * P : (j + 1) * P, :],
+                in_=xt[t][:].rearrange("p (g u) r -> p g r u", u=2),
             )
 
-        def project(t):
-            for w in range(2):
-                acc[t, w] = psum_o.tile([P, COLS], F32, name="acc")
+        def quantise_x(b, g):
+            if g == 0:
+                x_codes[b] = stage.tile([P, PASSES, BLOCK], U32, align_bytes=64, name="x_codes")
+                x_planes[b] = stage.tile([P, PASSES, BLOCK], U8, align_bytes=64, name="x_planes")
+            nc.vector.quantize_mx(
+                out=x_codes[b][:, g, :].bitcast(FP8X4),
+                scales=x_planes[b][:, g, :],
+                in_=grouped[b][:, g].rearrange("p r t -> p (r t)"),
+            )
+
+        def project(s):
+            phase, half = divmod(s, 2)
+            b, w = divmod(phase, 2)
+            if half == 0:
+                u_t[phase] = u_pool.tile([P, HEADS, BLOCK], F32, name="u_t")
+            for h in (2 * half, 2 * half + 1):
+                vt[s, h] = psum_v.tile([P, BLOCK], F32, name="vt")
                 for g in range(PASSES):
                     nc.tensor.matmul_mx(
-                        out=acc[t, w][:],
-                        lhsT=x_codes[t][:, g, :].bitcast(FP8X4),
-                        lhsT_scale=x_planes[t][:, g, :],
-                        rhs=w_codes[:, w, g, :].bitcast(FP8X4),
-                        rhs_scale=w_planes[:, w, g, :],
+                        out=vt[s, h][:],
+                        lhsT=w_codes[:, w, g, h * D : (h + 1) * D].bitcast(FP8X4),
+                        lhsT_scale=w_planes[:, w, g, h * D : (h + 1) * D],
+                        rhs=x_codes[b][:, g, :].bitcast(FP8X4),
+                        rhs_scale=x_planes[b][:, g, :],
                         start=(g == 0),
                         stop=(g == PASSES - 1),
                     )
-
-        def times_gamma(t):
-            z[t] = z_pool.tile([P, 2 * HEADS, D], F32, name="z")
-            for w in range(2):
-                nc.vector.tensor_tensor(
-                    out=z[t][:, w * HEADS : (w + 1) * HEADS, :],
-                    in0=acc[t, w][:].rearrange("p (h d) -> p h d", h=HEADS),
-                    in1=gamma_heads,
-                    op=ALU.mult,
+                nc.scalar.activation(
+                    out=u_t[phase][:, h, :], in_=vt[s, h][:], func=ACT.Identity,
+                    bias=gb[:, 1:2], scale=gb[:, 0:1],
                 )
 
-        def plus_beta(t):
-            nc.gpsimd.tensor_tensor(out=z[t][:], in0=z[t][:], in1=beta_heads, op=ALU.add)
+        def transpose_back(s):
+            phase, half = divmod(s, 2)
+            for k in range(2):
+                j = 2 * half + k
+                ub[s, k] = psum_u.tile([P, HEADS, D], F32, name="ub")
+                for h in range(HEADS):
+                    nc.tensor.transpose(
+                        ub[s, k][:, h, :], u_t[phase][:, h, j * P : (j + 1) * P], ident[:]
+                    )
 
-        def moments(t):
-            stats[t] = small.tile([P, HEADS, 6], F32, name="stats")
-            for a in range(HEADS):
-                nc.vector.bn_stats(
-                    out=stats[t][:, a, :],
-                    in_=z[t][:, 2 * a : 2 * a + 2, :].rearrange("p h d -> p d h"),
-                )
+        def moments(s):
+            stats[s] = small.tile([P, 2, HEADS // 2, 6], F32, name="stats")
+            for k in range(2):
+                for a in range(HEADS // 2):
+                    nc.vector.bn_stats(
+                        out=stats[s][:, k, a, :],
+                        in_=ub[s, k][:, 2 * a : 2 * a + 2, :].rearrange("p h d -> p d h"),
+                    )
 
-        def root(t):
-            by_head = stats[t][:].rearrange("p a (h s) -> p (a h) s", s=3)
-            std[t] = small.tile([P, 2 * HEADS], F32, name="std")
+        def root(s):
+            w = (s // 2) % 2
+            by_head = stats[s][:].rearrange("p k a (h c) -> p (k a h) c", c=3)
+            std[s] = small.tile([P, 2 * HEADS], F32, name="std")
             nc.scalar.activation(
-                out=std[t][:, 0:HEADS], in_=by_head[:, 0:HEADS, 2], func=ACT.Sqrt,
-                bias=eps[:, 0:1], scale=1.0,
-            )
-            nc.scalar.activation(
-                out=std[t][:, HEADS:], in_=by_head[:, HEADS:, 2], func=ACT.Sqrt,
-                bias=eps[:, 1:2], scale=1.0 / D,
+                out=std[s][:], in_=by_head[:, :, 2], func=ACT.Sqrt,
+                bias=eps[:, w : w + 1], scale=(1.0 if w == 0 else 1.0 / D),
             )
 
-        def scale_and_shift(t):
-            by_head = stats[t][:].rearrange("p a (h s) -> p (a h) s", s=3)
-            rstd[t] = small.tile([P, 2 * HEADS], F32, name="rstd")
-            nc.vector.reciprocal(out=rstd[t][:], in_=std[t][:])
-            shift[t] = small.tile([P, 2 * HEADS], F32, name="shift")
+        def scale_and_shift(s):
+            by_head = stats[s][:].rearrange("p k a (h c) -> p (k a h) c", c=3)
+            rstd[s] = small.tile([P, 2 * HEADS], F32, name="rstd")
+            nc.vector.reciprocal(out=rstd[s][:], in_=std[s][:])
+            shift[s] = small.tile([P, 2 * HEADS], F32, name="shift")
             nc.vector.scalar_tensor_tensor(
-                out=shift[t][:], in0=by_head[:, :, 1], scalar=-1.0, in1=rstd[t][:],
+                out=shift[s][:], in0=by_head[:, :, 1], scalar=-1.0, in1=rstd[s][:],
                 op0=ALU.mult, op1=ALU.mult,
             )
 
-        def normalise_and_store(t):
-            feat = feat_pool.tile([P, 2 * HEADS, D], F32, name="feat")
-            for h in range(2 * HEADS):
-                nc.scalar.activation(
-                    out=feat[:, h, :], in_=z[t][:, h, :], func=ACT.Identity,
-                    bias=shift[t][:, h : h + 1], scale=rstd[t][:, h : h + 1],
-                )
-            for w in range(2):
-                nc.scalar.dma_start(
+        def normalise_and_store(s):
+            phase, half = divmod(s, 2)
+            b, w = divmod(phase, 2)
+            by_head = stats[s][:].rearrange("p k a (h c) -> p (k a h) c", c=3)
+            for k in range(2):
+                t = b * TILES_PER_BLOCK + 2 * half + k
+                feat = feat_pool.tile([P, HEADS, D], F32, name="feat")
+                on_vector = k == 1 and half == 1
+                for h in range(HEADS):
+                    c = k * HEADS + h
+                    if on_vector:
+                        nc.vector.tensor_scalar(
+                            out=feat[:, h, :], in0=ub[s, k][:, h, :],
+                            scalar1=by_head[:, c, 1:2], scalar2=rstd[s][:, c : c + 1],
+                            op0=ALU.subtract, op1=ALU.mult,
+                        )
+                    else:
+                        nc.scalar.activation(
+                            out=feat[:, h, :], in_=ub[s, k][:, h, :], func=ACT.Identity,
+                            bias=shift[s][:, c : c + 1], scale=rstd[s][:, c : c + 1],
+                        )
+                nc.sync.dma_start(
                     out=out_rows[w][t * P : (t + 1) * P, :],
-                    in_=feat[:, w * HEADS : (w + 1) * HEADS, :].rearrange("p h d -> p (h d)"),
+                    in_=feat[:].rearrange("p h d -> p (h d)"),
                 )
 
-        def run(stage_of_tile, t):
-            if 0 <= t < N_TILES:
-                stage_of_tile(t)
+        def run(stage_fn, i, n):
+            if 0 <= i < n:
+                stage_fn(i)
 
         with tc.manual_schedule():
-            for i in range(-4, N_TILES + 4):
-                run(times_gamma, i)
-                run(plus_beta, i)
-                run(quantise_x, i + 2)
-                run(moments, i - 2)
-                run(scale_and_shift, i - 3)
-                run(project, i + 1)
-                run(transpose_x, i + 4)
-                run(copy_x, i + 3)
-                run(normalise_and_store, i - 4)
-                run(root, i - 2)
+            for s in range(-7, N_STEPS + 3):
+                run(root, s - 3, N_STEPS)
+                run(scale_and_shift, s - 3, N_STEPS)
+                run(project, s, N_STEPS)
+                run(normalise_and_store, s - 3, N_STEPS)
+                run(transpose_back, s - 2, N_STEPS)
+                run(transpose_x, s + 7, N_TILES)
+                run(copy_x, s + 6, N_TILES)
+                b, g = divmod(s + 2, TILES_PER_BLOCK)
+                if g < PASSES and 0 <= b < N_TILES // TILES_PER_BLOCK:
+                    quantise_x(b, g)
+                run(moments, s - 2, N_STEPS)

@@ -22,9 +22,9 @@ D = 128
 COLS = HEADS * D
 LN_EPS = 1e-5
 N_TILES = TOKENS // P
-BLOCK = 512
-TILES_PER_BLOCK = BLOCK // P
-N_STEPS = N_TILES
+CHUNK = 256
+TILES_PER_CHUNK = CHUNK // P
+N_STEPS = 2 * (TOKENS // CHUNK)
 
 FLOPS = 2 * TOKENS * HID * 2 * COLS
 
@@ -39,10 +39,10 @@ def tile_rebasedlinearattention_pa_t_kernel(
     with ExitStack() as ctx:
         const = ctx.enter_context(tc.tile_pool(name="const", bufs=1))
         x_pool = ctx.enter_context(tc.tile_pool(name="x", bufs=N_TILES))
-        stage = ctx.enter_context(tc.tile_pool(name="stage", bufs=2))
+        stage = ctx.enter_context(tc.tile_pool(name="stage", bufs=3))
         u_pool = ctx.enter_context(tc.tile_pool(name="u", bufs=3))
         feat_pool = ctx.enter_context(tc.tile_pool(name="feat", bufs=8))
-        small = ctx.enter_context(tc.tile_pool(name="small", bufs=4))
+        small = ctx.enter_context(tc.tile_pool(name="small", bufs=8))
         psum_x = ctx.enter_context(tc.psum_pool(name="psum_x", bufs=2))
         psum_v = ctx.enter_context(tc.psum_pool(name="psum_v", bufs=2))
         psum_u = ctx.enter_context(tc.psum_pool(name="psum_u", bufs=4))
@@ -64,23 +64,30 @@ def tile_rebasedlinearattention_pa_t_kernel(
             x_sb = x_pool.tile([P, HID], BF16, name="x_sb")
             x_tiles.append(x_sb)
 
-        for t in range(TILES_PER_BLOCK):
+        def load_x(t):
             nc.sync.dma_start(out=x_tiles[t][:], in_=x_rows[t * P : (t + 1) * P, :])
-        nc.sync.dma_start(out=gb_rows[0:1, :], in_=gamma.rearrange("(o d) -> o d", o=1))
-        nc.sync.dma_start(out=gb_rows[1:2, :], in_=beta.rearrange("(o d) -> o d", o=1))
-        for w, words in enumerate((Wq_words, Wk_words)):
+
+        def load_weight(w, words, scales):
             nc.sync.dma_start(
                 out=w_codes[:, w].bitcast(I32),
                 in_=words.rearrange("g p n t -> p g (n t)").bitcast(I32),
             )
-        for w, scales in enumerate((Wq_scales, Wk_scales)):
             for quad in range(4):
                 nc.sync.dma_start(
                     out=w_planes[32 * quad : 32 * quad + 4, w].bitcast(I32),
                     in_=scales[:, 4 * quad : 4 * quad + 4, :].rearrange("g r n -> r g n").bitcast(I32),
                 )
-        for t in range(TILES_PER_BLOCK, N_TILES):
-            nc.sync.dma_start(out=x_tiles[t][:], in_=x_rows[t * P : (t + 1) * P, :])
+
+        nc.sync.dma_start(out=gb_rows[0:1, :], in_=gamma.rearrange("(o d) -> o d", o=1))
+        nc.sync.dma_start(out=gb_rows[1:2, :], in_=beta.rearrange("(o d) -> o d", o=1))
+        load_x(0)
+        load_x(1)
+        load_weight(0, Wq_words, Wq_scales)
+        load_x(2)
+        load_x(3)
+        load_weight(1, Wk_words, Wk_scales)
+        for t in range(4, N_TILES):
+            load_x(t)
 
         gb_square = const.tile([P, P], F32)
         nc.vector.tensor_copy(out=gb_square[:], in_=gb_rows[:])
@@ -104,130 +111,145 @@ def tile_rebasedlinearattention_pa_t_kernel(
                     )
 
         def copy_x(t):
-            b, j = divmod(t, TILES_PER_BLOCK)
+            c, j = divmod(t, TILES_PER_CHUNK)
             if j == 0:
-                grouped[b] = stage.tile([P, PASSES, BLOCK, 4], BF16, align_bytes=64, name="grouped")
+                grouped[c] = stage.tile([P, PASSES, CHUNK, 4], BF16, align_bytes=64, name="grouped")
             grouped_words = (
-                grouped[b][:]
+                grouped[c][:]
                 .rearrange("p g r t -> p (g r t)")
                 .bitcast(F32)
                 .rearrange("p (g r u) -> p g r u", g=PASSES, u=2)
             )
-            nc.vector.tensor_copy(
+            nc.scalar.copy(
                 out=grouped_words[:, :, j * P : (j + 1) * P, :],
                 in_=xt[t][:].rearrange("p (g u) r -> p g r u", u=2),
             )
 
-        def quantise_x(b, g):
+        def quantise_x(i):
+            c, g = divmod(i, PASSES)
             if g == 0:
-                x_codes[b] = stage.tile([P, PASSES, BLOCK], U32, align_bytes=64, name="x_codes")
-                x_planes[b] = stage.tile([P, PASSES, BLOCK], U8, align_bytes=64, name="x_planes")
+                x_codes[c] = stage.tile([P, PASSES, CHUNK], U32, align_bytes=64, name="x_codes")
+                x_planes[c] = stage.tile([P, PASSES, CHUNK], U8, align_bytes=64, name="x_planes")
             nc.vector.quantize_mx(
-                out=x_codes[b][:, g, :].bitcast(FP8X4),
-                scales=x_planes[b][:, g, :],
-                in_=grouped[b][:, g].rearrange("p r t -> p (r t)"),
+                out=x_codes[c][:, g, :].bitcast(FP8X4),
+                scales=x_planes[c][:, g, :],
+                in_=grouped[c][:, g].rearrange("p r t -> p (r t)"),
             )
 
         def project(s):
-            phase, half = divmod(s, 2)
-            b, w = divmod(phase, 2)
-            if half == 0:
-                u_t[phase] = u_pool.tile([P, HEADS, BLOCK], F32, name="u_t")
-            for h in (2 * half, 2 * half + 1):
-                vt[s, h] = psum_v.tile([P, BLOCK], F32, name="vt")
-                for g in range(PASSES):
-                    nc.tensor.matmul_mx(
-                        out=vt[s, h][:],
-                        lhsT=w_codes[:, w, g, h * D : (h + 1) * D].bitcast(FP8X4),
-                        lhsT_scale=w_planes[:, w, g, h * D : (h + 1) * D],
-                        rhs=x_codes[b][:, g, :].bitcast(FP8X4),
-                        rhs_scale=x_planes[b][:, g, :],
-                        start=(g == 0),
-                        stop=(g == PASSES - 1),
-                    )
+            c, w = divmod(s, 2)
+            for pair in range(HEADS // 2):
+                vt[s, pair] = psum_v.tile([P, 2, CHUNK], F32, name="vt")
+                for i in range(2):
+                    h = 2 * pair + i
+                    for g in range(PASSES):
+                        nc.tensor.matmul_mx(
+                            out=vt[s, pair][:, i, :],
+                            lhsT=w_codes[:, w, g, h * D : (h + 1) * D].bitcast(FP8X4),
+                            lhsT_scale=w_planes[:, w, g, h * D : (h + 1) * D],
+                            rhs=x_codes[c][:, g, :].bitcast(FP8X4),
+                            rhs_scale=x_planes[c][:, g, :],
+                            start=(g == 0),
+                            stop=(g == PASSES - 1),
+                        )
+
+        def affine(s):
+            u_t[s] = u_pool.tile([P, HEADS, CHUNK], F32, name="u_t")
+            for pair in range(HEADS // 2):
                 nc.scalar.activation(
-                    out=u_t[phase][:, h, :], in_=vt[s, h][:], func=ACT.Identity,
-                    bias=gb[:, 1:2], scale=gb[:, 0:1],
+                    out=u_t[s][:, 2 * pair : 2 * pair + 2, :], in_=vt[s, pair][:],
+                    func=ACT.Identity, bias=gb[:, 1:2], scale=gb[:, 0:1],
                 )
 
         def transpose_back(s):
-            phase, half = divmod(s, 2)
-            for k in range(2):
-                j = 2 * half + k
-                ub[s, k] = psum_u.tile([P, HEADS, D], F32, name="ub")
+            for j in range(TILES_PER_CHUNK):
+                ub[s, j] = psum_u.tile([P, HEADS, D], F32, name="ub")
                 for h in range(HEADS):
                     nc.tensor.transpose(
-                        ub[s, k][:, h, :], u_t[phase][:, h, j * P : (j + 1) * P], ident[:]
+                        ub[s, j][:, h, :], u_t[s][:, h, j * P : (j + 1) * P], ident[:]
                     )
 
-        def moments(s):
-            stats[s] = small.tile([P, 2, HEADS // 2, 6], F32, name="stats")
-            for k in range(2):
-                for a in range(HEADS // 2):
-                    nc.vector.bn_stats(
-                        out=stats[s][:, k, a, :],
-                        in_=ub[s, k][:, 2 * a : 2 * a + 2, :].rearrange("p h d -> p d h"),
-                    )
+        def moments(s, j):
+            stats[s, j] = small.tile([P, HEADS // 2, 6], F32, name="stats")
+            for a in range(HEADS // 2):
+                nc.vector.bn_stats(
+                    out=stats[s, j][:, a, :],
+                    in_=ub[s, j][:, 2 * a : 2 * a + 2, :].rearrange("p h d -> p d h"),
+                )
 
-        def root(s):
-            w = (s // 2) % 2
-            by_head = stats[s][:].rearrange("p k a (h c) -> p (k a h) c", c=3)
-            std[s] = small.tile([P, 2 * HEADS], F32, name="std")
+        def by_head(s, j):
+            return stats[s, j][:].rearrange("p a (h c) -> p (a h) c", c=3)
+
+        def root(s, j):
+            w = s % 2
+            std[s, j] = small.tile([P, HEADS], F32, name="std")
             nc.scalar.activation(
-                out=std[s][:], in_=by_head[:, :, 2], func=ACT.Sqrt,
+                out=std[s, j][:], in_=by_head(s, j)[:, :, 2], func=ACT.Sqrt,
                 bias=eps[:, w : w + 1], scale=(1.0 if w == 0 else 1.0 / D),
             )
 
-        def scale_and_shift(s):
-            by_head = stats[s][:].rearrange("p k a (h c) -> p (k a h) c", c=3)
-            rstd[s] = small.tile([P, 2 * HEADS], F32, name="rstd")
-            nc.vector.reciprocal(out=rstd[s][:], in_=std[s][:])
-            shift[s] = small.tile([P, 2 * HEADS], F32, name="shift")
+        def reciprocal(s, j):
+            rstd[s, j] = small.tile([P, HEADS], F32, name="rstd")
+            nc.vector.reciprocal(out=rstd[s, j][:], in_=std[s, j][:])
+
+        def minus_mean_over_std(s, j):
+            shift[s, j] = small.tile([P, HEADS], F32, name="shift")
             nc.vector.scalar_tensor_tensor(
-                out=shift[s][:], in0=by_head[:, :, 1], scalar=-1.0, in1=rstd[s][:],
+                out=shift[s, j][:], in0=by_head(s, j)[:, :, 1], scalar=-1.0, in1=rstd[s, j][:],
                 op0=ALU.mult, op1=ALU.mult,
             )
 
-        def normalise_and_store(s):
-            phase, half = divmod(s, 2)
-            b, w = divmod(phase, 2)
-            by_head = stats[s][:].rearrange("p k a (h c) -> p (k a h) c", c=3)
-            for k in range(2):
-                t = b * TILES_PER_BLOCK + 2 * half + k
-                feat = feat_pool.tile([P, HEADS, D], F32, name="feat")
-                on_vector = k == 1 and half == 1
-                for h in range(HEADS):
-                    c = k * HEADS + h
-                    if on_vector:
-                        nc.vector.tensor_scalar(
-                            out=feat[:, h, :], in0=ub[s, k][:, h, :],
-                            scalar1=by_head[:, c, 1:2], scalar2=rstd[s][:, c : c + 1],
-                            op0=ALU.subtract, op1=ALU.mult,
-                        )
-                    else:
-                        nc.scalar.activation(
-                            out=feat[:, h, :], in_=ub[s, k][:, h, :], func=ACT.Identity,
-                            bias=shift[s][:, c : c + 1], scale=rstd[s][:, c : c + 1],
-                        )
-                nc.sync.dma_start(
-                    out=out_rows[w][t * P : (t + 1) * P, :],
-                    in_=feat[:].rearrange("p h d -> p (h d)"),
-                )
+        def store(s, j, feat):
+            c, w = divmod(s, 2)
+            t = c * TILES_PER_CHUNK + j
+            nc.sync.dma_start(
+                out=out_rows[w][t * P : (t + 1) * P, :], in_=feat[:].rearrange("p h d -> p (h d)")
+            )
 
-        def run(stage_fn, i, n):
-            if 0 <= i < n:
-                stage_fn(i)
+        def normalise_on_scalar(s, j):
+            feat = feat_pool.tile([P, HEADS, D], F32, name="feat")
+            for h in range(HEADS):
+                nc.scalar.activation(
+                    out=feat[:, h, :], in_=ub[s, j][:, h, :], func=ACT.Identity,
+                    bias=shift[s, j][:, h : h + 1], scale=rstd[s, j][:, h : h + 1],
+                )
+            store(s, j, feat)
+
+        def normalise_on_vector(s, j):
+            feat = feat_pool.tile([P, HEADS, D], F32, name="feat")
+            for h in range(HEADS):
+                nc.vector.tensor_scalar(
+                    out=feat[:, h, :], in0=ub[s, j][:, h, :],
+                    scalar1=by_head(s, j)[:, h, 1:2], scalar2=rstd[s, j][:, h : h + 1],
+                    op0=ALU.subtract, op1=ALU.mult,
+                )
+            store(s, j, feat)
 
         with tc.manual_schedule():
-            for s in range(-7, N_STEPS + 3):
-                run(root, s - 3, N_STEPS)
-                run(scale_and_shift, s - 3, N_STEPS)
-                run(project, s, N_STEPS)
-                run(normalise_and_store, s - 3, N_STEPS)
-                run(transpose_back, s - 2, N_STEPS)
-                run(transpose_x, s + 7, N_TILES)
-                run(copy_x, s + 6, N_TILES)
-                b, g = divmod(s + 2, TILES_PER_BLOCK)
-                if g < PASSES and 0 <= b < N_TILES // TILES_PER_BLOCK:
-                    quantise_x(b, g)
-                run(moments, s - 2, N_STEPS)
+            for s in range(-5, N_STEPS + 2):
+                old, last = s - 2, s - 1
+                if 0 <= old < N_STEPS:
+                    root(old, 0)
+                if 0 <= s + 4 < N_TILES:
+                    copy_x(s + 4)
+                if 0 <= old < N_STEPS:
+                    root(old, 1)
+                    reciprocal(old, 0)
+                if 0 <= s + 2 < N_STEPS:
+                    quantise_x(s + 2)
+                if 0 <= old < N_STEPS:
+                    reciprocal(old, 1)
+                    minus_mean_over_std(old, 0)
+                    normalise_on_vector(old, 1)
+                if 0 <= s < N_STEPS:
+                    project(s)
+                    affine(s)
+                if 0 <= old < N_STEPS:
+                    normalise_on_scalar(old, 0)
+                if 0 <= last < N_STEPS:
+                    transpose_back(last)
+                if 0 <= s + 5 < N_TILES:
+                    transpose_x(s + 5)
+                if 0 <= last < N_STEPS:
+                    moments(last, 0)
+                    moments(last, 1)

@@ -58,6 +58,8 @@ def tile_rebasedlinearattention_pa_t_kernel(
         nc.vector.memset(eps[:, 1:2], LN_EPS)
         gb_rows = const.tile([P, P], BF16)
         nc.vector.memset(gb_rows[:], 0.0)
+        warm = const.tile([P, 2], F32)
+        nc.scalar.activation(out=warm[:], in_=eps[:], func=ACT.Abs_reciprocal_sqrt)
 
         x_tiles = []
         for t in range(N_TILES):
@@ -97,7 +99,7 @@ def tile_rebasedlinearattention_pa_t_kernel(
         nc.vector.tensor_copy(out=gb[:], in_=gb_t[:, 0, 0:2])
 
         xt, grouped, x_codes, x_planes, vt, u_t, ub = {}, {}, {}, {}, {}, {}, {}
-        stats, std, rstd, shift = {}, {}, {}, {}
+        stats, rstd, shift = {}, {}, {}
 
         def transpose_x(t):
             x_words = x_tiles[t][:].bitcast(F32)
@@ -120,10 +122,11 @@ def tile_rebasedlinearattention_pa_t_kernel(
                 .bitcast(F32)
                 .rearrange("p (g r u) -> p g r u", g=PASSES, u=2)
             )
-            nc.scalar.copy(
-                out=grouped_words[:, :, j * P : (j + 1) * P, :],
-                in_=xt[t][:].rearrange("p (g u) r -> p g r u", u=2),
-            )
+            planes = xt[t][:].rearrange("p (g u) r -> p g r u", u=2)
+            if j == 0:
+                nc.scalar.copy(out=grouped_words[:, :, j * P : (j + 1) * P, :], in_=planes)
+            else:
+                nc.vector.tensor_copy(out=grouped_words[:, :, j * P : (j + 1) * P, :], in_=planes)
 
         def quantise_x(i):
             c, g = divmod(i, PASSES)
@@ -180,17 +183,13 @@ def tile_rebasedlinearattention_pa_t_kernel(
         def by_head(s, j):
             return stats[s, j][:].rearrange("p a (h c) -> p (a h) c", c=3)
 
-        def root(s, j):
+        def one_over_std(s, j):
             w = s % 2
-            std[s, j] = small.tile([P, HEADS], F32, name="std")
+            rstd[s, j] = small.tile([P, HEADS], F32, name="rstd")
             nc.scalar.activation(
-                out=std[s, j][:], in_=by_head(s, j)[:, :, 2], func=ACT.Sqrt,
+                out=rstd[s, j][:], in_=by_head(s, j)[:, :, 2], func=ACT.Abs_reciprocal_sqrt,
                 bias=eps[:, w : w + 1], scale=(1.0 if w == 0 else 1.0 / D),
             )
-
-        def reciprocal(s, j):
-            rstd[s, j] = small.tile([P, HEADS], F32, name="rstd")
-            nc.vector.reciprocal(out=rstd[s, j][:], in_=std[s, j][:])
 
         def minus_mean_over_std(s, j):
             shift[s, j] = small.tile([P, HEADS], F32, name="shift")
@@ -228,17 +227,18 @@ def tile_rebasedlinearattention_pa_t_kernel(
         with tc.manual_schedule():
             for s in range(-5, N_STEPS + 2):
                 old, last = s - 2, s - 1
+                on_scalar = (s + 4) % TILES_PER_CHUNK == 0
                 if 0 <= old < N_STEPS:
-                    root(old, 0)
-                if 0 <= s + 4 < N_TILES:
+                    one_over_std(old, 0)
+                if 0 <= s + 4 < N_TILES and on_scalar:
                     copy_x(s + 4)
                 if 0 <= old < N_STEPS:
-                    root(old, 1)
-                    reciprocal(old, 0)
+                    one_over_std(old, 1)
                 if 0 <= s + 2 < N_STEPS:
                     quantise_x(s + 2)
+                if 0 <= s + 4 < N_TILES and not on_scalar:
+                    copy_x(s + 4)
                 if 0 <= old < N_STEPS:
-                    reciprocal(old, 1)
                     minus_mean_over_std(old, 0)
                     normalise_on_vector(old, 1)
                 if 0 <= s < N_STEPS:

@@ -21,12 +21,14 @@ HEADS = 4
 D = 128
 COLS = HEADS * D
 LN_EPS = 1e-5
-N_TILES = TOKENS // P
 CHUNK = 256
-TILES_PER_CHUNK = CHUNK // P
-N_STEPS = 2 * (TOKENS // CHUNK)
+TILES = CHUNK // P
+N_CHUNKS = TOKENS // CHUNK
 
 FLOPS = 2 * TOKENS * HID * 2 * COLS
+
+Q_ON_VECTOR = ((0, 0), (0, 1))
+K_ON_GPSIMD = ((1, 2), (1, 3))
 
 
 def tile_rebasedlinearattention_pa_t_kernel(
@@ -38,36 +40,44 @@ def tile_rebasedlinearattention_pa_t_kernel(
 
     with ExitStack() as ctx:
         const = ctx.enter_context(tc.tile_pool(name="const", bufs=1))
-        x_pool = ctx.enter_context(tc.tile_pool(name="x", bufs=N_TILES))
+        x_pool = ctx.enter_context(tc.tile_pool(name="x", bufs=6))
         stage = ctx.enter_context(tc.tile_pool(name="stage", bufs=3))
         u_pool = ctx.enter_context(tc.tile_pool(name="u", bufs=3))
-        feat_pool = ctx.enter_context(tc.tile_pool(name="feat", bufs=8))
-        small = ctx.enter_context(tc.tile_pool(name="small", bufs=8))
-        psum_x = ctx.enter_context(tc.psum_pool(name="psum_x", bufs=2))
+        k_pool = ctx.enter_context(tc.tile_pool(name="k", bufs=6))
+        feat_pool = ctx.enter_context(tc.tile_pool(name="feat", bufs=6))
+        small = ctx.enter_context(tc.tile_pool(name="small", bufs=6))
         psum_v = ctx.enter_context(tc.psum_pool(name="psum_v", bufs=2))
+        psum_s = ctx.enter_context(tc.psum_pool(name="psum_s", bufs=2))
         psum_u = ctx.enter_context(tc.psum_pool(name="psum_u", bufs=4))
 
         ident = const.tile([P, P], F32)
         make_identity(nc, ident[:])
-
         w_planes = const.tile([P, 2, PASSES, COLS], U8, align_bytes=64)
         nc.vector.memset(w_planes[:].rearrange("p w g n -> p (w g n)").bitcast(I32), 0)
         w_codes = const.tile([P, 2, PASSES, COLS], U32, align_bytes=64)
         eps = const.tile([P, 2], F32)
         nc.vector.memset(eps[:, 0:1], D * LN_EPS)
         nc.vector.memset(eps[:, 1:2], LN_EPS)
-        gb_rows = const.tile([P, P], BF16)
-        nc.vector.memset(gb_rows[:], 0.0)
+        gb_row = const.tile([P, 2 * D], BF16)
+        nc.vector.memset(gb_row[:], 0.0)
+        ones = const.tile([P, P], BF16)
+        nc.vector.memset(ones[:], 1.0)
         warm = const.tile([P, 2], F32)
         nc.scalar.activation(out=warm[:], in_=eps[:], func=ACT.Abs_reciprocal_sqrt)
+        gb = const.tile([P, 2], F32)
+        gamma_rows = const.tile([P, HEADS, D], F32)
+        beta_rows = const.tile([P, HEADS, D], F32)
 
-        x_tiles = []
-        for t in range(N_TILES):
-            x_sb = x_pool.tile([P, HID], BF16, name="x_sb")
-            x_tiles.append(x_sb)
+        x_sb, xt, grouped, x_codes, x_planes = {}, {}, {}, {}, {}
+        vt, u_t, ub, vk, t_sb, u_sb, feat = {}, {}, {}, {}, {}, {}, {}
+        stats, rstd, shift = {}, {}, {}
 
-        def load_x(t):
-            nc.sync.dma_start(out=x_tiles[t][:], in_=x_rows[t * P : (t + 1) * P, :])
+        def load_x(c):
+            x_sb[c] = x_pool.tile([P, TILES, HID], BF16, name="x_sb")
+            nc.sync.dma_start(
+                out=x_sb[c][:],
+                in_=x_rows[c * CHUNK : (c + 1) * CHUNK, :].rearrange("(j p) k -> p j k", p=P),
+            )
 
         def load_weight(w, words, scales):
             nc.sync.dma_start(
@@ -80,176 +90,221 @@ def tile_rebasedlinearattention_pa_t_kernel(
                     in_=scales[:, 4 * quad : 4 * quad + 4, :].rearrange("g r n -> r g n").bitcast(I32),
                 )
 
-        nc.sync.dma_start(out=gb_rows[0:1, :], in_=gamma.rearrange("(o d) -> o d", o=1))
-        nc.sync.dma_start(out=gb_rows[1:2, :], in_=beta.rearrange("(o d) -> o d", o=1))
-        load_x(0)
-        load_x(1)
-        load_weight(0, Wq_words, Wq_scales)
-        load_x(2)
-        load_x(3)
-        load_weight(1, Wk_words, Wk_scales)
-        for t in range(4, N_TILES):
-            load_x(t)
+        def load_gamma_beta():
+            nc.sync.dma_start(out=gb_row[0:1, 0:D], in_=gamma.rearrange("(o d) -> o d", o=1))
+            nc.sync.dma_start(out=gb_row[0:1, D : 2 * D], in_=beta.rearrange("(o d) -> o d", o=1))
 
-        gb_square = const.tile([P, P], F32)
-        nc.vector.tensor_copy(out=gb_square[:], in_=gb_rows[:])
-        gb_t = psum_x.tile([P, PASSES * 2, P], F32, name="xt")
-        nc.tensor.transpose(gb_t[:, 0, :], gb_square[:], ident[:])
-        gb = const.tile([P, 2], F32)
-        nc.vector.tensor_copy(out=gb[:], in_=gb_t[:, 0, 0:2])
+        def spread_gamma_beta():
+            for i, rows in enumerate((gamma_rows, beta_rows)):
+                bank = psum_u.tile([P, HEADS, D], F32, name="ub")
+                for h in range(HEADS):
+                    nc.tensor.matmul(out=bank[:, h, :], lhsT=ones[:], rhs=gb_row[:, i * D : (i + 1) * D], start=True, stop=True)
+                nc.vector.tensor_copy(out=rows[:], in_=bank[:])
+            bank = psum_u.tile([P, HEADS, D], F32, name="ub")
+            for i in range(2):
+                nc.tensor.matmul(out=bank[:, i, 0:2], lhsT=gb_row[:, i * D : (i + 1) * D], rhs=ones[:, 0:2], start=True, stop=True)
+            nc.vector.tensor_copy(out=gb[:], in_=bank[:, 0:2, 0])
 
-        xt, grouped, x_codes, x_planes, vt, u_t, ub = {}, {}, {}, {}, {}, {}, {}
-        stats, rstd, shift = {}, {}, {}
-
-        def transpose_x(t):
-            x_words = x_tiles[t][:].bitcast(F32)
-            xt[t] = psum_x.tile([P, PASSES * 2, P], F32, name="xt")
+        def transpose_x(c, j):
+            x_words = x_sb[c][:, j, :].bitcast(F32)
+            xt[c, j] = psum_s.tile([P, PASSES * 2, P], F32, name="shared")
             for g in range(PASSES):
                 for u in range(2):
-                    nc.tensor.transpose(
-                        xt[t][:, 2 * g + u, :],
-                        x_words[:, 256 * g + u : 256 * (g + 1) : 2],
-                        ident[:],
-                    )
+                    nc.tensor.transpose(xt[c, j][:, 2 * g + u, :], x_words[:, 256 * g + u : 256 * (g + 1) : 2], ident[:])
 
-        def copy_x(t):
-            c, j = divmod(t, TILES_PER_CHUNK)
+        def copy_x(c, j):
             if j == 0:
                 grouped[c] = stage.tile([P, PASSES, CHUNK, 4], BF16, align_bytes=64, name="grouped")
             grouped_words = (
-                grouped[c][:]
-                .rearrange("p g r t -> p (g r t)")
-                .bitcast(F32)
-                .rearrange("p (g r u) -> p g r u", g=PASSES, u=2)
+                grouped[c][:].rearrange("p g r t -> p (g r t)").bitcast(F32).rearrange("p (g r u) -> p g r u", g=PASSES, u=2)
             )
-            planes = xt[t][:].rearrange("p (g u) r -> p g r u", u=2)
-            if j == 0:
-                nc.scalar.copy(out=grouped_words[:, :, j * P : (j + 1) * P, :], in_=planes)
-            else:
-                nc.vector.tensor_copy(out=grouped_words[:, :, j * P : (j + 1) * P, :], in_=planes)
+            planes = xt[c, j][:].rearrange("p (g u) r -> p g r u", u=2)
+            nc.scalar.copy(out=grouped_words[:, :, j * P : (j + 1) * P, :], in_=planes)
 
-        def quantise_x(i):
-            c, g = divmod(i, PASSES)
-            if g == 0:
-                x_codes[c] = stage.tile([P, PASSES, CHUNK], U32, align_bytes=64, name="x_codes")
-                x_planes[c] = stage.tile([P, PASSES, CHUNK], U8, align_bytes=64, name="x_planes")
+        def quantise_x(c):
+            x_codes[c] = stage.tile([P, PASSES, CHUNK], U32, align_bytes=64, name="x_codes")
+            x_planes[c] = stage.tile([P, PASSES, CHUNK], U8, align_bytes=64, name="x_planes")
             nc.vector.quantize_mx(
-                out=x_codes[c][:, g, :].bitcast(FP8X4),
-                scales=x_planes[c][:, g, :],
-                in_=grouped[c][:, g].rearrange("p r t -> p (r t)"),
+                out=x_codes[c][:].rearrange("p g r -> p (g r)").bitcast(FP8X4),
+                scales=x_planes[c][:].rearrange("p g r -> p (g r)"),
+                in_=grouped[c][:].rearrange("p g r t -> p (g r t)"),
             )
 
-        def project(s):
-            c, w = divmod(s, 2)
+        def project_q(c):
             for pair in range(HEADS // 2):
-                vt[s, pair] = psum_v.tile([P, 2, CHUNK], F32, name="vt")
+                vt[c, pair] = psum_v.tile([P, 2, CHUNK], F32, name="vt")
                 for i in range(2):
                     h = 2 * pair + i
                     for g in range(PASSES):
                         nc.tensor.matmul_mx(
-                            out=vt[s, pair][:, i, :],
-                            lhsT=w_codes[:, w, g, h * D : (h + 1) * D].bitcast(FP8X4),
-                            lhsT_scale=w_planes[:, w, g, h * D : (h + 1) * D],
+                            out=vt[c, pair][:, i, :],
+                            lhsT=w_codes[:, 0, g, h * D : (h + 1) * D].bitcast(FP8X4),
+                            lhsT_scale=w_planes[:, 0, g, h * D : (h + 1) * D],
                             rhs=x_codes[c][:, g, :].bitcast(FP8X4),
                             rhs_scale=x_planes[c][:, g, :],
-                            start=(g == 0),
-                            stop=(g == PASSES - 1),
+                            start=(g == 0), stop=(g == PASSES - 1),
                         )
 
-        def affine(s):
-            u_t[s] = u_pool.tile([P, HEADS, CHUNK], F32, name="u_t")
-            for pair in range(HEADS // 2):
-                nc.scalar.activation(
-                    out=u_t[s][:, 2 * pair : 2 * pair + 2, :], in_=vt[s, pair][:],
-                    func=ACT.Identity, bias=gb[:, 1:2], scale=gb[:, 0:1],
-                )
+        def affine_q(c, pair):
+            if pair == 0:
+                u_t[c] = u_pool.tile([P, HEADS, CHUNK], F32, name="u_t")
+            nc.scalar.activation(
+                out=u_t[c][:, 2 * pair : 2 * pair + 2, :], in_=vt[c, pair][:],
+                func=ACT.Identity, bias=gb[:, 1:2], scale=gb[:, 0:1],
+            )
 
-        def transpose_back(s):
-            for j in range(TILES_PER_CHUNK):
-                ub[s, j] = psum_u.tile([P, HEADS, D], F32, name="ub")
+        def transpose_back(c):
+            for j in range(TILES):
+                ub[c, j] = psum_u.tile([P, HEADS, D], F32, name="ub")
                 for h in range(HEADS):
-                    nc.tensor.transpose(
-                        ub[s, j][:, h, :], u_t[s][:, h, j * P : (j + 1) * P], ident[:]
+                    nc.tensor.transpose(ub[c, j][:, h, :], u_t[c][:, h, j * P : (j + 1) * P], ident[:])
+
+        def project_k(c):
+            for j in range(TILES):
+                vk[c, j] = psum_s.tile([P, HEADS, D], F32, name="shared")
+                for g in range(PASSES):
+                    nc.tensor.matmul_mx(
+                        out=vk[c, j][:].rearrange("p h d -> p (h d)"),
+                        lhsT=x_codes[c][:, g, j * P : (j + 1) * P].bitcast(FP8X4),
+                        lhsT_scale=x_planes[c][:, g, j * P : (j + 1) * P],
+                        rhs=w_codes[:, 1, g, :].bitcast(FP8X4),
+                        rhs_scale=w_planes[:, 1, g, :],
+                        start=(g == 0), stop=(g == PASSES - 1),
                     )
 
-        def moments(s, j):
-            stats[s, j] = small.tile([P, HEADS // 2, 6], F32, name="stats")
+        def times_gamma(c, j):
+            t_sb[c, j] = k_pool.tile([P, HEADS, D], F32, name="t_sb")
+            nc.vector.tensor_tensor(out=t_sb[c, j][:], in0=vk[c, j][:], in1=gamma_rows[:], op=ALU.mult)
+
+        def plus_beta(c, j):
+            u_sb[c, j] = k_pool.tile([P, HEADS, D], F32, name="u_sb")
+            nc.gpsimd.tensor_tensor(out=u_sb[c, j][:], in0=t_sb[c, j][:], in1=beta_rows[:], op=ALU.add)
+
+        def source(w, c, j):
+            return ub[c, j] if w == 0 else u_sb[c, j]
+
+        def moments(w, c, j):
+            if j == 0:
+                stats[w, c] = small.tile([P, TILES, HEADS // 2, 6], F32, name="stats%d" % w)
             for a in range(HEADS // 2):
                 nc.vector.bn_stats(
-                    out=stats[s, j][:, a, :],
-                    in_=ub[s, j][:, 2 * a : 2 * a + 2, :].rearrange("p h d -> p d h"),
+                    out=stats[w, c][:, j, a, :],
+                    in_=source(w, c, j)[:, 2 * a : 2 * a + 2, :].rearrange("p h d -> p d h"),
                 )
 
-        def by_head(s, j):
-            return stats[s, j][:].rearrange("p a (h c) -> p (a h) c", c=3)
+        def by_block(w, c):
+            return stats[w, c][:].rearrange("p j a (h s) -> p (j a h) s", s=3)
 
-        def one_over_std(s, j):
-            w = s % 2
-            rstd[s, j] = small.tile([P, HEADS], F32, name="rstd")
+        def one_over_std(w, c):
+            rstd[w, c] = small.tile([P, TILES * HEADS], F32, name="rstd%d" % w)
             nc.scalar.activation(
-                out=rstd[s, j][:], in_=by_head(s, j)[:, :, 2], func=ACT.Abs_reciprocal_sqrt,
+                out=rstd[w, c][:], in_=by_block(w, c)[:, :, 2], func=ACT.Abs_reciprocal_sqrt,
                 bias=eps[:, w : w + 1], scale=(1.0 if w == 0 else 1.0 / D),
             )
 
-        def minus_mean_over_std(s, j):
-            shift[s, j] = small.tile([P, HEADS], F32, name="shift")
+        def minus_mean_over_std(w, c):
+            shift[w, c] = small.tile([P, TILES * HEADS], F32, name="shift%d" % w)
             nc.vector.scalar_tensor_tensor(
-                out=shift[s, j][:], in0=by_head(s, j)[:, :, 1], scalar=-1.0, in1=rstd[s, j][:],
+                out=shift[w, c][:], in0=by_block(w, c)[:, :, 1], scalar=-1.0, in1=rstd[w, c][:],
                 op0=ALU.mult, op1=ALU.mult,
             )
 
-        def store(s, j, feat):
-            c, w = divmod(s, 2)
-            t = c * TILES_PER_CHUNK + j
-            nc.sync.dma_start(
-                out=out_rows[w][t * P : (t + 1) * P, :], in_=feat[:].rearrange("p h d -> p (h d)")
-            )
-
-        def normalise_on_scalar(s, j):
-            feat = feat_pool.tile([P, HEADS, D], F32, name="feat")
-            for h in range(HEADS):
+        def normalise(engine, w, c, j, h):
+            if (w, c, j) not in feat:
+                feat[w, c, j] = feat_pool.tile([P, HEADS, D], F32, name="feat%d" % w)
+            b = j * HEADS + h
+            if engine == "scalar":
                 nc.scalar.activation(
-                    out=feat[:, h, :], in_=ub[s, j][:, h, :], func=ACT.Identity,
-                    bias=shift[s, j][:, h : h + 1], scale=rstd[s, j][:, h : h + 1],
+                    out=feat[w, c, j][:, h, :], in_=source(w, c, j)[:, h, :], func=ACT.Identity,
+                    bias=shift[w, c][:, b : b + 1], scale=rstd[w, c][:, b : b + 1],
                 )
-            store(s, j, feat)
-
-        def normalise_on_vector(s, j):
-            feat = feat_pool.tile([P, HEADS, D], F32, name="feat")
-            for h in range(HEADS):
-                nc.vector.tensor_scalar(
-                    out=feat[:, h, :], in0=ub[s, j][:, h, :],
-                    scalar1=by_head(s, j)[:, h, 1:2], scalar2=rstd[s, j][:, h : h + 1],
+            else:
+                eng = nc.vector if engine == "vector" else nc.gpsimd
+                eng.tensor_scalar(
+                    out=feat[w, c, j][:, h, :], in0=source(w, c, j)[:, h, :],
+                    scalar1=by_block(w, c)[:, b, 1:2], scalar2=rstd[w, c][:, b : b + 1],
                     op0=ALU.subtract, op1=ALU.mult,
                 )
-            store(s, j, feat)
+
+        def store(w, c, j):
+            t = c * TILES + j
+            nc.sync.dma_start(out=out_rows[w][t * P : (t + 1) * P, :], in_=feat[w, c, j][:].rearrange("p h d -> p (h d)"))
+
+        plan = []
+
+        def at(when, fn, *args):
+            plan.append((when, len(plan), fn, args))
+
+        blocks = [(j, h) for j in range(TILES) for h in range(HEADS)]
+        at(-9.0, load_gamma_beta)
+        at(-8.9, load_x, 0)
+        at(-8.8, load_weight, 0, Wq_words, Wq_scales)
+        at(-8.7, load_x, 1)
+        at(-8.6, load_weight, 1, Wk_words, Wk_scales)
+        at(-8.5, load_x, 2)
+        at(-8.4, load_x, 3)
+        at(-1.30, spread_gamma_beta)
+        for c in range(N_CHUNKS):
+            if c >= 4:
+                at(c - 4 + 0.5, load_x, c)
+            at(c - 2 + T_XT, transpose_x, c, 0)
+            at(c - 2 + T_XT + 0.01, transpose_x, c, 1)
+            at(c - 2 + T_A0, copy_x, c, 0)
+            at(c - 2 + T_A1, copy_x, c, 1)
+            at(c - 1 + T_Q, quantise_x, c)
+            at(c, project_q, c)
+            at(c + 0.01, project_k, c)
+            at(c + T_C, affine_q, c, 0)
+            at(c + T_C + 0.01, affine_q, c, 1)
+            at(c + T_BT, transpose_back, c)
+            at(c + T_P1, times_gamma, c, 0)
+            at(c + T_P1 + 0.01, times_gamma, c, 1)
+            at(c + T_P1 + 0.02, plus_beta, c, 0)
+            at(c + T_P1 + 0.03, plus_beta, c, 1)
+            at(c + T_D, moments, 0, c, 0)
+            at(c + T_D + 0.01, moments, 0, c, 1)
+            at(c + T_RQ, one_over_std, 0, c)
+            at(c + T_P3A, moments, 1, c, 0)
+            at(c + T_P3B, moments, 1, c, 1)
+            at(c + T_RK, one_over_std, 1, c)
+            at(c + T_S, minus_mean_over_std, 0, c)
+            at(c + T_S + 0.001, minus_mean_over_std, 1, c)
+            n = 0
+            for j, h in blocks:
+                n += 1
+                if (j, h) in Q_ON_VECTOR:
+                    at(c + T_EV + 0.001 * n, normalise, "vector", 0, c, j, h)
+                else:
+                    at(c + T_EA + 0.001 * n, normalise, "scalar", 0, c, j, h)
+                if h == HEADS - 1:
+                    at(c + T_EA + 0.001 * n + 0.0005, store, 0, c, j)
+            for j, h in blocks:
+                n += 1
+                if (j, h) in K_ON_GPSIMD:
+                    at(c + T_EG + 0.001 * n, normalise, "gpsimd", 1, c, j, h)
+                else:
+                    at(c + T_EA + 0.001 * n, normalise, "scalar", 1, c, j, h)
+                if h == HEADS - 1:
+                    at(c + (T_EG if j == 1 else T_EA) + 0.001 * n + 0.0005, store, 1, c, j)
 
         with tc.manual_schedule():
-            for s in range(-5, N_STEPS + 2):
-                old, last = s - 2, s - 1
-                on_scalar = (s + 4) % TILES_PER_CHUNK == 0
-                if 0 <= old < N_STEPS:
-                    one_over_std(old, 0)
-                if 0 <= s + 4 < N_TILES and on_scalar:
-                    copy_x(s + 4)
-                if 0 <= old < N_STEPS:
-                    one_over_std(old, 1)
-                if 0 <= s + 2 < N_STEPS:
-                    quantise_x(s + 2)
-                if 0 <= s + 4 < N_TILES and not on_scalar:
-                    copy_x(s + 4)
-                if 0 <= old < N_STEPS:
-                    minus_mean_over_std(old, 0)
-                    normalise_on_vector(old, 1)
-                if 0 <= s < N_STEPS:
-                    project(s)
-                    affine(s)
-                if 0 <= old < N_STEPS:
-                    normalise_on_scalar(old, 0)
-                if 0 <= last < N_STEPS:
-                    transpose_back(last)
-                if 0 <= s + 5 < N_TILES:
-                    transpose_x(s + 5)
-                if 0 <= last < N_STEPS:
-                    moments(last, 0)
-                    moments(last, 1)
+            for when, n, fn, args in sorted(plan, key=lambda e: (e[0], e[1])):
+                fn(*args)
+
+
+T_C = 0.19
+T_BT = 0.52
+T_XT = 0.66
+T_A0 = 0.85
+T_A1 = 0.97
+T_P1 = 0.43
+T_D = 0.68
+T_RQ = 0.96
+T_P3A = 0.93
+T_EV = 1.05
+T_P3B = 1.14
+T_RK = 1.195
+T_S = 1.33
+T_Q = 0.27
+T_EA = 1.46
+T_EG = 2.12

@@ -27,8 +27,8 @@ N_CHUNKS = TOKENS // CHUNK
 
 FLOPS = 2 * TOKENS * HID * 2 * COLS
 
-Q_ON_VECTOR = ((0, 0), (0, 1))
-K_ON_GPSIMD = ((1, 2), (1, 3))
+ON_SCALAR = ((), ((1, 0), (1, 1), (1, 2), (1, 3)))
+LEAD = 2
 
 
 def tile_rebasedlinearattention_pa_t_kernel(
@@ -40,14 +40,12 @@ def tile_rebasedlinearattention_pa_t_kernel(
 
     with ExitStack() as ctx:
         const = ctx.enter_context(tc.tile_pool(name="const", bufs=1))
-        x_pool = ctx.enter_context(tc.tile_pool(name="x", bufs=6))
-        stage = ctx.enter_context(tc.tile_pool(name="stage", bufs=3))
-        u_pool = ctx.enter_context(tc.tile_pool(name="u", bufs=3))
-        k_pool = ctx.enter_context(tc.tile_pool(name="k", bufs=6))
-        feat_pool = ctx.enter_context(tc.tile_pool(name="feat", bufs=6))
-        small = ctx.enter_context(tc.tile_pool(name="small", bufs=6))
-        psum_v = ctx.enter_context(tc.psum_pool(name="psum_v", bufs=2))
-        psum_s = ctx.enter_context(tc.psum_pool(name="psum_s", bufs=2))
+        x_pool = ctx.enter_context(tc.tile_pool(name="x", bufs=7))
+        stage = ctx.enter_context(tc.tile_pool(name="stage", bufs=4))
+        u_pool = ctx.enter_context(tc.tile_pool(name="u", bufs=4))
+        feat_pool = ctx.enter_context(tc.tile_pool(name="feat", bufs=10))
+        small = ctx.enter_context(tc.tile_pool(name="small", bufs=8))
+        psum_s = ctx.enter_context(tc.psum_pool(name="psum_s", bufs=4))
         psum_u = ctx.enter_context(tc.psum_pool(name="psum_u", bufs=4))
 
         ident = const.tile([P, P], F32)
@@ -60,16 +58,14 @@ def tile_rebasedlinearattention_pa_t_kernel(
         nc.vector.memset(eps[:, 1:2], LN_EPS)
         gb_row = const.tile([P, 2 * D], BF16)
         nc.vector.memset(gb_row[:], 0.0)
-        ones = const.tile([P, P], BF16)
+        ones = const.tile([P, 2], BF16)
         nc.vector.memset(ones[:], 1.0)
         warm = const.tile([P, 2], F32)
         nc.scalar.activation(out=warm[:], in_=eps[:], func=ACT.Abs_reciprocal_sqrt)
         gb = const.tile([P, 2], F32)
-        gamma_rows = const.tile([P, HEADS, D], F32)
-        beta_rows = const.tile([P, HEADS, D], F32)
 
         x_sb, xt, grouped, x_codes, x_planes = {}, {}, {}, {}, {}
-        vt, u_t, ub, vk, t_sb, u_sb, feat = {}, {}, {}, {}, {}, {}, {}
+        vt, u_t, ub, feat = {}, {}, {}, {}
         stats, rstd, shift = {}, {}, {}
 
         def load_x(c):
@@ -94,15 +90,10 @@ def tile_rebasedlinearattention_pa_t_kernel(
             nc.sync.dma_start(out=gb_row[0:1, 0:D], in_=gamma.rearrange("(o d) -> o d", o=1))
             nc.sync.dma_start(out=gb_row[0:1, D : 2 * D], in_=beta.rearrange("(o d) -> o d", o=1))
 
-        def spread_gamma_beta():
-            for i, rows in enumerate((gamma_rows, beta_rows)):
-                bank = psum_u.tile([P, HEADS, D], F32, name="ub")
-                for h in range(HEADS):
-                    nc.tensor.matmul(out=bank[:, h, :], lhsT=ones[:], rhs=gb_row[:, i * D : (i + 1) * D], start=True, stop=True)
-                nc.vector.tensor_copy(out=rows[:], in_=bank[:])
+        def gamma_beta_columns():
             bank = psum_u.tile([P, HEADS, D], F32, name="ub")
             for i in range(2):
-                nc.tensor.matmul(out=bank[:, i, 0:2], lhsT=gb_row[:, i * D : (i + 1) * D], rhs=ones[:, 0:2], start=True, stop=True)
+                nc.tensor.matmul(out=bank[:, i, 0:2], lhsT=gb_row[:, i * D : (i + 1) * D], rhs=ones[:], start=True, stop=True)
             nc.vector.tensor_copy(out=gb[:], in_=bank[:, 0:2, 0])
 
         def transpose_x(c, j):
@@ -130,98 +121,73 @@ def tile_rebasedlinearattention_pa_t_kernel(
                 in_=grouped[c][:].rearrange("p g r t -> p (g r t)"),
             )
 
-        def project_q(c):
+        def project(w, c):
             for pair in range(HEADS // 2):
-                vt[c, pair] = psum_v.tile([P, 2, CHUNK], F32, name="vt")
+                vt[w, c, pair] = psum_s.tile([P, 2, CHUNK], F32, name="shared")
                 for i in range(2):
                     h = 2 * pair + i
                     for g in range(PASSES):
                         nc.tensor.matmul_mx(
-                            out=vt[c, pair][:, i, :],
-                            lhsT=w_codes[:, 0, g, h * D : (h + 1) * D].bitcast(FP8X4),
-                            lhsT_scale=w_planes[:, 0, g, h * D : (h + 1) * D],
+                            out=vt[w, c, pair][:, i, :],
+                            lhsT=w_codes[:, w, g, h * D : (h + 1) * D].bitcast(FP8X4),
+                            lhsT_scale=w_planes[:, w, g, h * D : (h + 1) * D],
                             rhs=x_codes[c][:, g, :].bitcast(FP8X4),
                             rhs_scale=x_planes[c][:, g, :],
                             start=(g == 0), stop=(g == PASSES - 1),
                         )
 
-        def affine_q(c, pair):
+        def affine(w, c, pair):
             if pair == 0:
-                u_t[c] = u_pool.tile([P, HEADS, CHUNK], F32, name="u_t")
+                u_t[w, c] = u_pool.tile([P, HEADS, CHUNK], F32, name="u_t")
             nc.scalar.activation(
-                out=u_t[c][:, 2 * pair : 2 * pair + 2, :], in_=vt[c, pair][:],
+                out=u_t[w, c][:, 2 * pair : 2 * pair + 2, :], in_=vt[w, c, pair][:],
                 func=ACT.Identity, bias=gb[:, 1:2], scale=gb[:, 0:1],
             )
 
-        def transpose_back(c):
+        def transpose_back(w, c):
             for j in range(TILES):
-                ub[c, j] = psum_u.tile([P, HEADS, D], F32, name="ub")
+                ub[w, c, j] = psum_u.tile([P, HEADS, D], F32, name="ub")
                 for h in range(HEADS):
-                    nc.tensor.transpose(ub[c, j][:, h, :], u_t[c][:, h, j * P : (j + 1) * P], ident[:])
-
-        def project_k(c):
-            for j in range(TILES):
-                vk[c, j] = psum_s.tile([P, HEADS, D], F32, name="shared")
-                for g in range(PASSES):
-                    nc.tensor.matmul_mx(
-                        out=vk[c, j][:].rearrange("p h d -> p (h d)"),
-                        lhsT=x_codes[c][:, g, j * P : (j + 1) * P].bitcast(FP8X4),
-                        lhsT_scale=x_planes[c][:, g, j * P : (j + 1) * P],
-                        rhs=w_codes[:, 1, g, :].bitcast(FP8X4),
-                        rhs_scale=w_planes[:, 1, g, :],
-                        start=(g == 0), stop=(g == PASSES - 1),
-                    )
-
-        def times_gamma(c, j):
-            t_sb[c, j] = k_pool.tile([P, HEADS, D], F32, name="t_sb")
-            nc.vector.tensor_tensor(out=t_sb[c, j][:], in0=vk[c, j][:], in1=gamma_rows[:], op=ALU.mult)
-
-        def plus_beta(c, j):
-            u_sb[c, j] = k_pool.tile([P, HEADS, D], F32, name="u_sb")
-            nc.gpsimd.tensor_tensor(out=u_sb[c, j][:], in0=t_sb[c, j][:], in1=beta_rows[:], op=ALU.add)
-
-        def source(w, c, j):
-            return ub[c, j] if w == 0 else u_sb[c, j]
+                    nc.tensor.transpose(ub[w, c, j][:, h, :], u_t[w, c][:, h, j * P : (j + 1) * P], ident[:])
 
         def moments(w, c, j):
             if j == 0:
-                stats[w, c] = small.tile([P, TILES, HEADS // 2, 6], F32, name="stats%d" % w)
+                stats[w, c] = small.tile([P, TILES, HEADS // 2, 6], F32, name="stats")
             for a in range(HEADS // 2):
                 nc.vector.bn_stats(
                     out=stats[w, c][:, j, a, :],
-                    in_=source(w, c, j)[:, 2 * a : 2 * a + 2, :].rearrange("p h d -> p d h"),
+                    in_=ub[w, c, j][:, 2 * a : 2 * a + 2, :].rearrange("p h d -> p d h"),
                 )
 
         def by_block(w, c):
             return stats[w, c][:].rearrange("p j a (h s) -> p (j a h) s", s=3)
 
         def one_over_std(w, c):
-            rstd[w, c] = small.tile([P, TILES * HEADS], F32, name="rstd%d" % w)
+            rstd[w, c] = small.tile([P, TILES * HEADS], F32, name="rstd")
             nc.scalar.activation(
                 out=rstd[w, c][:], in_=by_block(w, c)[:, :, 2], func=ACT.Abs_reciprocal_sqrt,
                 bias=eps[:, w : w + 1], scale=(1.0 if w == 0 else 1.0 / D),
             )
 
         def minus_mean_over_std(w, c):
-            shift[w, c] = small.tile([P, TILES * HEADS], F32, name="shift%d" % w)
+            shift[w, c] = small.tile([P, TILES * HEADS], F32, name="shift")
             nc.vector.scalar_tensor_tensor(
                 out=shift[w, c][:], in0=by_block(w, c)[:, :, 1], scalar=-1.0, in1=rstd[w, c][:],
                 op0=ALU.mult, op1=ALU.mult,
             )
 
-        def normalise(engine, w, c, j, h):
+        def normalise(w, c, j, h):
             if (w, c, j) not in feat:
-                feat[w, c, j] = feat_pool.tile([P, HEADS, D], F32, name="feat%d" % w)
+                feat[w, c, j] = feat_pool.tile([P, HEADS, D], F32, name="feat")
             b = j * HEADS + h
-            if engine == "scalar":
+            if (j, h) in ON_SCALAR[w]:
                 nc.scalar.activation(
-                    out=feat[w, c, j][:, h, :], in_=source(w, c, j)[:, h, :], func=ACT.Identity,
+                    out=feat[w, c, j][:, h, :], in_=ub[w, c, j][:, h, :], func=ACT.Identity,
                     bias=shift[w, c][:, b : b + 1], scale=rstd[w, c][:, b : b + 1],
                 )
             else:
-                eng = nc.vector if engine == "vector" else nc.gpsimd
-                eng.tensor_scalar(
-                    out=feat[w, c, j][:, h, :], in0=source(w, c, j)[:, h, :],
+                nc.vector.tensor_scalar(
+                    out=feat[w, c, j][:, h, :], in0=ub[w, c, j][:, h, :],
                     scalar1=by_block(w, c)[:, b, 1:2], scalar2=rstd[w, c][:, b : b + 1],
                     op0=ALU.subtract, op1=ALU.mult,
                 )
@@ -236,75 +202,55 @@ def tile_rebasedlinearattention_pa_t_kernel(
             plan.append((when, len(plan), fn, args))
 
         blocks = [(j, h) for j in range(TILES) for h in range(HEADS)]
-        at(-9.0, load_gamma_beta)
-        at(-8.9, load_x, 0)
-        at(-8.8, load_weight, 0, Wq_words, Wq_scales)
-        at(-8.7, load_x, 1)
+        at(-9.0, load_x, 0)
+        at(-8.9, load_weight, 0, Wq_words, Wq_scales)
+        at(-8.8, load_x, 1)
+        at(-8.7, load_gamma_beta)
         at(-8.6, load_weight, 1, Wk_words, Wk_scales)
-        at(-8.5, load_x, 2)
-        at(-8.4, load_x, 3)
-        at(-1.30, spread_gamma_beta)
+        for c in range(2, 5):
+            at(-8.5 + 0.01 * c, load_x, c)
+        at(-0.5, gamma_beta_columns)
         for c in range(N_CHUNKS):
-            if c >= 4:
-                at(c - 4 + 0.5, load_x, c)
-            at(c - 2 + T_XT, transpose_x, c, 0)
-            at(c - 2 + T_XT + 0.01, transpose_x, c, 1)
-            at(c - 2 + T_A0, copy_x, c, 0)
-            at(c - 2 + T_A1, copy_x, c, 1)
-            at(c - 1 + T_Q, quantise_x, c)
-            at(c, project_q, c)
-            at(c + 0.01, project_k, c)
-            at(c + T_C, affine_q, c, 0)
-            at(c + T_C + 0.01, affine_q, c, 1)
-            at(c + T_BT, transpose_back, c)
-            at(c + T_P1, times_gamma, c, 0)
-            at(c + T_P1 + 0.01, times_gamma, c, 1)
-            at(c + T_P1 + 0.02, plus_beta, c, 0)
-            at(c + T_P1 + 0.03, plus_beta, c, 1)
-            at(c + T_D, moments, 0, c, 0)
-            at(c + T_D + 0.01, moments, 0, c, 1)
-            at(c + T_RQ, one_over_std, 0, c)
-            at(c + T_P3A, moments, 1, c, 0)
-            at(c + T_P3B, moments, 1, c, 1)
-            at(c + T_RK, one_over_std, 1, c)
-            at(c + T_S, minus_mean_over_std, 0, c)
-            at(c + T_S + 0.001, minus_mean_over_std, 1, c)
-            n = 0
-            for j, h in blocks:
-                n += 1
-                if (j, h) in Q_ON_VECTOR:
-                    at(c + T_EV + 0.001 * n, normalise, "vector", 0, c, j, h)
-                else:
-                    at(c + T_EA + 0.001 * n, normalise, "scalar", 0, c, j, h)
-                if h == HEADS - 1:
-                    at(c + T_EA + 0.001 * n + 0.0005, store, 0, c, j)
-            for j, h in blocks:
-                n += 1
-                if (j, h) in K_ON_GPSIMD:
-                    at(c + T_EG + 0.001 * n, normalise, "gpsimd", 1, c, j, h)
-                else:
-                    at(c + T_EA + 0.001 * n, normalise, "scalar", 1, c, j, h)
-                if h == HEADS - 1:
-                    at(c + (T_EG if j == 1 else T_EA) + 0.001 * n + 0.0005, store, 1, c, j)
+            if c >= 5:
+                at(c - 5 + 0.5, load_x, c)
+            at(c - LEAD + T_XA, transpose_x, c, 0)
+            at(c - LEAD + T_XB, transpose_x, c, 1)
+            at(c - LEAD + T_A0, copy_x, c, 0)
+            at(c - LEAD + T_A1, copy_x, c, 1)
+            at(c - LEAD + T_Q, quantise_x, c)
+            for w in range(2):
+                at(c + 0.01 * w, project, w, c)
+                at(c + T_C[w], affine, w, c, 0)
+                at(c + T_C[w] + 0.01, affine, w, c, 1)
+                at(c + T_BT[w], transpose_back, w, c)
+                at(c + T_D[w], moments, w, c, 0)
+                at(c + T_D[w] + 0.01, moments, w, c, 1)
+                at(c + T_R[w], one_over_std, w, c)
+                at(c + T_S[w], minus_mean_over_std, w, c)
+                n = 0
+                last = {}
+                for j, h in blocks:
+                    n += 1
+                    when = c + (T_EA[w] if (j, h) in ON_SCALAR[w] else T_EV[w]) + 0.001 * n
+                    at(when, normalise, w, c, j, h)
+                    last[j] = max(last.get(j, when), when)
+                for j in range(TILES):
+                    at(last[j] + 0.0005, store, w, c, j)
 
         with tc.manual_schedule():
             for when, n, fn, args in sorted(plan, key=lambda e: (e[0], e[1])):
                 fn(*args)
 
 
-T_C = 0.19
-T_BT = 0.52
-T_XT = 0.66
-T_A0 = 0.85
-T_A1 = 0.97
-T_P1 = 0.43
-T_D = 0.68
-T_RQ = 0.96
-T_P3A = 0.93
-T_EV = 1.05
-T_P3B = 1.14
-T_RK = 1.195
-T_S = 1.33
-T_Q = 0.27
-T_EA = 1.46
-T_EG = 2.12
+T_C = (0.17, 0.42)
+T_BT = (0.49, 0.73)
+T_XA = 0.62
+T_XB = 0.87
+T_A0 = 0.79
+T_A1 = 0.99
+T_D = (0.61, 0.86)
+T_R = (0.90, 1.15)
+T_S = (0.92, 1.16)
+T_EA = (0.93, 1.66)
+T_EV = (1.10, 1.30)
+T_Q = 1.45

@@ -20,15 +20,20 @@ PASSES = HID // K_PASS
 HEADS = 4
 D = 128
 COLS = HEADS * D
+BANK = 512
 LN_EPS = 1e-5
-CHUNK = 256
-TILES = CHUNK // P
-N_CHUNKS = TOKENS // CHUNK
+N_TILES = TOKENS // P
+MOST = 2
 
 FLOPS = 2 * TOKENS * HID * 2 * COLS
 
-ON_SCALAR = ((), ((1, 0), (1, 1), (1, 2), (1, 3)))
+ROUNDS = [[2 * r, 2 * r + 1] for r in range(N_TILES // 2)]
+N_ROUNDS = len(ROUNDS)
 LEAD = 2
+
+ON_SCALAR = (((1, 3),), ((0, 0), (0, 1), (0, 2), (0, 3), (1, 0), (1, 1), (1, 2), (1, 3)))
+ON_SCALAR_LATE = (((1, 3),), ((0, 0), (0, 1), (0, 2), (0, 3), (1, 0), (1, 1), (1, 2), (1, 3)))
+ON_SCALAR_HALF = (((0, 0), (0, 1)), ((0, 2), (0, 3)))
 
 
 def tile_rebasedlinearattention_pa_t_kernel(
@@ -43,6 +48,7 @@ def tile_rebasedlinearattention_pa_t_kernel(
         x_pool = ctx.enter_context(tc.tile_pool(name="x", bufs=7))
         stage = ctx.enter_context(tc.tile_pool(name="stage", bufs=4))
         u_pool = ctx.enter_context(tc.tile_pool(name="u", bufs=4))
+        k_pool = ctx.enter_context(tc.tile_pool(name="k", bufs=4))
         feat_pool = ctx.enter_context(tc.tile_pool(name="feat", bufs=10))
         small = ctx.enter_context(tc.tile_pool(name="small", bufs=8))
         psum_s = ctx.enter_context(tc.psum_pool(name="psum_s", bufs=4))
@@ -50,29 +56,36 @@ def tile_rebasedlinearattention_pa_t_kernel(
 
         ident = const.tile([P, P], F32)
         make_identity(nc, ident[:])
+        gb_row = const.tile([P, 2 * D], BF16)
+        nc.vector.memset(gb_row[:], 0.0)
         w_planes = const.tile([P, 2, PASSES, COLS], U8, align_bytes=64)
         nc.vector.memset(w_planes[:].rearrange("p w g n -> p (w g n)").bitcast(I32), 0)
         w_codes = const.tile([P, 2, PASSES, COLS], U32, align_bytes=64)
         eps = const.tile([P, 2], F32)
         nc.vector.memset(eps[:, 0:1], D * LN_EPS)
         nc.vector.memset(eps[:, 1:2], LN_EPS)
-        gb_row = const.tile([P, 2 * D], BF16)
-        nc.vector.memset(gb_row[:], 0.0)
-        ones = const.tile([P, 2], BF16)
+        ones = const.tile([P, P], BF16)
         nc.vector.memset(ones[:], 1.0)
         warm = const.tile([P, 2], F32)
         nc.scalar.activation(out=warm[:], in_=eps[:], func=ACT.Abs_reciprocal_sqrt)
         gb = const.tile([P, 2], F32)
+        gb_rows = const.tile([P, 2, 2, D], F32)
+        vk, t_sb, u_sb = {}, {}, {}
 
         x_sb, xt, grouped, x_codes, x_planes = {}, {}, {}, {}, {}
         vt, u_t, ub, feat = {}, {}, {}, {}
         stats, rstd, shift = {}, {}, {}
 
-        def load_x(c):
-            x_sb[c] = x_pool.tile([P, TILES, HID], BF16, name="x_sb")
+        def width(r):
+            return len(ROUNDS[r])
+
+        def load_x(r):
+            n = width(r)
+            x_sb[r] = x_pool.tile([P, MOST, HID], BF16, name="x_sb")
+            first = ROUNDS[r][0] * P
             nc.sync.dma_start(
-                out=x_sb[c][:],
-                in_=x_rows[c * CHUNK : (c + 1) * CHUNK, :].rearrange("(j p) k -> p j k", p=P),
+                out=x_sb[r][:, 0:n, :],
+                in_=x_rows[first : first + n * P, :].rearrange("(j p) k -> p j k", p=P),
             )
 
         def load_weight(w, words, scales):
@@ -93,164 +106,224 @@ def tile_rebasedlinearattention_pa_t_kernel(
         def gamma_beta_columns():
             bank = psum_u.tile([P, HEADS, D], F32, name="ub")
             for i in range(2):
-                nc.tensor.matmul(out=bank[:, i, 0:2], lhsT=gb_row[:, i * D : (i + 1) * D], rhs=ones[:], start=True, stop=True)
+                nc.tensor.matmul(out=bank[:, i, 0:2], lhsT=gb_row[:, i * D : (i + 1) * D], rhs=ones[:, 0:2], start=True, stop=True)
             nc.vector.tensor_copy(out=gb[:], in_=bank[:, 0:2, 0])
 
-        def transpose_x(c, j):
-            x_words = x_sb[c][:, j, :].bitcast(F32)
-            xt[c, j] = psum_s.tile([P, PASSES * 2, P], F32, name="shared")
+        def gamma_beta_rows():
+            bank = psum_u.tile([P, HEADS, D], F32, name="ub")
+            for i in range(2):
+                for twice in range(2):
+                    nc.tensor.matmul(out=bank[:, 2 * i + twice, :], lhsT=ones[:], rhs=gb_row[:, i * D : (i + 1) * D], start=True, stop=True)
+            nc.vector.tensor_copy(out=gb_rows[:].rearrange("p i t d -> p (i t) d"), in_=bank[:])
+
+        def transpose_x(r, j):
+            x_words = x_sb[r][:, j, :].bitcast(F32)
+            xt[r, j] = psum_s.tile([P, PASSES * 2, P], F32, name="shared")
             for g in range(PASSES):
                 for u in range(2):
-                    nc.tensor.transpose(xt[c, j][:, 2 * g + u, :], x_words[:, 256 * g + u : 256 * (g + 1) : 2], ident[:])
+                    nc.tensor.transpose(xt[r, j][:, 2 * g + u, :], x_words[:, 256 * g + u : 256 * (g + 1) : 2], ident[:])
 
-        def copy_x(c, j):
+        def copy_x(r, j):
+            n = width(r)
             if j == 0:
-                grouped[c] = stage.tile([P, PASSES, CHUNK, 4], BF16, align_bytes=64, name="grouped")
-            grouped_words = (
-                grouped[c][:].rearrange("p g r t -> p (g r t)").bitcast(F32).rearrange("p (g r u) -> p g r u", g=PASSES, u=2)
-            )
-            planes = xt[c, j][:].rearrange("p (g u) r -> p g r u", u=2)
-            nc.scalar.copy(out=grouped_words[:, :, j * P : (j + 1) * P, :], in_=planes)
+                grouped[r] = stage.tile([P, MOST * HID], BF16, align_bytes=64, name="grouped")
+            grouped_words = grouped[r][:, 0 : n * HID].bitcast(F32).rearrange("p (g r u) -> p g r u", g=PASSES, u=2)
+            planes = xt[r, j][:].rearrange("p (g u) r -> p g r u", u=2)
+            if r == 0 and j == width(r) - 1 and HEAD_ON_VECTOR:
+                nc.vector.tensor_copy(out=grouped_words[:, :, j * P : (j + 1) * P, :], in_=planes)
+            else:
+                nc.scalar.copy(out=grouped_words[:, :, j * P : (j + 1) * P, :], in_=planes)
 
-        def quantise_x(c):
-            x_codes[c] = stage.tile([P, PASSES, CHUNK], U32, align_bytes=64, name="x_codes")
-            x_planes[c] = stage.tile([P, PASSES, CHUNK], U8, align_bytes=64, name="x_planes")
+        def quantise_x(r):
+            n = width(r)
+            x_codes[r] = stage.tile([P, MOST * HID // 4], U32, align_bytes=64, name="x_codes")
+            x_planes[r] = stage.tile([P, MOST * HID // 4], U8, align_bytes=64, name="x_planes")
             nc.vector.quantize_mx(
-                out=x_codes[c][:].rearrange("p g r -> p (g r)").bitcast(FP8X4),
-                scales=x_planes[c][:].rearrange("p g r -> p (g r)"),
-                in_=grouped[c][:].rearrange("p g r t -> p (g r t)"),
+                out=x_codes[r][:, 0 : n * HID // 4].bitcast(FP8X4),
+                scales=x_planes[r][:, 0 : n * HID // 4],
+                in_=grouped[r][:, 0 : n * HID],
             )
 
-        def project(w, c):
-            for pair in range(HEADS // 2):
-                vt[w, c, pair] = psum_s.tile([P, 2, CHUNK], F32, name="shared")
-                for i in range(2):
-                    h = 2 * pair + i
+        def tiles_f(w):
+            return MOST if w == 0 else 1
+
+        def project(w, r):
+            all_tokens = width(r) * P
+            tokens = tiles_f(w) * P
+            per_bank = BANK // tokens
+            for b in range(HEADS // per_bank):
+                vt[w, r, b] = psum_s.tile([P, BANK], F32, name="shared")
+                for i in range(per_bank):
+                    h = per_bank * b + i
                     for g in range(PASSES):
                         nc.tensor.matmul_mx(
-                            out=vt[w, c, pair][:, i, :],
+                            out=vt[w, r, b][:, i * tokens : (i + 1) * tokens],
                             lhsT=w_codes[:, w, g, h * D : (h + 1) * D].bitcast(FP8X4),
                             lhsT_scale=w_planes[:, w, g, h * D : (h + 1) * D],
-                            rhs=x_codes[c][:, g, :].bitcast(FP8X4),
-                            rhs_scale=x_planes[c][:, g, :],
+                            rhs=x_codes[r][:, g * all_tokens : g * all_tokens + tokens].bitcast(FP8X4),
+                            rhs_scale=x_planes[r][:, g * all_tokens : g * all_tokens + tokens],
                             start=(g == 0), stop=(g == PASSES - 1),
                         )
 
-        def affine(w, c, pair):
-            if pair == 0:
-                u_t[w, c] = u_pool.tile([P, HEADS, CHUNK], F32, name="u_t")
+        def project_tokens(r):
+            all_tokens = width(r) * P
+            vk[r] = psum_s.tile([P, HEADS, D], F32, name="shared")
+            for g in range(PASSES):
+                nc.tensor.matmul_mx(
+                    out=vk[r][:].rearrange("p h d -> p (h d)"),
+                    lhsT=x_codes[r][:, g * all_tokens + P : g * all_tokens + 2 * P].bitcast(FP8X4),
+                    lhsT_scale=x_planes[r][:, g * all_tokens + P : g * all_tokens + 2 * P],
+                    rhs=w_codes[:, 1, g, :].bitcast(FP8X4),
+                    rhs_scale=w_planes[:, 1, g, :],
+                    start=(g == 0), stop=(g == PASSES - 1),
+                )
+
+        def times_gamma(r):
+            t_sb[r] = k_pool.tile([P, HEADS, D], F32, name="t_sb")
+            for a in range(HEADS // 2):
+                nc.vector.tensor_tensor(out=t_sb[r][:, 2 * a : 2 * a + 2, :], in0=vk[r][:, 2 * a : 2 * a + 2, :], in1=gb_rows[:, 0], op=ALU.mult)
+
+        def plus_beta(r):
+            u_sb[r] = k_pool.tile([P, HEADS, D], F32, name="u_sb")
+            for a in range(HEADS // 2):
+                nc.gpsimd.tensor_tensor(out=u_sb[r][:, 2 * a : 2 * a + 2, :], in0=t_sb[r][:, 2 * a : 2 * a + 2, :], in1=gb_rows[:, 1], op=ALU.add)
+
+        def source(w, r, j):
+            return u_sb[r] if (w == 1 and j == 1) else ub[w, r, j]
+
+        def affine(w, r, b):
+            if b == 0:
+                u_t[w, r] = u_pool.tile([P, MOST * BANK], F32, name="u_t")
             nc.scalar.activation(
-                out=u_t[w, c][:, 2 * pair : 2 * pair + 2, :], in_=vt[w, c, pair][:],
+                out=u_t[w, r][:, b * BANK : (b + 1) * BANK], in_=vt[w, r, b][:],
                 func=ACT.Identity, bias=gb[:, 1:2], scale=gb[:, 0:1],
             )
 
-        def transpose_back(w, c):
-            for j in range(TILES):
-                ub[w, c, j] = psum_u.tile([P, HEADS, D], F32, name="ub")
+        def transpose_back(w, r):
+            n = tiles_f(w)
+            for j in range(n):
+                ub[w, r, j] = psum_u.tile([P, HEADS, D], F32, name="ub")
                 for h in range(HEADS):
-                    nc.tensor.transpose(ub[w, c, j][:, h, :], u_t[w, c][:, h, j * P : (j + 1) * P], ident[:])
+                    nc.tensor.transpose(ub[w, r, j][:, h, :], u_t[w, r][:, (h * n + j) * P : (h * n + j + 1) * P], ident[:])
 
-        def moments(w, c, j):
+        def moments(w, r, j):
             if j == 0:
-                stats[w, c] = small.tile([P, TILES, HEADS // 2, 6], F32, name="stats")
+                stats[w, r] = small.tile([P, MOST, HEADS // 2, 6], F32, name="stats")
             for a in range(HEADS // 2):
                 nc.vector.bn_stats(
-                    out=stats[w, c][:, j, a, :],
-                    in_=ub[w, c, j][:, 2 * a : 2 * a + 2, :].rearrange("p h d -> p d h"),
+                    out=stats[w, r][:, j, a, :],
+                    in_=source(w, r, j)[:, 2 * a : 2 * a + 2, :].rearrange("p h d -> p d h"),
                 )
 
-        def by_block(w, c):
-            return stats[w, c][:].rearrange("p j a (h s) -> p (j a h) s", s=3)
+        def by_block(w, r):
+            return stats[w, r][:, 0 : width(r)].rearrange("p j a (h s) -> p (j a h) s", s=3)
 
-        def one_over_std(w, c):
-            rstd[w, c] = small.tile([P, TILES * HEADS], F32, name="rstd")
+        def one_over_std(w, r):
+            rstd[w, r] = small.tile([P, MOST * HEADS], F32, name="rstd")
             nc.scalar.activation(
-                out=rstd[w, c][:], in_=by_block(w, c)[:, :, 2], func=ACT.Abs_reciprocal_sqrt,
+                out=rstd[w, r][:, 0 : width(r) * HEADS], in_=by_block(w, r)[:, :, 2], func=ACT.Abs_reciprocal_sqrt,
                 bias=eps[:, w : w + 1], scale=(1.0 if w == 0 else 1.0 / D),
             )
 
-        def minus_mean_over_std(w, c):
-            shift[w, c] = small.tile([P, TILES * HEADS], F32, name="shift")
+        def minus_mean_over_std(w, r):
+            shift[w, r] = small.tile([P, MOST * HEADS], F32, name="shift")
             nc.vector.scalar_tensor_tensor(
-                out=shift[w, c][:], in0=by_block(w, c)[:, :, 1], scalar=-1.0, in1=rstd[w, c][:],
-                op0=ALU.mult, op1=ALU.mult,
+                out=shift[w, r][:, 0 : width(r) * HEADS], in0=by_block(w, r)[:, :, 1], scalar=-1.0,
+                in1=rstd[w, r][:, 0 : width(r) * HEADS], op0=ALU.mult, op1=ALU.mult,
             )
 
-        def normalise(w, c, j, h):
-            if (w, c, j) not in feat:
-                feat[w, c, j] = feat_pool.tile([P, HEADS, D], F32, name="feat")
+        def on_scalar(w, r):
+            if width(r) < MOST:
+                return ON_SCALAR_HALF[w]
+            return ON_SCALAR[w] if r < N_ROUNDS - LEAD else ON_SCALAR_LATE[w]
+
+        def normalise(w, r, j, h):
+            if (w, r, j) not in feat:
+                feat[w, r, j] = feat_pool.tile([P, HEADS, D], F32, name="feat")
             b = j * HEADS + h
-            if (j, h) in ON_SCALAR[w]:
+            if (j, h) in on_scalar(w, r):
                 nc.scalar.activation(
-                    out=feat[w, c, j][:, h, :], in_=ub[w, c, j][:, h, :], func=ACT.Identity,
-                    bias=shift[w, c][:, b : b + 1], scale=rstd[w, c][:, b : b + 1],
+                    out=feat[w, r, j][:, h, :], in_=source(w, r, j)[:, h, :], func=ACT.Identity,
+                    bias=shift[w, r][:, b : b + 1], scale=rstd[w, r][:, b : b + 1],
                 )
             else:
                 nc.vector.tensor_scalar(
-                    out=feat[w, c, j][:, h, :], in0=ub[w, c, j][:, h, :],
-                    scalar1=by_block(w, c)[:, b, 1:2], scalar2=rstd[w, c][:, b : b + 1],
+                    out=feat[w, r, j][:, h, :], in0=source(w, r, j)[:, h, :],
+                    scalar1=by_block(w, r)[:, b, 1:2], scalar2=rstd[w, r][:, b : b + 1],
                     op0=ALU.subtract, op1=ALU.mult,
                 )
 
-        def store(w, c, j):
-            t = c * TILES + j
-            nc.sync.dma_start(out=out_rows[w][t * P : (t + 1) * P, :], in_=feat[w, c, j][:].rearrange("p h d -> p (h d)"))
+        def store(w, r, j):
+            t = ROUNDS[r][j]
+            nc.sync.dma_start(out=out_rows[w][t * P : (t + 1) * P, :], in_=feat[w, r, j][:].rearrange("p h d -> p (h d)"))
 
         plan = []
 
         def at(when, fn, *args):
             plan.append((when, len(plan), fn, args))
 
-        blocks = [(j, h) for j in range(TILES) for h in range(HEADS)]
         at(-9.0, load_x, 0)
         at(-8.9, load_weight, 0, Wq_words, Wq_scales)
         at(-8.8, load_x, 1)
         at(-8.7, load_gamma_beta)
         at(-8.6, load_weight, 1, Wk_words, Wk_scales)
-        for c in range(2, 5):
-            at(-8.5 + 0.01 * c, load_x, c)
-        at(-0.5, gamma_beta_columns)
-        for c in range(N_CHUNKS):
-            if c >= 5:
-                at(c - 5 + 0.5, load_x, c)
-            at(c - LEAD + T_XA, transpose_x, c, 0)
-            at(c - LEAD + T_XB, transpose_x, c, 1)
-            at(c - LEAD + T_A0, copy_x, c, 0)
-            at(c - LEAD + T_A1, copy_x, c, 1)
-            at(c - LEAD + T_Q, quantise_x, c)
+        for r in range(2, 5):
+            at(-8.5 + 0.01 * r, load_x, r)
+        at(-0.05, gamma_beta_columns)
+        at(-0.04, gamma_beta_rows)
+        for r in range(N_ROUNDS):
+            n = width(r)
+            if r >= 5:
+                at(r - 5 + 0.5, load_x, r)
+            at(r - LEAD + T_XA, transpose_x, r, 0)
+            at(r - LEAD + T_A0, copy_x, r, 0)
+            if n > 1:
+                at(r - LEAD + T_XB, transpose_x, r, 1)
+                at(r - LEAD + T_A1, copy_x, r, 1)
+            at(r - LEAD + T_Q, quantise_x, r)
             for w in range(2):
-                at(c + 0.01 * w, project, w, c)
-                at(c + T_C[w], affine, w, c, 0)
-                at(c + T_C[w] + 0.01, affine, w, c, 1)
-                at(c + T_BT[w], transpose_back, w, c)
-                at(c + T_D[w], moments, w, c, 0)
-                at(c + T_D[w] + 0.01, moments, w, c, 1)
-                at(c + T_R[w], one_over_std, w, c)
-                at(c + T_S[w], minus_mean_over_std, w, c)
-                n = 0
+                at(r + 0.01 * w, project, w, r)
+                for b in range(tiles_f(w)):
+                    at(r + T_C[w] + 0.01 * b, affine, w, r, b)
+                at(r + T_BT[w], transpose_back, w, r)
+                for j in range(tiles_f(w)):
+                    at(r + T_D[w] + 0.01 * j, moments, w, r, j)
+                if w == 1:
+                    at(r + 0.02, project_tokens, r)
+                    at(r + T_P1, times_gamma, r)
+                    at(r + T_P1 + 0.001, plus_beta, r)
+                    at(r + T_P3, moments, 1, r, 1)
+                at(r + T_R[w], one_over_std, w, r)
+                if on_scalar(w, r):
+                    at(r + T_S[w], minus_mean_over_std, w, r)
+                i = 0
                 last = {}
-                for j, h in blocks:
-                    n += 1
-                    when = c + (T_EA[w] if (j, h) in ON_SCALAR[w] else T_EV[w]) + 0.001 * n
-                    at(when, normalise, w, c, j, h)
-                    last[j] = max(last.get(j, when), when)
-                for j in range(TILES):
-                    at(last[j] + 0.0005, store, w, c, j)
+                for j in range(n):
+                    for h in range(HEADS):
+                        i += 1
+                        when = r + (T_EA[w] if (j, h) in on_scalar(w, r) else T_EV[w][j]) + 0.001 * i
+                        at(when, normalise, w, r, j, h)
+                        last[j] = max(last.get(j, when), when)
+                for j in range(n):
+                    at(last[j] + 0.0005, store, w, r, j)
 
         with tc.manual_schedule():
-            for when, n, fn, args in sorted(plan, key=lambda e: (e[0], e[1])):
+            for when, i, fn, args in sorted(plan, key=lambda e: (e[0], e[1])):
                 fn(*args)
 
 
-T_C = (0.17, 0.42)
+HEAD_ON_VECTOR = False
+T_P1 = 0.55
+T_P3 = 1.00
+T_C = (0.17, 0.44)
 T_BT = (0.49, 0.73)
 T_XA = 0.62
 T_XB = 0.87
 T_A0 = 0.79
 T_A1 = 0.99
 T_D = (0.61, 0.86)
-T_R = (0.90, 1.15)
-T_S = (0.92, 1.16)
-T_EA = (0.93, 1.66)
-T_EV = (1.10, 1.30)
+T_R = (0.862, 1.43)
+T_S = (1.434, 1.435)
+T_EA = (1.455, 1.46)
+T_EV = ((0.90, 1.10), (1.30, 1.30))
 T_Q = 1.45

@@ -31,9 +31,9 @@ ROUNDS = [[2 * r, 2 * r + 1] for r in range(N_TILES // 2)]
 N_ROUNDS = len(ROUNDS)
 LEAD = 2
 
-ON_SCALAR = (((1, 3),), ((0, 0), (0, 1), (0, 2), (0, 3), (1, 0), (1, 1), (1, 2), (1, 3)))
+ON_SCALAR = (((1, 2), (1, 3)), ((0, 0), (0, 1), (0, 2), (0, 3), (1, 0), (1, 1), (1, 2), (1, 3)))
 ON_SCALAR_LATE = (((1, 3),), ((0, 0), (0, 1), (0, 2), (0, 3), (1, 0), (1, 1), (1, 2), (1, 3)))
-ON_SCALAR_HALF = (((0, 0), (0, 1)), ((0, 2), (0, 3)))
+ON_SCALAR_LAST = (((0, 0), (0, 1), (0, 2), (0, 3), (1, 0), (1, 1), (1, 2), (1, 3)), ())
 
 
 def tile_rebasedlinearattention_pa_t_kernel(
@@ -144,14 +144,14 @@ def tile_rebasedlinearattention_pa_t_kernel(
                 in_=grouped[r][:, 0 : n * HID],
             )
 
-        def tiles_f(w):
-            return MOST if w == 0 else 1
+        def banks_f(w):
+            return 2 if w == 0 else 1
 
         def project(w, r):
             all_tokens = width(r) * P
-            tokens = tiles_f(w) * P
+            tokens = all_tokens
             per_bank = BANK // tokens
-            for b in range(HEADS // per_bank):
+            for b in range(banks_f(w)):
                 vt[w, r, b] = psum_s.tile([P, BANK], F32, name="shared")
                 for i in range(per_bank):
                     h = per_bank * b + i
@@ -167,29 +167,32 @@ def tile_rebasedlinearattention_pa_t_kernel(
 
         def project_tokens(r):
             all_tokens = width(r) * P
-            vk[r] = psum_s.tile([P, HEADS, D], F32, name="shared")
-            for g in range(PASSES):
-                nc.tensor.matmul_mx(
-                    out=vk[r][:].rearrange("p h d -> p (h d)"),
-                    lhsT=x_codes[r][:, g * all_tokens + P : g * all_tokens + 2 * P].bitcast(FP8X4),
-                    lhsT_scale=x_planes[r][:, g * all_tokens + P : g * all_tokens + 2 * P],
-                    rhs=w_codes[:, 1, g, :].bitcast(FP8X4),
-                    rhs_scale=w_planes[:, 1, g, :],
-                    start=(g == 0), stop=(g == PASSES - 1),
-                )
+            vk[r] = psum_s.tile([P, MOST, 2, D], F32, name="shared")
+            for j in range(MOST):
+                for g in range(PASSES):
+                    nc.tensor.matmul_mx(
+                        out=vk[r][:, j].rearrange("p h d -> p (h d)"),
+                        lhsT=x_codes[r][:, g * all_tokens + j * P : g * all_tokens + (j + 1) * P].bitcast(FP8X4),
+                        lhsT_scale=x_planes[r][:, g * all_tokens + j * P : g * all_tokens + (j + 1) * P],
+                        rhs=w_codes[:, 1, g, 2 * D : 4 * D].bitcast(FP8X4),
+                        rhs_scale=w_planes[:, 1, g, 2 * D : 4 * D],
+                        start=(g == 0), stop=(g == PASSES - 1),
+                    )
 
         def times_gamma(r):
-            t_sb[r] = k_pool.tile([P, HEADS, D], F32, name="t_sb")
-            for a in range(HEADS // 2):
-                nc.vector.tensor_tensor(out=t_sb[r][:, 2 * a : 2 * a + 2, :], in0=vk[r][:, 2 * a : 2 * a + 2, :], in1=gb_rows[:, 0], op=ALU.mult)
+            t_sb[r] = k_pool.tile([P, MOST, 2, D], F32, name="t_sb")
+            for j in range(MOST):
+                nc.vector.tensor_tensor(out=t_sb[r][:, j], in0=vk[r][:, j], in1=gb_rows[:, 0], op=ALU.mult)
 
         def plus_beta(r):
-            u_sb[r] = k_pool.tile([P, HEADS, D], F32, name="u_sb")
-            for a in range(HEADS // 2):
-                nc.gpsimd.tensor_tensor(out=u_sb[r][:, 2 * a : 2 * a + 2, :], in0=t_sb[r][:, 2 * a : 2 * a + 2, :], in1=gb_rows[:, 1], op=ALU.add)
+            u_sb[r] = k_pool.tile([P, MOST, 2, D], F32, name="u_sb")
+            for j in range(MOST):
+                nc.gpsimd.tensor_tensor(out=u_sb[r][:, j], in0=t_sb[r][:, j], in1=gb_rows[:, 1], op=ALU.add)
 
-        def source(w, r, j):
-            return u_sb[r] if (w == 1 and j == 1) else ub[w, r, j]
+        def source(w, r, j, a):
+            if w == 0:
+                return ub[w, r, j][:, 2 * a : 2 * a + 2, :]
+            return ub[w, r, 0][:, 2 * j : 2 * j + 2, :] if a == 0 else u_sb[r][:, j]
 
         def affine(w, r, b):
             if b == 0:
@@ -200,20 +203,22 @@ def tile_rebasedlinearattention_pa_t_kernel(
             )
 
         def transpose_back(w, r):
-            n = tiles_f(w)
+            n = width(r)
+            if w == 1:
+                ub[w, r, 0] = psum_u.tile([P, HEADS, D], F32, name="ub")
+                for j in range(n):
+                    for h in range(2):
+                        nc.tensor.transpose(ub[w, r, 0][:, 2 * j + h, :], u_t[w, r][:, (h * n + j) * P : (h * n + j + 1) * P], ident[:])
+                return
             for j in range(n):
                 ub[w, r, j] = psum_u.tile([P, HEADS, D], F32, name="ub")
                 for h in range(HEADS):
                     nc.tensor.transpose(ub[w, r, j][:, h, :], u_t[w, r][:, (h * n + j) * P : (h * n + j + 1) * P], ident[:])
 
-        def moments(w, r, j):
-            if j == 0:
+        def moments(w, r, j, a):
+            if (w, r) not in stats:
                 stats[w, r] = small.tile([P, MOST, HEADS // 2, 6], F32, name="stats")
-            for a in range(HEADS // 2):
-                nc.vector.bn_stats(
-                    out=stats[w, r][:, j, a, :],
-                    in_=source(w, r, j)[:, 2 * a : 2 * a + 2, :].rearrange("p h d -> p d h"),
-                )
+            nc.vector.bn_stats(out=stats[w, r][:, j, a, :], in_=source(w, r, j, a).rearrange("p h d -> p d h"))
 
         def by_block(w, r):
             return stats[w, r][:, 0 : width(r)].rearrange("p j a (h s) -> p (j a h) s", s=3)
@@ -233,22 +238,28 @@ def tile_rebasedlinearattention_pa_t_kernel(
             )
 
         def on_scalar(w, r):
-            if width(r) < MOST:
-                return ON_SCALAR_HALF[w]
-            return ON_SCALAR[w] if r < N_ROUNDS - LEAD else ON_SCALAR_LATE[w]
+            if r == N_ROUNDS - 1:
+                return ON_SCALAR_LAST[w]
+            return ON_SCALAR[w]
 
         def normalise(w, r, j, h):
             if (w, r, j) not in feat:
                 feat[w, r, j] = feat_pool.tile([P, HEADS, D], F32, name="feat")
             b = j * HEADS + h
-            if (j, h) in on_scalar(w, r):
+            if w == 1 and (j, h) in ON_GPSIMD and r < N_ROUNDS - 1:
+                nc.gpsimd.tensor_scalar(
+                    out=feat[w, r, j][:, h, :], in0=source(w, r, j, h // 2)[:, h % 2, :],
+                    scalar1=by_block(w, r)[:, b, 1:2], scalar2=rstd[w, r][:, b : b + 1],
+                    op0=ALU.subtract, op1=ALU.mult,
+                )
+            elif (j, h) in on_scalar(w, r):
                 nc.scalar.activation(
-                    out=feat[w, r, j][:, h, :], in_=source(w, r, j)[:, h, :], func=ACT.Identity,
+                    out=feat[w, r, j][:, h, :], in_=source(w, r, j, h // 2)[:, h % 2, :], func=ACT.Identity,
                     bias=shift[w, r][:, b : b + 1], scale=rstd[w, r][:, b : b + 1],
                 )
             else:
                 nc.vector.tensor_scalar(
-                    out=feat[w, r, j][:, h, :], in0=source(w, r, j)[:, h, :],
+                    out=feat[w, r, j][:, h, :], in0=source(w, r, j, h // 2)[:, h % 2, :],
                     scalar1=by_block(w, r)[:, b, 1:2], scalar2=rstd[w, r][:, b : b + 1],
                     op0=ALU.subtract, op1=ALU.mult,
                 )
@@ -283,25 +294,32 @@ def tile_rebasedlinearattention_pa_t_kernel(
             at(r - LEAD + T_Q, quantise_x, r)
             for w in range(2):
                 at(r + 0.01 * w, project, w, r)
-                for b in range(tiles_f(w)):
+                for b in range(banks_f(w)):
                     at(r + T_C[w] + 0.01 * b, affine, w, r, b)
                 at(r + T_BT[w], transpose_back, w, r)
-                for j in range(tiles_f(w)):
-                    at(r + T_D[w] + 0.01 * j, moments, w, r, j)
+                for j in range(n):
+                    for a in range(banks_f(w)):
+                        at(r + T_D[w] + 0.01 * j + 0.001 * a, moments, w, r, j, a)
                 if w == 1:
                     at(r + 0.02, project_tokens, r)
                     at(r + T_P1, times_gamma, r)
                     at(r + T_P1 + 0.001, plus_beta, r)
-                    at(r + T_P3, moments, 1, r, 1)
-                at(r + T_R[w], one_over_std, w, r)
+                    for j in range(n):
+                        at(r + (T_P3_LAST if r == N_ROUNDS - 1 else T_P3) + 0.001 * j, moments, 1, r, j, 1)
+                final = r == N_ROUNDS - 1
+                at(r + (T_R_LAST[w] if final else T_R[w]), one_over_std, w, r)
                 if on_scalar(w, r):
-                    at(r + T_S[w], minus_mean_over_std, w, r)
+                    at(r + (T_S_LAST[w] if final else T_S[w]), minus_mean_over_std, w, r)
                 i = 0
                 last = {}
                 for j in range(n):
                     for h in range(HEADS):
                         i += 1
                         when = r + (T_EA[w] if (j, h) in on_scalar(w, r) else T_EV[w][j]) + 0.001 * i
+                        if w == 1 and (j, h) in ON_GPSIMD:
+                            when = r + T_EG + 0.001 * i
+                        if final:
+                            when = r + T_E_LAST[w][j] + 0.001 * i
                         at(when, normalise, w, r, j, h)
                         last[j] = max(last.get(j, when), when)
                 for j in range(n):
@@ -313,6 +331,12 @@ def tile_rebasedlinearattention_pa_t_kernel(
 
 
 HEAD_ON_VECTOR = False
+ON_GPSIMD = ((0, 3), (1, 3))
+T_EG = 1.56
+T_R_LAST = (0.862, 0.895)
+T_S_LAST = (0.865, 0.0)
+T_P3_LAST = 0.87
+T_E_LAST = ((0.88, 0.90), (0.92, 0.94))
 T_P1 = 0.55
 T_P3 = 1.00
 T_C = (0.17, 0.44)

@@ -249,8 +249,8 @@ def tile_rebasedlinearattention_pa_t_kernel(
             if w == 1 and (j, h) in ON_GPSIMD and r < N_ROUNDS - 1:
                 nc.gpsimd.tensor_scalar(
                     out=feat[w, r, j][:, h, :], in0=source(w, r, j, h // 2)[:, h % 2, :],
-                    scalar1=by_block(w, r)[:, b, 1:2], scalar2=rstd[w, r][:, b : b + 1],
-                    op0=ALU.subtract, op1=ALU.mult,
+                    scalar1=rstd[w, r][:, b : b + 1], scalar2=shift[w, r][:, b : b + 1],
+                    op0=ALU.mult, op1=ALU.add,
                 )
             elif (j, h) in on_scalar(w, r):
                 nc.scalar.activation(

@@ -18,22 +18,31 @@ HID = 1024
 K_PASS = 512
 PASSES = HID // K_PASS
 HEADS = 4
+PAIRS = HEADS // 2
 D = 128
 COLS = HEADS * D
-BANK = 512
 LN_EPS = 1e-5
-N_TILES = TOKENS // P
-MOST = 2
+TILES = 2
+ROUND = TILES * P
+N_ROUNDS = TOKENS // ROUND
+Q, K = 0, 1
+
+X_LEAD = 2
+LOAD_LEAD = 5
 
 FLOPS = 2 * TOKENS * HID * 2 * COLS
 
-ROUNDS = [[2 * r, 2 * r + 1] for r in range(N_TILES // 2)]
-N_ROUNDS = len(ROUNDS)
-LEAD = 2
 
-ON_SCALAR = (((1, 2), (1, 3)), ((0, 0), (0, 1), (0, 2), (0, 3), (1, 0), (1, 1), (1, 2), (1, 3)))
-ON_SCALAR_LATE = (((1, 3),), ((0, 0), (0, 1), (0, 2), (0, 3), (1, 0), (1, 1), (1, 2), (1, 3)))
-ON_SCALAR_LAST = (((0, 0), (0, 1), (0, 2), (0, 3), (1, 0), (1, 1), (1, 2), (1, 3)), ())
+def features_first(w):
+    return (0, 1) if w == Q else (0,)
+
+
+def normaliser(w, r, j, h):
+    if r == N_ROUNDS - 1:
+        return "scalar" if w == Q else "vector"
+    if w == K:
+        return "gpsimd" if h == 3 else "scalar"
+    return "scalar" if (j == 1 and h >= 2) else "vector"
 
 
 def tile_rebasedlinearattention_pa_t_kernel(
@@ -45,47 +54,41 @@ def tile_rebasedlinearattention_pa_t_kernel(
 
     with ExitStack() as ctx:
         const = ctx.enter_context(tc.tile_pool(name="const", bufs=1))
-        x_pool = ctx.enter_context(tc.tile_pool(name="x", bufs=7))
+        x_pool = ctx.enter_context(tc.tile_pool(name="x", bufs=LOAD_LEAD - X_LEAD + 2))
         stage = ctx.enter_context(tc.tile_pool(name="stage", bufs=4))
         u_pool = ctx.enter_context(tc.tile_pool(name="u", bufs=4))
         k_pool = ctx.enter_context(tc.tile_pool(name="k", bufs=4))
-        feat_pool = ctx.enter_context(tc.tile_pool(name="feat", bufs=10))
+        feat_pool = ctx.enter_context(tc.tile_pool(name="feat", bufs=12))
         small = ctx.enter_context(tc.tile_pool(name="small", bufs=8))
-        psum_s = ctx.enter_context(tc.psum_pool(name="psum_s", bufs=4))
-        psum_u = ctx.enter_context(tc.psum_pool(name="psum_u", bufs=4))
+        psum_in = ctx.enter_context(tc.psum_pool(name="psum_in", bufs=4))
+        psum_back = ctx.enter_context(tc.psum_pool(name="psum_back", bufs=4))
 
         ident = const.tile([P, P], F32)
         make_identity(nc, ident[:])
-        gb_row = const.tile([P, 2 * D], BF16)
-        nc.vector.memset(gb_row[:], 0.0)
         w_planes = const.tile([P, 2, PASSES, COLS], U8, align_bytes=64)
         nc.vector.memset(w_planes[:].rearrange("p w g n -> p (w g n)").bitcast(I32), 0)
         w_codes = const.tile([P, 2, PASSES, COLS], U32, align_bytes=64)
         eps = const.tile([P, 2], F32)
-        nc.vector.memset(eps[:, 0:1], D * LN_EPS)
-        nc.vector.memset(eps[:, 1:2], LN_EPS)
+        nc.vector.memset(eps[:, Q : Q + 1], D * LN_EPS)
+        nc.vector.memset(eps[:, K : K + 1], LN_EPS)
+        gb_row = const.tile([P, 2, D], BF16)
+        nc.vector.memset(gb_row[:], 0.0)
         ones = const.tile([P, P], BF16)
         nc.vector.memset(ones[:], 1.0)
         warm = const.tile([P, 2], F32)
         nc.scalar.activation(out=warm[:], in_=eps[:], func=ACT.Abs_reciprocal_sqrt)
-        gb = const.tile([P, 2], F32)
-        gb_rows = const.tile([P, 2, 2, D], F32)
-        vk, t_sb, u_sb = {}, {}, {}
+        gb_column = const.tile([P, 2], F32)
+        gb_spread = const.tile([P, 2, 2, D], F32)
 
         x_sb, xt, grouped, x_codes, x_planes = {}, {}, {}, {}, {}
-        vt, u_t, ub, feat = {}, {}, {}, {}
+        product, u_t, back, scaled, shifted, feat = {}, {}, {}, {}, {}, {}
         stats, rstd, shift = {}, {}, {}
 
-        def width(r):
-            return len(ROUNDS[r])
-
         def load_x(r):
-            n = width(r)
-            x_sb[r] = x_pool.tile([P, MOST, HID], BF16, name="x_sb")
-            first = ROUNDS[r][0] * P
+            x_sb[r] = x_pool.tile([P, TILES, HID], BF16, name="x_sb")
             nc.sync.dma_start(
-                out=x_sb[r][:, 0:n, :],
-                in_=x_rows[first : first + n * P, :].rearrange("(j p) k -> p j k", p=P),
+                out=x_sb[r][:],
+                in_=x_rows[r * ROUND : (r + 1) * ROUND, :].rearrange("(j p) k -> p j k", p=P),
             )
 
         def load_weight(w, words, scales):
@@ -93,261 +96,245 @@ def tile_rebasedlinearattention_pa_t_kernel(
                 out=w_codes[:, w].bitcast(I32),
                 in_=words.rearrange("g p n t -> p g (n t)").bitcast(I32),
             )
-            for quad in range(4):
+            for b in range(4):
                 nc.sync.dma_start(
-                    out=w_planes[32 * quad : 32 * quad + 4, w].bitcast(I32),
-                    in_=scales[:, 4 * quad : 4 * quad + 4, :].rearrange("g r n -> r g n").bitcast(I32),
+                    out=w_planes[32 * b : 32 * b + 4, w].bitcast(I32),
+                    in_=scales[:, 4 * b : 4 * b + 4, :].rearrange("g r n -> r g n").bitcast(I32),
                 )
 
         def load_gamma_beta():
-            nc.sync.dma_start(out=gb_row[0:1, 0:D], in_=gamma.rearrange("(o d) -> o d", o=1))
-            nc.sync.dma_start(out=gb_row[0:1, D : 2 * D], in_=beta.rearrange("(o d) -> o d", o=1))
+            nc.sync.dma_start(out=gb_row[0:1, 0, :], in_=gamma.rearrange("(o d) -> o d", o=1))
+            nc.sync.dma_start(out=gb_row[0:1, 1, :], in_=beta.rearrange("(o d) -> o d", o=1))
 
-        def gamma_beta_columns():
-            bank = psum_u.tile([P, HEADS, D], F32, name="ub")
+        def spread_gamma_beta():
+            bank = psum_back.tile([P, HEADS, D], F32, name="back")
             for i in range(2):
-                nc.tensor.matmul(out=bank[:, i, 0:2], lhsT=gb_row[:, i * D : (i + 1) * D], rhs=ones[:, 0:2], start=True, stop=True)
-            nc.vector.tensor_copy(out=gb[:], in_=bank[:, 0:2, 0])
-
-        def gamma_beta_rows():
-            bank = psum_u.tile([P, HEADS, D], F32, name="ub")
+                nc.tensor.matmul(out=bank[:, i, 0:2], lhsT=gb_row[:, i, :], rhs=ones[:, 0:2], start=True, stop=True)
+            nc.vector.tensor_copy(out=gb_column[:], in_=bank[:, 0:2, 0])
+            bank = psum_back.tile([P, HEADS, D], F32, name="back")
             for i in range(2):
                 for twice in range(2):
-                    nc.tensor.matmul(out=bank[:, 2 * i + twice, :], lhsT=ones[:], rhs=gb_row[:, i * D : (i + 1) * D], start=True, stop=True)
-            nc.vector.tensor_copy(out=gb_rows[:].rearrange("p i t d -> p (i t) d"), in_=bank[:])
+                    nc.tensor.matmul(out=bank[:, 2 * i + twice, :], lhsT=ones[:], rhs=gb_row[:, i, :], start=True, stop=True)
+            nc.vector.tensor_copy(out=gb_spread[:].rearrange("p i t d -> p (i t) d"), in_=bank[:])
 
         def transpose_x(r, j):
             x_words = x_sb[r][:, j, :].bitcast(F32)
-            xt[r, j] = psum_s.tile([P, PASSES * 2, P], F32, name="shared")
+            xt[r, j] = psum_in.tile([P, PASSES * 2, P], F32, name="bank")
             for g in range(PASSES):
                 for u in range(2):
                     nc.tensor.transpose(xt[r, j][:, 2 * g + u, :], x_words[:, 256 * g + u : 256 * (g + 1) : 2], ident[:])
 
         def copy_x(r, j):
-            n = width(r)
             if j == 0:
-                grouped[r] = stage.tile([P, MOST * HID], BF16, align_bytes=64, name="grouped")
-            grouped_words = grouped[r][:, 0 : n * HID].bitcast(F32).rearrange("p (g r u) -> p g r u", g=PASSES, u=2)
-            planes = xt[r, j][:].rearrange("p (g u) r -> p g r u", u=2)
-            if r == 0 and j == width(r) - 1 and HEAD_ON_VECTOR:
-                nc.vector.tensor_copy(out=grouped_words[:, :, j * P : (j + 1) * P, :], in_=planes)
-            else:
-                nc.scalar.copy(out=grouped_words[:, :, j * P : (j + 1) * P, :], in_=planes)
+                grouped[r] = stage.tile([P, PASSES, ROUND, 4], BF16, align_bytes=64, name="grouped")
+            words = (
+                grouped[r][:].rearrange("p g r t -> p (g r t)").bitcast(F32).rearrange("p (g r u) -> p g r u", g=PASSES, u=2)
+            )
+            nc.scalar.copy(out=words[:, :, j * P : (j + 1) * P, :], in_=xt[r, j][:].rearrange("p (g u) r -> p g r u", u=2))
 
         def quantise_x(r):
-            n = width(r)
-            x_codes[r] = stage.tile([P, MOST * HID // 4], U32, align_bytes=64, name="x_codes")
-            x_planes[r] = stage.tile([P, MOST * HID // 4], U8, align_bytes=64, name="x_planes")
+            x_codes[r] = stage.tile([P, PASSES, ROUND], U32, align_bytes=64, name="x_codes")
+            x_planes[r] = stage.tile([P, PASSES, ROUND], U8, align_bytes=64, name="x_planes")
             nc.vector.quantize_mx(
-                out=x_codes[r][:, 0 : n * HID // 4].bitcast(FP8X4),
-                scales=x_planes[r][:, 0 : n * HID // 4],
-                in_=grouped[r][:, 0 : n * HID],
+                out=x_codes[r][:].rearrange("p g r -> p (g r)").bitcast(FP8X4),
+                scales=x_planes[r][:].rearrange("p g r -> p (g r)"),
+                in_=grouped[r][:].rearrange("p g r t -> p (g r t)"),
             )
 
-        def banks_f(w):
-            return 2 if w == 0 else 1
-
-        def project(w, r):
-            all_tokens = width(r) * P
-            tokens = all_tokens
-            per_bank = BANK // tokens
-            for b in range(banks_f(w)):
-                vt[w, r, b] = psum_s.tile([P, BANK], F32, name="shared")
-                for i in range(per_bank):
-                    h = per_bank * b + i
+        def project_features_first(w, r):
+            for a in features_first(w):
+                product[w, r, a] = psum_in.tile([P, 2, ROUND], F32, name="bank")
+                for i in range(2):
+                    h = 2 * a + i
                     for g in range(PASSES):
                         nc.tensor.matmul_mx(
-                            out=vt[w, r, b][:, i * tokens : (i + 1) * tokens],
+                            out=product[w, r, a][:, i, :],
                             lhsT=w_codes[:, w, g, h * D : (h + 1) * D].bitcast(FP8X4),
                             lhsT_scale=w_planes[:, w, g, h * D : (h + 1) * D],
-                            rhs=x_codes[r][:, g * all_tokens : g * all_tokens + tokens].bitcast(FP8X4),
-                            rhs_scale=x_planes[r][:, g * all_tokens : g * all_tokens + tokens],
+                            rhs=x_codes[r][:, g, :].bitcast(FP8X4),
+                            rhs_scale=x_planes[r][:, g, :],
                             start=(g == 0), stop=(g == PASSES - 1),
                         )
 
-        def project_tokens(r):
-            all_tokens = width(r) * P
-            vk[r] = psum_s.tile([P, MOST, 2, D], F32, name="shared")
-            for j in range(MOST):
+        def project_tokens_first(r):
+            product[K, r, 1] = psum_in.tile([P, TILES, 2, D], F32, name="bank")
+            for j in range(TILES):
                 for g in range(PASSES):
                     nc.tensor.matmul_mx(
-                        out=vk[r][:, j].rearrange("p h d -> p (h d)"),
-                        lhsT=x_codes[r][:, g * all_tokens + j * P : g * all_tokens + (j + 1) * P].bitcast(FP8X4),
-                        lhsT_scale=x_planes[r][:, g * all_tokens + j * P : g * all_tokens + (j + 1) * P],
-                        rhs=w_codes[:, 1, g, 2 * D : 4 * D].bitcast(FP8X4),
-                        rhs_scale=w_planes[:, 1, g, 2 * D : 4 * D],
+                        out=product[K, r, 1][:, j].rearrange("p h d -> p (h d)"),
+                        lhsT=x_codes[r][:, g, j * P : (j + 1) * P].bitcast(FP8X4),
+                        lhsT_scale=x_planes[r][:, g, j * P : (j + 1) * P],
+                        rhs=w_codes[:, K, g, 2 * D : 4 * D].bitcast(FP8X4),
+                        rhs_scale=w_planes[:, K, g, 2 * D : 4 * D],
                         start=(g == 0), stop=(g == PASSES - 1),
                     )
 
-        def times_gamma(r):
-            t_sb[r] = k_pool.tile([P, MOST, 2, D], F32, name="t_sb")
-            for j in range(MOST):
-                nc.vector.tensor_tensor(out=t_sb[r][:, j], in0=vk[r][:, j], in1=gb_rows[:, 0], op=ALU.mult)
-
-        def plus_beta(r):
-            u_sb[r] = k_pool.tile([P, MOST, 2, D], F32, name="u_sb")
-            for j in range(MOST):
-                nc.gpsimd.tensor_tensor(out=u_sb[r][:, j], in0=t_sb[r][:, j], in1=gb_rows[:, 1], op=ALU.add)
-
-        def source(w, r, j, a):
-            if w == 0:
-                return ub[w, r, j][:, 2 * a : 2 * a + 2, :]
-            return ub[w, r, 0][:, 2 * j : 2 * j + 2, :] if a == 0 else u_sb[r][:, j]
-
-        def affine(w, r, b):
-            if b == 0:
-                u_t[w, r] = u_pool.tile([P, MOST * BANK], F32, name="u_t")
+        def affine(w, r, a):
+            if a == 0:
+                u_t[w, r] = u_pool.tile([P, HEADS, ROUND], F32, name="u_t")
             nc.scalar.activation(
-                out=u_t[w, r][:, b * BANK : (b + 1) * BANK], in_=vt[w, r, b][:],
-                func=ACT.Identity, bias=gb[:, 1:2], scale=gb[:, 0:1],
+                out=u_t[w, r][:, 2 * a : 2 * a + 2, :], in_=product[w, r, a][:],
+                func=ACT.Identity, bias=gb_column[:, 1:2], scale=gb_column[:, 0:1],
             )
 
         def transpose_back(w, r):
-            n = width(r)
-            if w == 1:
-                ub[w, r, 0] = psum_u.tile([P, HEADS, D], F32, name="ub")
-                for j in range(n):
-                    for h in range(2):
-                        nc.tensor.transpose(ub[w, r, 0][:, 2 * j + h, :], u_t[w, r][:, (h * n + j) * P : (h * n + j + 1) * P], ident[:])
-                return
-            for j in range(n):
-                ub[w, r, j] = psum_u.tile([P, HEADS, D], F32, name="ub")
-                for h in range(HEADS):
-                    nc.tensor.transpose(ub[w, r, j][:, h, :], u_t[w, r][:, (h * n + j) * P : (h * n + j + 1) * P], ident[:])
+            if w == K:
+                back[w, r, 0] = psum_back.tile([P, TILES, 2, D], F32, name="back")
+            for j in range(TILES):
+                if w == Q:
+                    back[w, r, j] = psum_back.tile([P, PAIRS, 2, D], F32, name="back")
+                for a in features_first(w):
+                    for i in range(2):
+                        bank = back[w, r, j][:, a] if w == Q else back[w, r, 0][:, j]
+                        nc.tensor.transpose(bank[:, i, :], u_t[w, r][:, 2 * a + i, j * P : (j + 1) * P], ident[:])
+
+        def times_gamma(r):
+            scaled[r] = k_pool.tile([P, TILES, 2, D], F32, name="scaled")
+            for j in range(TILES):
+                nc.vector.tensor_tensor(out=scaled[r][:, j], in0=product[K, r, 1][:, j], in1=gb_spread[:, 0], op=ALU.mult)
+
+        def plus_beta(r):
+            shifted[r] = k_pool.tile([P, TILES, 2, D], F32, name="shifted")
+            for j in range(TILES):
+                nc.gpsimd.tensor_tensor(out=shifted[r][:, j], in0=scaled[r][:, j], in1=gb_spread[:, 1], op=ALU.add)
+
+        def pair(w, r, j, a):
+            if w == Q:
+                return back[w, r, j][:, a]
+            return back[w, r, 0][:, j] if a == 0 else shifted[r][:, j]
 
         def moments(w, r, j, a):
             if (w, r) not in stats:
-                stats[w, r] = small.tile([P, MOST, HEADS // 2, 6], F32, name="stats")
-            nc.vector.bn_stats(out=stats[w, r][:, j, a, :], in_=source(w, r, j, a).rearrange("p h d -> p d h"))
+                stats[w, r] = small.tile([P, TILES, PAIRS, 6], F32, name="stats")
+            nc.vector.bn_stats(out=stats[w, r][:, j, a, :], in_=pair(w, r, j, a).rearrange("p h d -> p d h"))
 
         def by_block(w, r):
-            return stats[w, r][:, 0 : width(r)].rearrange("p j a (h s) -> p (j a h) s", s=3)
+            return stats[w, r][:].rearrange("p j a (h s) -> p (j a h) s", s=3)
 
         def one_over_std(w, r):
-            rstd[w, r] = small.tile([P, MOST * HEADS], F32, name="rstd")
+            rstd[w, r] = small.tile([P, TILES * HEADS], F32, name="rstd")
             nc.scalar.activation(
-                out=rstd[w, r][:, 0 : width(r) * HEADS], in_=by_block(w, r)[:, :, 2], func=ACT.Abs_reciprocal_sqrt,
-                bias=eps[:, w : w + 1], scale=(1.0 if w == 0 else 1.0 / D),
+                out=rstd[w, r][:], in_=by_block(w, r)[:, :, 2], func=ACT.Abs_reciprocal_sqrt,
+                bias=eps[:, w : w + 1], scale=(1.0 if w == Q else 1.0 / D),
             )
 
         def minus_mean_over_std(w, r):
-            shift[w, r] = small.tile([P, MOST * HEADS], F32, name="shift")
+            shift[w, r] = small.tile([P, TILES * HEADS], F32, name="shift")
             nc.vector.scalar_tensor_tensor(
-                out=shift[w, r][:, 0 : width(r) * HEADS], in0=by_block(w, r)[:, :, 1], scalar=-1.0,
-                in1=rstd[w, r][:, 0 : width(r) * HEADS], op0=ALU.mult, op1=ALU.mult,
+                out=shift[w, r][:], in0=by_block(w, r)[:, :, 1], scalar=-1.0, in1=rstd[w, r][:],
+                op0=ALU.mult, op1=ALU.mult,
             )
-
-        def on_scalar(w, r):
-            if r == N_ROUNDS - 1:
-                return ON_SCALAR_LAST[w]
-            return ON_SCALAR[w]
 
         def normalise(w, r, j, h):
             if (w, r, j) not in feat:
                 feat[w, r, j] = feat_pool.tile([P, HEADS, D], F32, name="feat")
             b = j * HEADS + h
-            if w == 1 and (j, h) in ON_GPSIMD and r < N_ROUNDS - 1:
-                nc.gpsimd.tensor_scalar(
-                    out=feat[w, r, j][:, h, :], in0=source(w, r, j, h // 2)[:, h % 2, :],
-                    scalar1=rstd[w, r][:, b : b + 1], scalar2=shift[w, r][:, b : b + 1],
-                    op0=ALU.mult, op1=ALU.add,
-                )
-            elif (j, h) in on_scalar(w, r):
+            out, value = feat[w, r, j][:, h, :], pair(w, r, j, h // 2)[:, h % 2, :]
+            engine = normaliser(w, r, j, h)
+            if engine == "scalar":
                 nc.scalar.activation(
-                    out=feat[w, r, j][:, h, :], in_=source(w, r, j, h // 2)[:, h % 2, :], func=ACT.Identity,
-                    bias=shift[w, r][:, b : b + 1], scale=rstd[w, r][:, b : b + 1],
+                    out=out, in_=value, func=ACT.Identity, bias=shift[w, r][:, b : b + 1], scale=rstd[w, r][:, b : b + 1]
+                )
+            elif engine == "gpsimd":
+                nc.gpsimd.tensor_scalar(
+                    out=out, in0=value, scalar1=rstd[w, r][:, b : b + 1], scalar2=shift[w, r][:, b : b + 1],
+                    op0=ALU.mult, op1=ALU.add,
                 )
             else:
                 nc.vector.tensor_scalar(
-                    out=feat[w, r, j][:, h, :], in0=source(w, r, j, h // 2)[:, h % 2, :],
-                    scalar1=by_block(w, r)[:, b, 1:2], scalar2=rstd[w, r][:, b : b + 1],
+                    out=out, in0=value, scalar1=by_block(w, r)[:, b, 1:2], scalar2=rstd[w, r][:, b : b + 1],
                     op0=ALU.subtract, op1=ALU.mult,
                 )
 
+        def normalise_on(engine, w, r, j):
+            for h in range(HEADS):
+                if normaliser(w, r, j, h) == engine:
+                    normalise(w, r, j, h)
+
         def store(w, r, j):
-            t = ROUNDS[r][j]
+            t = r * TILES + j
             nc.sync.dma_start(out=out_rows[w][t * P : (t + 1) * P, :], in_=feat[w, r, j][:].rearrange("p h d -> p (h d)"))
 
-        plan = []
-
-        def at(when, fn, *args):
-            plan.append((when, len(plan), fn, args))
-
-        at(-9.0, load_x, 0)
-        at(-8.9, load_weight, 0, Wq_words, Wq_scales)
-        at(-8.8, load_x, 1)
-        at(-8.7, load_gamma_beta)
-        at(-8.6, load_weight, 1, Wk_words, Wk_scales)
-        for r in range(2, 5):
-            at(-8.5 + 0.01 * r, load_x, r)
-        at(-0.05, gamma_beta_columns)
-        at(-0.04, gamma_beta_rows)
-        for r in range(N_ROUNDS):
-            n = width(r)
-            if r >= 5:
-                at(r - 5 + 0.5, load_x, r)
-            at(r - LEAD + T_XA, transpose_x, r, 0)
-            at(r - LEAD + T_A0, copy_x, r, 0)
-            if n > 1:
-                at(r - LEAD + T_XB, transpose_x, r, 1)
-                at(r - LEAD + T_A1, copy_x, r, 1)
-            at(r - LEAD + T_Q, quantise_x, r)
-            for w in range(2):
-                at(r + 0.01 * w, project, w, r)
-                for b in range(banks_f(w)):
-                    at(r + T_C[w] + 0.01 * b, affine, w, r, b)
-                at(r + T_BT[w], transpose_back, w, r)
-                for j in range(n):
-                    for a in range(banks_f(w)):
-                        at(r + T_D[w] + 0.01 * j + 0.001 * a, moments, w, r, j, a)
-                if w == 1:
-                    at(r + 0.02, project_tokens, r)
-                    at(r + T_P1, times_gamma, r)
-                    at(r + T_P1 + 0.001, plus_beta, r)
-                    for j in range(n):
-                        at(r + (T_P3_LAST if r == N_ROUNDS - 1 else T_P3) + 0.001 * j, moments, 1, r, j, 1)
-                final = r == N_ROUNDS - 1
-                at(r + (T_R_LAST[w] if final else T_R[w]), one_over_std, w, r)
-                if on_scalar(w, r):
-                    at(r + (T_S_LAST[w] if final else T_S[w]), minus_mean_over_std, w, r)
-                i = 0
-                last = {}
-                for j in range(n):
-                    for h in range(HEADS):
-                        i += 1
-                        when = r + (T_EA[w] if (j, h) in on_scalar(w, r) else T_EV[w][j]) + 0.001 * i
-                        if w == 1 and (j, h) in ON_GPSIMD:
-                            when = r + T_EG + 0.001 * i
-                        if final:
-                            when = r + T_E_LAST[w][j] + 0.001 * i
-                        at(when, normalise, w, r, j, h)
-                        last[j] = max(last.get(j, when), when)
-                for j in range(n):
-                    at(last[j] + 0.0005, store, w, r, j)
+        load_x(0)
+        load_weight(Q, Wq_words, Wq_scales)
+        load_x(1)
+        load_gamma_beta()
+        load_weight(K, Wk_words, Wk_scales)
+        for r in range(2, LOAD_LEAD):
+            load_x(r)
 
         with tc.manual_schedule():
-            for when, i, fn, args in sorted(plan, key=lambda e: (e[0], e[1])):
-                fn(*args)
+            for r in range(-X_LEAD, N_ROUNDS):
+                old, ahead = r - 1, r + X_LEAD
+                if old >= 0:
+                    for j in range(TILES):
+                        moments(K, old, j, 1)
+                if r >= 0:
+                    project_features_first(Q, r)
+                    project_features_first(K, r)
+                    project_tokens_first(r)
+                if old >= 0:
+                    normalise_on("vector", Q, old, 1)
+                if r >= 0:
+                    affine(Q, r, 0)
+                    affine(Q, r, 1)
+                if old >= 0:
+                    one_over_std(K, old)
+                    minus_mean_over_std(Q, old)
+                    minus_mean_over_std(K, old)
+                if r >= 0:
+                    affine(K, r, 0)
+                if 0 <= r + 1 < N_ROUNDS:
+                    quantise_x(r + 1)
+                if old >= 0:
+                    normalise_on("scalar", Q, old, 1)
+                    store(Q, old, 1)
+                    normalise_on("scalar", K, old, 0)
+                    normalise_on("scalar", K, old, 1)
+                if r >= 0:
+                    transpose_back(Q, r)
+                    if r + LOAD_LEAD < N_ROUNDS:
+                        load_x(r + LOAD_LEAD)
+                    times_gamma(r)
+                    plus_beta(r)
+                if old >= 0:
+                    for j in range(TILES):
+                        normalise_on("gpsimd", K, old, j)
+                        store(K, old, j)
+                if r >= 0:
+                    for j in range(TILES):
+                        for a in range(PAIRS):
+                            moments(Q, r, j, a)
+                if ahead < N_ROUNDS:
+                    transpose_x(ahead, 0)
+                if r >= 0:
+                    transpose_back(K, r)
+                if ahead < N_ROUNDS:
+                    copy_x(ahead, 0)
+                if r >= 0:
+                    moments(K, r, 0, 0)
+                    one_over_std(Q, r)
+                    if r == N_ROUNDS - 1:
+                        minus_mean_over_std(Q, r)
+                    moments(K, r, 1, 0)
+                if ahead < N_ROUNDS:
+                    transpose_x(ahead, 1)
+                if r == -1:
+                    spread_gamma_beta()
+                if 0 <= r < N_ROUNDS - 1:
+                    normalise_on("vector", Q, r, 0)
+                    store(Q, r, 0)
+                if ahead < N_ROUNDS:
+                    copy_x(ahead, 1)
 
-
-HEAD_ON_VECTOR = False
-ON_GPSIMD = ((0, 3), (1, 3))
-T_EG = 1.56
-T_R_LAST = (0.862, 0.895)
-T_S_LAST = (0.865, 0.0)
-T_P3_LAST = 0.87
-T_E_LAST = ((0.88, 0.90), (0.92, 0.94))
-T_P1 = 0.55
-T_P3 = 1.00
-T_C = (0.17, 0.44)
-T_BT = (0.49, 0.73)
-T_XA = 0.62
-T_XB = 0.87
-T_A0 = 0.79
-T_A1 = 0.99
-T_D = (0.61, 0.86)
-T_R = (0.862, 1.43)
-T_S = (1.434, 1.435)
-T_EA = (1.455, 1.46)
-T_EV = ((0.90, 1.10), (1.30, 1.30))
-T_Q = 1.45
+            last = N_ROUNDS - 1
+            for j in range(TILES):
+                moments(K, last, j, 1)
+            normalise_on("scalar", Q, last, 0)
+            store(Q, last, 0)
+            one_over_std(K, last)
+            normalise_on("scalar", Q, last, 1)
+            store(Q, last, 1)
+            for j in range(TILES):
+                normalise_on("vector", K, last, j)
+                store(K, last, j)

@@ -305,11 +305,10 @@ def tile_rebasedlinearattention_pa_t_kernel(
                     for j in range(TILES):
                         for a in range(PAIRS):
                             moments(Q, r, j, a)
-                if ahead < N_ROUNDS:
-                    transpose_x(ahead, 0)
                 if r >= 0:
                     transpose_back(K, r)
                 if ahead < N_ROUNDS:
+                    transpose_x(ahead, 0)
                     copy_x(ahead, 0)
                 if r >= 0:
                     moments(K, r, 0, 0)

@@ -33,16 +33,14 @@ LOAD_LEAD = 5
 FLOPS = 2 * TOKENS * HID * 2 * COLS
 
 
-def features_first(w):
-    return (0, 1) if w == Q else (0,)
-
-
 def normaliser(w, r, j, h):
-    if r == N_ROUNDS - 1:
-        return "scalar" if w == Q else "vector"
+    if w == K and r == N_ROUNDS - 1:
+        return ("scalar", "vector", "vector", "scalar")[h]
+    if w == K and r == N_ROUNDS - 2:
+        return ("vector", "vector", "vector", "gpsimd")[h]
     if w == K:
-        return "gpsimd" if h == 3 else "scalar"
-    return "scalar" if (j == 1 and h >= 2) else "vector"
+        return "gpsimd" if h == 3 or (h == 2 and j == 0) else "scalar"
+    return "scalar"
 
 
 def tile_rebasedlinearattention_pa_t_kernel(
@@ -78,7 +76,7 @@ def tile_rebasedlinearattention_pa_t_kernel(
         warm = const.tile([P, 2], F32)
         nc.scalar.activation(out=warm[:], in_=eps[:], func=ACT.Abs_reciprocal_sqrt)
         gb_column = const.tile([P, 2], F32)
-        gb_spread = const.tile([P, 2, 2, D], F32)
+        gb_spread = const.tile([P, 2, HEADS, D], F32)
 
         x_sb, xt, grouped, x_codes, x_planes = {}, {}, {}, {}, {}
         product, u_t, back, scaled, shifted, feat = {}, {}, {}, {}, {}, {}
@@ -112,10 +110,12 @@ def tile_rebasedlinearattention_pa_t_kernel(
                 nc.tensor.matmul(out=bank[:, i, 0:2], lhsT=gb_row[:, i, :], rhs=ones[:, 0:2], start=True, stop=True)
             nc.vector.tensor_copy(out=gb_column[:], in_=bank[:, 0:2, 0])
             bank = psum_back.tile([P, HEADS, D], F32, name="back")
-            for i in range(2):
-                for twice in range(2):
-                    nc.tensor.matmul(out=bank[:, 2 * i + twice, :], lhsT=ones[:], rhs=gb_row[:, i, :], start=True, stop=True)
-            nc.vector.tensor_copy(out=gb_spread[:].rearrange("p i t d -> p (i t) d"), in_=bank[:])
+            nc.tensor.matmul(
+                out=bank[:, 0:2, :].rearrange("p i d -> p (i d)"), lhsT=ones[:],
+                rhs=gb_row[:].rearrange("p i d -> p (i d)"), start=True, stop=True,
+            )
+            for h in range(HEADS):
+                nc.vector.tensor_copy(out=gb_spread[:, :, h, :], in_=bank[:, 0:2, :])
 
         def transpose_x(r, j):
             x_words = x_sb[r][:, j, :].bitcast(F32)
@@ -141,108 +141,110 @@ def tile_rebasedlinearattention_pa_t_kernel(
                 in_=grouped[r][:].rearrange("p g r t -> p (g r t)"),
             )
 
-        def project_features_first(w, r):
-            for a in features_first(w):
-                product[w, r, a] = psum_in.tile([P, 2, ROUND], F32, name="bank")
+        def project_q(r):
+            for a in range(PAIRS):
+                product[Q, r, a] = psum_in.tile([P, 2, ROUND], F32, name="bank")
                 for i in range(2):
                     h = 2 * a + i
                     for g in range(PASSES):
                         nc.tensor.matmul_mx(
-                            out=product[w, r, a][:, i, :],
-                            lhsT=w_codes[:, w, g, h * D : (h + 1) * D].bitcast(FP8X4),
-                            lhsT_scale=w_planes[:, w, g, h * D : (h + 1) * D],
+                            out=product[Q, r, a][:, i, :],
+                            lhsT=w_codes[:, Q, g, h * D : (h + 1) * D].bitcast(FP8X4),
+                            lhsT_scale=w_planes[:, Q, g, h * D : (h + 1) * D],
                             rhs=x_codes[r][:, g, :].bitcast(FP8X4),
                             rhs_scale=x_planes[r][:, g, :],
                             start=(g == 0), stop=(g == PASSES - 1),
                         )
 
-        def project_tokens_first(r):
-            product[K, r, 1] = psum_in.tile([P, TILES, 2, D], F32, name="bank")
+        def project_k(r):
             for j in range(TILES):
+                product[K, r, j] = psum_in.tile([P, HEADS, D], F32, name="bank")
                 for g in range(PASSES):
                     nc.tensor.matmul_mx(
-                        out=product[K, r, 1][:, j].rearrange("p h d -> p (h d)"),
+                        out=product[K, r, j][:].rearrange("p h d -> p (h d)"),
                         lhsT=x_codes[r][:, g, j * P : (j + 1) * P].bitcast(FP8X4),
                         lhsT_scale=x_planes[r][:, g, j * P : (j + 1) * P],
-                        rhs=w_codes[:, K, g, 2 * D : 4 * D].bitcast(FP8X4),
-                        rhs_scale=w_planes[:, K, g, 2 * D : 4 * D],
+                        rhs=w_codes[:, K, g, :].bitcast(FP8X4),
+                        rhs_scale=w_planes[:, K, g, :],
                         start=(g == 0), stop=(g == PASSES - 1),
                     )
 
-        def affine(w, r, a):
+        def affine(r, a):
             if a == 0:
-                u_t[w, r] = u_pool.tile([P, HEADS, ROUND], F32, name="u_t")
+                u_t[r] = u_pool.tile([P, HEADS, ROUND], F32, name="u_t")
             nc.scalar.activation(
-                out=u_t[w, r][:, 2 * a : 2 * a + 2, :], in_=product[w, r, a][:],
+                out=u_t[r][:, 2 * a : 2 * a + 2, :], in_=product[Q, r, a][:],
                 func=ACT.Identity, bias=gb_column[:, 1:2], scale=gb_column[:, 0:1],
             )
 
-        def transpose_back(w, r):
-            if w == K:
-                back[w, r, 0] = psum_back.tile([P, TILES, 2, D], F32, name="back")
+        def transpose_back(r):
             for j in range(TILES):
-                if w == Q:
-                    back[w, r, j] = psum_back.tile([P, PAIRS, 2, D], F32, name="back")
-                for a in features_first(w):
-                    for i in range(2):
-                        bank = back[w, r, j][:, a] if w == Q else back[w, r, 0][:, j]
-                        nc.tensor.transpose(bank[:, i, :], u_t[w, r][:, 2 * a + i, j * P : (j + 1) * P], ident[:])
+                back[r, j] = psum_back.tile([P, HEADS, D], F32, name="back")
+                for h in range(HEADS):
+                    nc.tensor.transpose(back[r, j][:, h, :], u_t[r][:, h, j * P : (j + 1) * P], ident[:])
 
-        def times_gamma(r):
-            scaled[r] = k_pool.tile([P, TILES, 2, D], F32, name="scaled")
-            for j in range(TILES):
-                nc.vector.tensor_tensor(out=scaled[r][:, j], in0=product[K, r, 1][:, j], in1=gb_spread[:, 0], op=ALU.mult)
+        def times_gamma(r, j):
+            if j == 0:
+                scaled[r] = k_pool.tile([P, TILES, HEADS, D], F32, name="scaled")
+            nc.vector.tensor_tensor(out=scaled[r][:, j], in0=product[K, r, j][:], in1=gb_spread[:, 0], op=ALU.mult)
 
-        def plus_beta(r):
-            shifted[r] = k_pool.tile([P, TILES, 2, D], F32, name="shifted")
-            for j in range(TILES):
-                nc.gpsimd.tensor_tensor(out=shifted[r][:, j], in0=scaled[r][:, j], in1=gb_spread[:, 1], op=ALU.add)
+        def plus_beta(r, j):
+            if j == 0:
+                shifted[r] = k_pool.tile([P, TILES, HEADS, D], F32, name="shifted")
+            nc.gpsimd.tensor_tensor(out=shifted[r][:, j], in0=scaled[r][:, j], in1=gb_spread[:, 1], op=ALU.add)
 
-        def pair(w, r, j, a):
-            if w == Q:
-                return back[w, r, j][:, a]
-            return back[w, r, 0][:, j] if a == 0 else shifted[r][:, j]
+        def affined(w, r, j):
+            return back[r, j][:] if w == Q else shifted[r][:, j]
+
+        def epoch(w, r):
+            return r if w == Q else r + 1
 
         def moments(w, r, j, a):
-            if (w, r) not in stats:
-                stats[w, r] = small.tile([P, TILES, PAIRS, 6], F32, name="stats")
-            nc.vector.bn_stats(out=stats[w, r][:, j, a, :], in_=pair(w, r, j, a).rearrange("p h d -> p d h"))
+            e = epoch(w, r)
+            if e not in stats:
+                stats[e] = small.tile([P, 2, TILES, PAIRS, 6], F32, name="stats")
+            nc.vector.bn_stats(
+                out=stats[e][:, w, j, a, :], in_=affined(w, r, j)[:, 2 * a : 2 * a + 2, :].rearrange("p h d -> p d h")
+            )
 
-        def by_block(w, r):
-            return stats[w, r][:].rearrange("p j a (h s) -> p (j a h) s", s=3)
+        def by_block(e):
+            return stats[e][:].rearrange("p w j a (h s) -> p w (j a h) s", s=3)
 
         def one_over_std(w, r):
-            rstd[w, r] = small.tile([P, TILES * HEADS], F32, name="rstd")
+            e = epoch(w, r)
+            if e not in rstd:
+                rstd[e] = small.tile([P, 2, TILES * HEADS], F32, name="rstd")
             nc.scalar.activation(
-                out=rstd[w, r][:], in_=by_block(w, r)[:, :, 2], func=ACT.Abs_reciprocal_sqrt,
+                out=rstd[e][:, w, :], in_=by_block(e)[:, w, :, 2], func=ACT.Abs_reciprocal_sqrt,
                 bias=eps[:, w : w + 1], scale=(1.0 if w == Q else 1.0 / D),
             )
 
-        def minus_mean_over_std(w, r):
-            shift[w, r] = small.tile([P, TILES * HEADS], F32, name="shift")
+        def minus_mean_over_std(e):
+            shift[e] = small.tile([P, 2, TILES * HEADS], F32, name="shift")
+            ws = slice(0 if e < N_ROUNDS else 1, 2 if e > 0 else 1)
             nc.vector.scalar_tensor_tensor(
-                out=shift[w, r][:], in0=by_block(w, r)[:, :, 1], scalar=-1.0, in1=rstd[w, r][:],
+                out=shift[e][:, ws, :], in0=by_block(e)[:, ws, :, 1], scalar=-1.0, in1=rstd[e][:, ws, :],
                 op0=ALU.mult, op1=ALU.mult,
             )
 
         def normalise(w, r, j, h):
             if (w, r, j) not in feat:
                 feat[w, r, j] = feat_pool.tile([P, HEADS, D], F32, name="feat")
-            b = j * HEADS + h
-            out, value = feat[w, r, j][:, h, :], pair(w, r, j, h // 2)[:, h % 2, :]
+            e, b = epoch(w, r), j * HEADS + h
+            out, value = feat[w, r, j][:, h, :], affined(w, r, j)[:, h, :]
             engine = normaliser(w, r, j, h)
             if engine == "scalar":
                 nc.scalar.activation(
-                    out=out, in_=value, func=ACT.Identity, bias=shift[w, r][:, b : b + 1], scale=rstd[w, r][:, b : b + 1]
+                    out=out, in_=value, func=ACT.Identity, bias=shift[e][:, w, b : b + 1], scale=rstd[e][:, w, b : b + 1]
                 )
             elif engine == "gpsimd":
                 nc.gpsimd.tensor_scalar(
-                    out=out, in0=value, scalar1=rstd[w, r][:, b : b + 1], scalar2=shift[w, r][:, b : b + 1],
+                    out=out, in0=value, scalar1=rstd[e][:, w, b : b + 1], scalar2=shift[e][:, w, b : b + 1],
                     op0=ALU.mult, op1=ALU.add,
                 )
             else:
                 nc.vector.tensor_scalar(
-                    out=out, in0=value, scalar1=by_block(w, r)[:, b, 1:2], scalar2=rstd[w, r][:, b : b + 1],
+                    out=out, in0=value, scalar1=by_block(e)[:, w, b, 1:2], scalar2=rstd[e][:, w, b : b + 1],
                     op0=ALU.subtract, op1=ALU.mult,
                 )
 
@@ -264,76 +266,63 @@ def tile_rebasedlinearattention_pa_t_kernel(
             load_x(r)
 
         with tc.manual_schedule():
-            for r in range(-X_LEAD, N_ROUNDS):
-                old, ahead = r - 1, r + X_LEAD
-                if old >= 0:
-                    for j in range(TILES):
-                        moments(K, old, j, 1)
-                if r >= 0:
-                    project_features_first(Q, r)
-                    project_features_first(K, r)
-                    project_tokens_first(r)
-                if old >= 0:
-                    normalise_on("vector", Q, old, 1)
-                if r >= 0:
-                    affine(Q, r, 0)
-                    affine(Q, r, 1)
-                if old >= 0:
-                    one_over_std(K, old)
-                    minus_mean_over_std(Q, old)
-                    minus_mean_over_std(K, old)
-                if r >= 0:
-                    affine(K, r, 0)
+            for r in range(-X_LEAD, N_ROUNDS + 1):
+                ahead = r + X_LEAD
+                old_q, old_k = r - 1, r - 2
+                run, end_q, end_k = 0 <= r < N_ROUNDS, old_q >= 0, old_k >= 0
+                if run:
+                    project_q(r)
+                    project_k(r)
+                    affine(r, 0)
+                if end_q:
+                    one_over_std(Q, old_q)
+                if end_k:
+                    one_over_std(K, old_k)
+                if run:
+                    affine(r, 1)
                 if 0 <= r + 1 < N_ROUNDS:
                     quantise_x(r + 1)
-                if old >= 0:
-                    normalise_on("scalar", Q, old, 1)
-                    store(Q, old, 1)
-                    normalise_on("scalar", K, old, 0)
-                    normalise_on("scalar", K, old, 1)
-                if r >= 0:
-                    transpose_back(Q, r)
+                if end_q:
+                    minus_mean_over_std(old_q)
+                if end_k:
+                    for j in range(TILES):
+                        normalise_on("vector", K, old_k, j)
+                        normalise_on("gpsimd", K, old_k, j)
+                if end_q:
+                    for j in range(TILES):
+                        normalise_on("scalar", Q, old_q, j)
+                        store(Q, old_q, j)
+                if end_k:
+                    for j in range(TILES):
+                        normalise_on("scalar", K, old_k, j)
+                        store(K, old_k, j)
+                if run:
+                    transpose_back(r)
                     if r + LOAD_LEAD < N_ROUNDS:
                         load_x(r + LOAD_LEAD)
-                    times_gamma(r)
-                    plus_beta(r)
-                if old >= 0:
                     for j in range(TILES):
-                        normalise_on("gpsimd", K, old, j)
-                        store(K, old, j)
-                if r >= 0:
+                        times_gamma(r, j)
+                        plus_beta(r, j)
+                if old_q >= 0:
+                    for j in range(TILES):
+                        for a in range(PAIRS):
+                            moments(K, old_q, j, a)
+                if run:
                     for j in range(TILES):
                         for a in range(PAIRS):
                             moments(Q, r, j, a)
-                if r >= 0:
-                    transpose_back(K, r)
-                if ahead < N_ROUNDS:
-                    transpose_x(ahead, 0)
-                    copy_x(ahead, 0)
-                if r >= 0:
-                    moments(K, r, 0, 0)
-                    one_over_std(Q, r)
-                    if r == N_ROUNDS - 1:
-                        minus_mean_over_std(Q, r)
-                    moments(K, r, 1, 0)
-                if ahead < N_ROUNDS:
-                    transpose_x(ahead, 1)
-                if r == -1:
-                    spread_gamma_beta()
-                if 0 <= r < N_ROUNDS - 1:
-                    normalise_on("vector", Q, r, 0)
-                    store(Q, r, 0)
-                if ahead < N_ROUNDS:
-                    copy_x(ahead, 1)
+                for j in range(TILES):
+                    if ahead < N_ROUNDS:
+                        transpose_x(ahead, j)
+                    if r == -1 and j == 1:
+                        spread_gamma_beta()
+                    if ahead < N_ROUNDS:
+                        copy_x(ahead, j)
 
             last = N_ROUNDS - 1
-            for j in range(TILES):
-                moments(K, last, j, 1)
-            normalise_on("scalar", Q, last, 0)
-            store(Q, last, 0)
             one_over_std(K, last)
-            normalise_on("scalar", Q, last, 1)
-            store(Q, last, 1)
+            minus_mean_over_std(last + 1)
             for j in range(TILES):
                 normalise_on("vector", K, last, j)
+                normalise_on("scalar", K, last, j)
                 store(K, last, j)

@@ -37,9 +37,11 @@ def normaliser(w, r, j, h):
     if w == K and r == N_ROUNDS - 1:
         return ("scalar", "vector", "vector", "scalar")[h]
     if w == K and r == N_ROUNDS - 2:
-        return ("vector", "vector", "vector", "gpsimd")[h]
+        return "vector"
     if w == K:
-        return "gpsimd" if h == 3 or (h == 2 and j == 0) else "scalar"
+        return "gpsimd" if h == 3 and j == 1 else "scalar"
+    if h == 3 and j == 1:
+        return "vector"
     return "scalar"
 
 
@@ -284,6 +286,8 @@ def tile_rebasedlinearattention_pa_t_kernel(
                     quantise_x(r + 1)
                 if end_q:
                     minus_mean_over_std(old_q)
+                    for j in range(TILES):
+                        normalise_on("vector", Q, old_q, j)
                 if end_k:
                     for j in range(TILES):
                         normalise_on("vector", K, old_k, j)

@@ -28,6 +28,7 @@ N_ROUNDS = TOKENS // ROUND
 Q, K = 0, 1
 
 X_LEAD = 2
+WARM_UP = (6, 4)
 LOAD_LEAD = 5
 
 FLOPS = 2 * TOKENS * HID * 2 * COLS
@@ -63,6 +64,8 @@ def tile_rebasedlinearattention_pa_t_kernel(
         psum_in = ctx.enter_context(tc.psum_pool(name="psum_in", bufs=4))
         psum_back = ctx.enter_context(tc.psum_pool(name="psum_back", bufs=4))
 
+        still = const.tile([P, 512], BF16)
+        nc.vector.memset(still[:], 0.0)
         ident = const.tile([P, P], F32)
         make_identity(nc, ident[:])
         w_planes = const.tile([P, 2, PASSES, COLS], U8, align_bytes=64)
@@ -118,6 +121,13 @@ def tile_rebasedlinearattention_pa_t_kernel(
             )
             for h in range(HEADS):
                 nc.vector.tensor_copy(out=gb_spread[:, :, h, :], in_=bank[:, 0:2, :])
+
+        def keep_busy(n):
+            bank = psum_back.tile([P, HEADS, D], F32, name="back")
+            for i in range(n):
+                nc.tensor.matmul(
+                    out=bank[:].rearrange("p h d -> p (h d)"), lhsT=still[:, 0:P], rhs=still[:], start=True, stop=True
+                )
 
         def transpose_x(r, j):
             x_words = x_sb[r][:, j, :].bitcast(F32)
@@ -315,6 +325,8 @@ def tile_rebasedlinearattention_pa_t_kernel(
                     for j in range(TILES):
                         for a in range(PAIRS):
                             moments(Q, r, j, a)
+                if r < 0:
+                    keep_busy(WARM_UP[ahead])
                 for j in range(TILES):
                     if ahead < N_ROUNDS:
                         transpose_x(ahead, j)

@@ -40,7 +40,7 @@ def normaliser(w, r, j, h):
     if w == K and r == N_ROUNDS - 2:
         return "vector"
     if w == K:
-        return "gpsimd" if h == 3 and j == 1 else "scalar"
+        return "gpsimd" if h == 3 else "scalar"
     if h == 3 and j == 1:
         return "vector"
     return "scalar"

@@ -28,7 +28,7 @@ N_ROUNDS = TOKENS // ROUND
 Q, K = 0, 1
 
 X_LEAD = 2
-WARM_UP = (6, 4)
+WARM_UP = (6, 2)
 LOAD_LEAD = 5
 
 FLOPS = 2 * TOKENS * HID * 2 * COLS
@@ -81,7 +81,7 @@ def tile_rebasedlinearattention_pa_t_kernel(
         warm = const.tile([P, 2], F32)
         nc.scalar.activation(out=warm[:], in_=eps[:], func=ACT.Abs_reciprocal_sqrt)
         gb_column = const.tile([P, 2], F32)
-        gb_spread = const.tile([P, 2, HEADS, D], F32)
+        gb_spread = const.tile([P, 2, D], F32)
 
         x_sb, xt, grouped, x_codes, x_planes = {}, {}, {}, {}, {}
         product, u_t, back, scaled, shifted, feat = {}, {}, {}, {}, {}, {}
@@ -89,16 +89,17 @@ def tile_rebasedlinearattention_pa_t_kernel(
 
         def load_x(r):
             x_sb[r] = x_pool.tile([P, TILES, HID], BF16, name="x_sb")
-            nc.sync.dma_start(
-                out=x_sb[r][:],
-                in_=x_rows[r * ROUND : (r + 1) * ROUND, :].rearrange("(j p) k -> p j k", p=P),
-            )
+            rows = x_rows[r * ROUND : (r + 1) * ROUND, :].rearrange("(j p) k -> p j k", p=P)
+            for j in (0, 1) if r == 0 else (slice(0, TILES),):
+                nc.sync.dma_start(out=x_sb[r][:, j], in_=rows[:, j])
 
-        def load_weight(w, words, scales):
+        def load_codes(w, words):
             nc.sync.dma_start(
                 out=w_codes[:, w].bitcast(I32),
                 in_=words.rearrange("g p n t -> p g (n t)").bitcast(I32),
             )
+
+        def load_scales(w, scales):
             for b in range(4):
                 nc.sync.dma_start(
                     out=w_planes[32 * b : 32 * b + 4, w].bitcast(I32),
@@ -106,8 +107,8 @@ def tile_rebasedlinearattention_pa_t_kernel(
                 )
 
         def load_gamma_beta():
-            nc.sync.dma_start(out=gb_row[0:1, 0, :], in_=gamma.rearrange("(o d) -> o d", o=1))
-            nc.sync.dma_start(out=gb_row[0:1, 1, :], in_=beta.rearrange("(o d) -> o d", o=1))
+            nc.gpsimd.dma_start(out=gb_row[0:1, 0, :], in_=gamma.rearrange("(o d) -> o d", o=1))
+            nc.gpsimd.dma_start(out=gb_row[0:1, 1, :], in_=beta.rearrange("(o d) -> o d", o=1))
 
         def spread_gamma_beta():
             bank = psum_back.tile([P, HEADS, D], F32, name="back")
@@ -119,8 +120,10 @@ def tile_rebasedlinearattention_pa_t_kernel(
                 out=bank[:, 0:2, :].rearrange("p i d -> p (i d)"), lhsT=ones[:],
                 rhs=gb_row[:].rearrange("p i d -> p (i d)"), start=True, stop=True,
             )
-            for h in range(HEADS):
-                nc.vector.tensor_copy(out=gb_spread[:, :, h, :], in_=bank[:, 0:2, :])
+            nc.vector.tensor_copy(out=gb_spread[:], in_=bank[:, 0:2, :])
+
+        def for_all_heads(i):
+            return gb_spread[:, i : i + 1, :].to_broadcast([P, HEADS, D])
 
         def keep_busy(n):
             bank = psum_back.tile([P, HEADS, D], F32, name="back")
@@ -142,7 +145,8 @@ def tile_rebasedlinearattention_pa_t_kernel(
             words = (
                 grouped[r][:].rearrange("p g r t -> p (g r t)").bitcast(F32).rearrange("p (g r u) -> p g r u", g=PASSES, u=2)
             )
-            nc.scalar.copy(out=words[:, :, j * P : (j + 1) * P, :], in_=xt[r, j][:].rearrange("p (g u) r -> p g r u", u=2))
+            copy = nc.vector.tensor_copy if r < X_LEAD and j == 1 else nc.scalar.copy
+            copy(out=words[:, :, j * P : (j + 1) * P, :], in_=xt[r, j][:].rearrange("p (g u) r -> p g r u", u=2))
 
         def quantise_x(r):
             x_codes[r] = stage.tile([P, PASSES, ROUND], U32, align_bytes=64, name="x_codes")
@@ -198,12 +202,12 @@ def tile_rebasedlinearattention_pa_t_kernel(
         def times_gamma(r, j):
             if j == 0:
                 scaled[r] = k_pool.tile([P, TILES, HEADS, D], F32, name="scaled")
-            nc.vector.tensor_tensor(out=scaled[r][:, j], in0=product[K, r, j][:], in1=gb_spread[:, 0], op=ALU.mult)
+            nc.vector.tensor_tensor(out=scaled[r][:, j], in0=product[K, r, j][:], in1=for_all_heads(0), op=ALU.mult)
 
         def plus_beta(r, j):
             if j == 0:
                 shifted[r] = k_pool.tile([P, TILES, HEADS, D], F32, name="shifted")
-            nc.gpsimd.tensor_tensor(out=shifted[r][:, j], in0=scaled[r][:, j], in1=gb_spread[:, 1], op=ALU.add)
+            nc.gpsimd.tensor_tensor(out=shifted[r][:, j], in0=scaled[r][:, j], in1=for_all_heads(1), op=ALU.add)
 
         def affined(w, r, j):
             return back[r, j][:] if w == Q else shifted[r][:, j]
@@ -270,10 +274,12 @@ def tile_rebasedlinearattention_pa_t_kernel(
             nc.sync.dma_start(out=out_rows[w][t * P : (t + 1) * P, :], in_=feat[w, r, j][:].rearrange("p h d -> p (h d)"))
 
         load_x(0)
-        load_weight(Q, Wq_words, Wq_scales)
+        load_scales(Q, Wq_scales)
         load_x(1)
+        load_codes(Q, Wq_words)
+        load_codes(K, Wk_words)
         load_gamma_beta()
-        load_weight(K, Wk_words, Wk_scales)
+        load_scales(K, Wk_scales)
         for r in range(2, LOAD_LEAD):
             load_x(r)
 
@@ -327,13 +333,14 @@ def tile_rebasedlinearattention_pa_t_kernel(
                             moments(Q, r, j, a)
                 if r < 0:
                     keep_busy(WARM_UP[ahead])
-                for j in range(TILES):
-                    if ahead < N_ROUNDS:
-                        transpose_x(ahead, j)
-                    if r == -1 and j == 1:
-                        spread_gamma_beta()
-                    if ahead < N_ROUNDS:
-                        copy_x(ahead, j)
+                if ahead < N_ROUNDS:
+                    transpose_x(ahead, 0)
+                    copy_x(ahead, 0)
+                    transpose_x(ahead, 1)
+                if r == -1:
+                    spread_gamma_beta()
+                if ahead < N_ROUNDS:
+                    copy_x(ahead, 1)
 
             last = N_ROUNDS - 1
             one_over_std(K, last)

@@ -28,17 +28,17 @@ N_ROUNDS = TOKENS // ROUND
 Q, K = 0, 1
 
 X_LEAD = 2
-WARM_UP = (6, 2)
+WARM_UP = (4, 2)
 LOAD_LEAD = 5
 
 FLOPS = 2 * TOKENS * HID * 2 * COLS
 
 
 def normaliser(w, r, j, h):
-    if w == K and r == N_ROUNDS - 1:
-        return ("scalar", "vector", "vector", "scalar")[h]
+    if r == N_ROUNDS - 1:
+        return "scalar" if w == Q else "vector"
     if w == K and r == N_ROUNDS - 2:
-        return "vector"
+        return "gpsimd" if h == 3 else "scalar"
     if w == K:
         return "gpsimd" if h == 3 else "scalar"
     if h == 3 and j == 1:
@@ -65,7 +65,7 @@ def tile_rebasedlinearattention_pa_t_kernel(
         psum_back = ctx.enter_context(tc.psum_pool(name="psum_back", bufs=4))
 
         still = const.tile([P, 512], BF16)
-        nc.vector.memset(still[:], 0.0)
+        nc.vector.memset(still[:].bitcast(I32), 0)
         ident = const.tile([P, P], F32)
         make_identity(nc, ident[:])
         w_planes = const.tile([P, 2, PASSES, COLS], U8, align_bytes=64)
@@ -85,7 +85,7 @@ def tile_rebasedlinearattention_pa_t_kernel(
 
         x_sb, xt, grouped, x_codes, x_planes = {}, {}, {}, {}, {}
         product, u_t, back, scaled, shifted, feat = {}, {}, {}, {}, {}, {}
-        stats, rstd, shift = {}, {}, {}
+        stats, rstd, shift, finished = {}, {}, {}, {}
 
         def load_x(r):
             x_sb[r] = x_pool.tile([P, TILES, HID], BF16, name="x_sb")
@@ -107,8 +107,8 @@ def tile_rebasedlinearattention_pa_t_kernel(
                 )
 
         def load_gamma_beta():
-            nc.gpsimd.dma_start(out=gb_row[0:1, 0, :], in_=gamma.rearrange("(o d) -> o d", o=1))
-            nc.gpsimd.dma_start(out=gb_row[0:1, 1, :], in_=beta.rearrange("(o d) -> o d", o=1))
+            nc.sync.dma_start(out=gb_row[0:1, 0, :], in_=gamma.rearrange("(o d) -> o d", o=1))
+            nc.sync.dma_start(out=gb_row[0:1, 1, :], in_=beta.rearrange("(o d) -> o d", o=1))
 
         def spread_gamma_beta():
             bank = psum_back.tile([P, HEADS, D], F32, name="back")
@@ -157,22 +157,22 @@ def tile_rebasedlinearattention_pa_t_kernel(
                 in_=grouped[r][:].rearrange("p g r t -> p (g r t)"),
             )
 
-        def project_q(r):
+        def project_features_first(w, r):
             for a in range(PAIRS):
-                product[Q, r, a] = psum_in.tile([P, 2, ROUND], F32, name="bank")
+                product[w, r, a] = psum_in.tile([P, 2, ROUND], F32, name="bank")
                 for i in range(2):
                     h = 2 * a + i
                     for g in range(PASSES):
                         nc.tensor.matmul_mx(
-                            out=product[Q, r, a][:, i, :],
-                            lhsT=w_codes[:, Q, g, h * D : (h + 1) * D].bitcast(FP8X4),
-                            lhsT_scale=w_planes[:, Q, g, h * D : (h + 1) * D],
+                            out=product[w, r, a][:, i, :],
+                            lhsT=w_codes[:, w, g, h * D : (h + 1) * D].bitcast(FP8X4),
+                            lhsT_scale=w_planes[:, w, g, h * D : (h + 1) * D],
                             rhs=x_codes[r][:, g, :].bitcast(FP8X4),
                             rhs_scale=x_planes[r][:, g, :],
                             start=(g == 0), stop=(g == PASSES - 1),
                         )
 
-        def project_k(r):
+        def project_tokens_first(r):
             for j in range(TILES):
                 product[K, r, j] = psum_in.tile([P, HEADS, D], F32, name="bank")
                 for g in range(PASSES):
@@ -185,19 +185,20 @@ def tile_rebasedlinearattention_pa_t_kernel(
                         start=(g == 0), stop=(g == PASSES - 1),
                     )
 
-        def affine(r, a):
+        def affine(w, r, a):
             if a == 0:
-                u_t[r] = u_pool.tile([P, HEADS, ROUND], F32, name="u_t")
+                u_t[w, r] = u_pool.tile([P, HEADS, ROUND], F32, name="u_t")
             nc.scalar.activation(
-                out=u_t[r][:, 2 * a : 2 * a + 2, :], in_=product[Q, r, a][:],
+                out=u_t[w, r][:, 2 * a : 2 * a + 2, :], in_=product[w, r, a][:],
                 func=ACT.Identity, bias=gb_column[:, 1:2], scale=gb_column[:, 0:1],
             )
 
-        def transpose_back(r):
+        def transpose_back(w, r):
+            pool, name = (psum_back, "back") if w == Q else (psum_in, "bank")
             for j in range(TILES):
-                back[r, j] = psum_back.tile([P, HEADS, D], F32, name="back")
+                back[w, r, j] = pool.tile([P, HEADS, D], F32, name=name)
                 for h in range(HEADS):
-                    nc.tensor.transpose(back[r, j][:, h, :], u_t[r][:, h, j * P : (j + 1) * P], ident[:])
+                    nc.tensor.transpose(back[w, r, j][:, h, :], u_t[w, r][:, h, j * P : (j + 1) * P], ident[:])
 
         def times_gamma(r, j):
             if j == 0:
@@ -210,18 +211,20 @@ def tile_rebasedlinearattention_pa_t_kernel(
             nc.gpsimd.tensor_tensor(out=shifted[r][:, j], in0=scaled[r][:, j], in1=for_all_heads(1), op=ALU.add)
 
         def affined(w, r, j):
-            return back[r, j][:] if w == Q else shifted[r][:, j]
+            return shifted[r][:, j] if (w, r, j) not in back else back[w, r, j][:]
 
         def epoch(w, r):
             return r if w == Q else r + 1
 
-        def moments(w, r, j, a):
+        def moments(w, r):
             e = epoch(w, r)
             if e not in stats:
                 stats[e] = small.tile([P, 2, TILES, PAIRS, 6], F32, name="stats")
-            nc.vector.bn_stats(
-                out=stats[e][:, w, j, a, :], in_=affined(w, r, j)[:, 2 * a : 2 * a + 2, :].rearrange("p h d -> p d h")
-            )
+            for j in range(TILES):
+                for a in range(PAIRS):
+                    nc.vector.bn_stats(
+                        out=stats[e][:, w, j, a, :], in_=affined(w, r, j)[:, 2 * a : 2 * a + 2, :].rearrange("p h d -> p d h")
+                    )
 
         def by_block(e):
             return stats[e][:].rearrange("p w j a (h s) -> p w (j a h) s", s=3)
@@ -235,9 +238,9 @@ def tile_rebasedlinearattention_pa_t_kernel(
                 bias=eps[:, w : w + 1], scale=(1.0 if w == Q else 1.0 / D),
             )
 
-        def minus_mean_over_std(e):
-            shift[e] = small.tile([P, 2, TILES * HEADS], F32, name="shift")
-            ws = slice(0 if e < N_ROUNDS else 1, 2 if e > 0 else 1)
+        def minus_mean_over_std(e, ws):
+            if e not in shift:
+                shift[e] = small.tile([P, 2, TILES * HEADS], F32, name="shift")
             nc.vector.scalar_tensor_tensor(
                 out=shift[e][:, ws, :], in0=by_block(e)[:, ws, :, 1], scalar=-1.0, in1=rstd[e][:, ws, :],
                 op0=ALU.mult, op1=ALU.mult,
@@ -264,73 +267,63 @@ def tile_rebasedlinearattention_pa_t_kernel(
                     op0=ALU.subtract, op1=ALU.mult,
                 )
 
-        def normalise_on(engine, w, r, j):
-            for h in range(HEADS):
-                if normaliser(w, r, j, h) == engine:
-                    normalise(w, r, j, h)
-
-        def store(w, r, j):
-            t = r * TILES + j
-            nc.sync.dma_start(out=out_rows[w][t * P : (t + 1) * P, :], in_=feat[w, r, j][:].rearrange("p h d -> p (h d)"))
+        def normalise_on(engine, w, r):
+            for j in range(TILES):
+                for h in range(HEADS):
+                    if normaliser(w, r, j, h) == engine:
+                        normalise(w, r, j, h)
+                        finished[w, r, j] = finished.get((w, r, j), 0) + 1
+                        if finished[w, r, j] == HEADS:
+                            t = r * TILES + j
+                            nc.sync.dma_start(
+                                out=out_rows[w][t * P : (t + 1) * P, :], in_=feat[w, r, j][:].rearrange("p h d -> p (h d)")
+                            )
 
         load_x(0)
         load_scales(Q, Wq_scales)
         load_x(1)
         load_codes(Q, Wq_words)
-        load_codes(K, Wk_words)
         load_gamma_beta()
+        load_codes(K, Wk_words)
         load_scales(K, Wk_scales)
         for r in range(2, LOAD_LEAD):
             load_x(r)
 
         with tc.manual_schedule():
-            for r in range(-X_LEAD, N_ROUNDS + 1):
-                ahead = r + X_LEAD
-                old_q, old_k = r - 1, r - 2
-                run, end_q, end_k = 0 <= r < N_ROUNDS, old_q >= 0, old_k >= 0
-                if run:
-                    project_q(r)
-                    project_k(r)
-                    affine(r, 0)
-                if end_q:
-                    one_over_std(Q, old_q)
-                if end_k:
-                    one_over_std(K, old_k)
-                if run:
-                    affine(r, 1)
-                if 0 <= r + 1 < N_ROUNDS:
+            for r in range(-X_LEAD, N_ROUNDS - 1):
+                old, older, ahead = r - 1, r - 2, r + X_LEAD
+                if r >= 0:
+                    project_features_first(Q, r)
+                    project_tokens_first(r)
+                    affine(Q, r, 0)
+                if old >= 0:
+                    one_over_std(Q, old)
+                if older >= 0:
+                    one_over_std(K, older)
+                if r >= 0:
+                    affine(Q, r, 1)
+                if r + 1 >= 0:
                     quantise_x(r + 1)
-                if end_q:
-                    minus_mean_over_std(old_q)
-                    for j in range(TILES):
-                        normalise_on("vector", Q, old_q, j)
-                if end_k:
-                    for j in range(TILES):
-                        normalise_on("vector", K, old_k, j)
-                        normalise_on("gpsimd", K, old_k, j)
-                if end_q:
-                    for j in range(TILES):
-                        normalise_on("scalar", Q, old_q, j)
-                        store(Q, old_q, j)
-                if end_k:
-                    for j in range(TILES):
-                        normalise_on("scalar", K, old_k, j)
-                        store(K, old_k, j)
-                if run:
-                    transpose_back(r)
+                if old >= 0:
+                    minus_mean_over_std(old, slice(0, 2 if older >= 0 else 1))
+                    normalise_on("vector", Q, old)
+                if older >= 0:
+                    normalise_on("gpsimd", K, older)
+                if old >= 0:
+                    normalise_on("scalar", Q, old)
+                if older >= 0:
+                    normalise_on("scalar", K, older)
+                if r >= 0:
+                    transpose_back(Q, r)
                     if r + LOAD_LEAD < N_ROUNDS:
                         load_x(r + LOAD_LEAD)
                     for j in range(TILES):
                         times_gamma(r, j)
                         plus_beta(r, j)
-                if old_q >= 0:
-                    for j in range(TILES):
-                        for a in range(PAIRS):
-                            moments(K, old_q, j, a)
-                if run:
-                    for j in range(TILES):
-                        for a in range(PAIRS):
-                            moments(Q, r, j, a)
+                if old >= 0:
+                    moments(K, old)
+                if r >= 0:
+                    moments(Q, r)
                 if r < 0:
                     keep_busy(WARM_UP[ahead])
                 if ahead < N_ROUNDS:
@@ -342,10 +335,31 @@ def tile_rebasedlinearattention_pa_t_kernel(
                 if ahead < N_ROUNDS:
                     copy_x(ahead, 1)
 
-            last = N_ROUNDS - 1
+            last, old, older = N_ROUNDS - 1, N_ROUNDS - 2, N_ROUNDS - 3
+            for w in (Q, K):
+                project_features_first(w, last)
+                for a in range(PAIRS):
+                    affine(w, last, a)
+            moments(K, old)
+            one_over_std(Q, old)
+            one_over_std(K, older)
+            one_over_std(K, old)
+            minus_mean_over_std(old, slice(0, 2))
+            minus_mean_over_std(last, slice(1, 2))
+            normalise_on("vector", Q, old)
+            normalise_on("gpsimd", K, older)
+            normalise_on("scalar", Q, old)
+            transpose_back(Q, last)
+            transpose_back(K, last)
+            moments(Q, last)
+            normalise_on("scalar", K, older)
+            normalise_on("gpsimd", K, old)
+            one_over_std(Q, last)
+            moments(K, last)
+            minus_mean_over_std(last, slice(0, 1))
+            normalise_on("scalar", K, old)
             one_over_std(K, last)
-            minus_mean_over_std(last + 1)
-            for j in range(TILES):
-                normalise_on("vector", K, last, j)
-                normalise_on("scalar", K, last, j)
-                store(K, last, j)
+            minus_mean_over_std(last + 1, slice(1, 2))
+            normalise_on("scalar", Q, last)
+            normalise_on("vector", K, last)
+            normalise_on("scalar", K, last)

@@ -41,9 +41,7 @@ def normaliser(w, r, j, h):
         return "gpsimd" if h == 3 else "scalar"
     if w == K:
         return "gpsimd" if h == 3 else "scalar"
-    if h == 3 and j == 1:
-        return "vector"
-    return "scalar"
+    return "vector" if h == 3 else "scalar"
 
 
 def tile_rebasedlinearattention_pa_t_kernel(
@@ -309,10 +307,10 @@ def tile_rebasedlinearattention_pa_t_kernel(
                     normalise_on("vector", Q, old)
                 if older >= 0:
                     normalise_on("gpsimd", K, older)
-                if old >= 0:
-                    normalise_on("scalar", Q, old)
                 if older >= 0:
                     normalise_on("scalar", K, older)
+                if old >= 0:
+                    normalise_on("scalar", Q, old)
                 if r >= 0:
                     transpose_back(Q, r)
                     if r + LOAD_LEAD < N_ROUNDS:

@@ -40,8 +40,8 @@ def normaliser(w, r, j, h):
     if w == K and r == N_ROUNDS - 2:
         return "gpsimd" if h == 3 else "scalar"
     if w == K:
-        return "gpsimd" if h == 3 else "scalar"
-    return "vector" if h == 3 else "scalar"
+        return "gpsimd" if h == 3 and (j == 1 or r % 2 == 1) else "scalar"
+    return "vector" if h == 3 and (j == 1 or r % 2 == 1) else "scalar"
 
 
 def tile_rebasedlinearattention_pa_t_kernel(

from contextlib import ExitStack

import concourse.mybir as mybir
from concourse.masks import make_identity

BF16 = mybir.dt.bfloat16
F32 = mybir.dt.float32
I32 = mybir.dt.int32
U32 = mybir.dt.uint32
U8 = mybir.dt.uint8
FP8X4 = mybir.dt.float8_e4m3fn_x4
ALU = mybir.AluOpType
ACT = mybir.ActivationFunctionType

P = 128
TOKENS = 4 * 1024
HID = 1024
K_PASS = 512
PASSES = HID // K_PASS
HEADS = 4
PAIRS = HEADS // 2
D = 128
COLS = HEADS * D
LN_EPS = 1e-5
TILES = 2
ROUND = TILES * P
N_ROUNDS = TOKENS // ROUND
Q, K = 0, 1

X_LEAD = 2
WARM_UP = (4, 2)
LOAD_LEAD = 5

FLOPS = 2 * TOKENS * HID * 2 * COLS


def normaliser(w, r, j, h):
    if r == N_ROUNDS - 1:
        return "scalar" if w == Q else "vector"
    if w == K and r == N_ROUNDS - 2:
        return "gpsimd" if h == 3 else "scalar"
    if w == K:
        return "gpsimd" if h == 3 and (j == 1 or r % 2 == 1) else "scalar"
    return "vector" if h == 3 and (j == 1 or r % 2 == 1) else "scalar"


def tile_rebasedlinearattention_pa_t_kernel(
    tc, hidden_states, Wq_words, Wq_scales, Wk_words, Wk_scales, gamma, beta, out_0, out_1
):
    nc = tc.nc
    x_rows = hidden_states.rearrange("b t k -> (b t) k")
    out_rows = [o.rearrange("b t h d -> (b t) (h d)") for o in (out_0, out_1)]

    with ExitStack() as ctx:
        const = ctx.enter_context(tc.tile_pool(name="const", bufs=1))
        x_pool = ctx.enter_context(tc.tile_pool(name="x", bufs=LOAD_LEAD - X_LEAD + 2))
        stage = ctx.enter_context(tc.tile_pool(name="stage", bufs=4))
        u_pool = ctx.enter_context(tc.tile_pool(name="u", bufs=4))
        k_pool = ctx.enter_context(tc.tile_pool(name="k", bufs=4))
        feat_pool = ctx.enter_context(tc.tile_pool(name="feat", bufs=12))
        small = ctx.enter_context(tc.tile_pool(name="small", bufs=8))
        psum_in = ctx.enter_context(tc.psum_pool(name="psum_in", bufs=4))
        psum_back = ctx.enter_context(tc.psum_pool(name="psum_back", bufs=4))

        still = const.tile([P, 512], BF16)
        nc.vector.memset(still[:].bitcast(I32), 0)
        ident = const.tile([P, P], F32)
        make_identity(nc, ident[:])
        w_planes = const.tile([P, 2, PASSES, COLS], U8, align_bytes=64)
        nc.vector.memset(w_planes[:].rearrange("p w g n -> p (w g n)").bitcast(I32), 0)
        w_codes = const.tile([P, 2, PASSES, COLS], U32, align_bytes=64)
        eps = const.tile([P, 2], F32)
        nc.vector.memset(eps[:, Q : Q + 1], D * LN_EPS)
        nc.vector.memset(eps[:, K : K + 1], LN_EPS)
        gb_row = const.tile([P, 2, D], BF16)
        nc.vector.memset(gb_row[:], 0.0)
        ones = const.tile([P, P], BF16)
        nc.vector.memset(ones[:], 1.0)
        warm = const.tile([P, 2], F32)
        nc.scalar.activation(out=warm[:], in_=eps[:], func=ACT.Abs_reciprocal_sqrt)
        gb_column = const.tile([P, 2], F32)
        gb_spread = const.tile([P, 2, D], F32)

        x_sb, xt, grouped, x_codes, x_planes = {}, {}, {}, {}, {}
        product, u_t, back, scaled, shifted, feat = {}, {}, {}, {}, {}, {}
        stats, rstd, shift, finished = {}, {}, {}, {}

        def load_x(r):
            x_sb[r] = x_pool.tile([P, TILES, HID], BF16, name="x_sb")
            rows = x_rows[r * ROUND : (r + 1) * ROUND, :].rearrange("(j p) k -> p j k", p=P)
            for j in (0, 1) if r == 0 else (slice(0, TILES),):
                nc.sync.dma_start(out=x_sb[r][:, j], in_=rows[:, j])

        def load_codes(w, words):
            nc.sync.dma_start(
                out=w_codes[:, w].bitcast(I32),
                in_=words.rearrange("g p n t -> p g (n t)").bitcast(I32),
            )

        def load_scales(w, scales):
            for b in range(4):
                nc.sync.dma_start(
                    out=w_planes[32 * b : 32 * b + 4, w].bitcast(I32),
                    in_=scales[:, 4 * b : 4 * b + 4, :].rearrange("g r n -> r g n").bitcast(I32),
                )

        def load_gamma_beta():
            nc.sync.dma_start(out=gb_row[0:1, 0, :], in_=gamma.rearrange("(o d) -> o d", o=1))
            nc.sync.dma_start(out=gb_row[0:1, 1, :], in_=beta.rearrange("(o d) -> o d", o=1))

        def spread_gamma_beta():
            bank = psum_back.tile([P, HEADS, D], F32, name="back")
            for i in range(2):
                nc.tensor.matmul(out=bank[:, i, 0:2], lhsT=gb_row[:, i, :], rhs=ones[:, 0:2], start=True, stop=True)
            nc.vector.tensor_copy(out=gb_column[:], in_=bank[:, 0:2, 0])
            bank = psum_back.tile([P, HEADS, D], F32, name="back")
            nc.tensor.matmul(
                out=bank[:, 0:2, :].rearrange("p i d -> p (i d)"), lhsT=ones[:],
                rhs=gb_row[:].rearrange("p i d -> p (i d)"), start=True, stop=True,
            )
            nc.vector.tensor_copy(out=gb_spread[:], in_=bank[:, 0:2, :])

        def for_all_heads(i):
            return gb_spread[:, i : i + 1, :].to_broadcast([P, HEADS, D])

        def keep_busy(n):
            bank = psum_back.tile([P, HEADS, D], F32, name="back")
            for i in range(n):
                nc.tensor.matmul(
                    out=bank[:].rearrange("p h d -> p (h d)"), lhsT=still[:, 0:P], rhs=still[:], start=True, stop=True
                )

        def transpose_x(r, j):
            x_words = x_sb[r][:, j, :].bitcast(F32)
            xt[r, j] = psum_in.tile([P, PASSES * 2, P], F32, name="bank")
            for g in range(PASSES):
                for u in range(2):
                    nc.tensor.transpose(xt[r, j][:, 2 * g + u, :], x_words[:, 256 * g + u : 256 * (g + 1) : 2], ident[:])

        def copy_x(r, j):
            if j == 0:
                grouped[r] = stage.tile([P, PASSES, ROUND, 4], BF16, align_bytes=64, name="grouped")
            words = (
                grouped[r][:].rearrange("p g r t -> p (g r t)").bitcast(F32).rearrange("p (g r u) -> p g r u", g=PASSES, u=2)
            )
            copy = nc.vector.tensor_copy if r < X_LEAD and j == 1 else nc.scalar.copy
            copy(out=words[:, :, j * P : (j + 1) * P, :], in_=xt[r, j][:].rearrange("p (g u) r -> p g r u", u=2))

        def quantise_x(r):
            x_codes[r] = stage.tile([P, PASSES, ROUND], U32, align_bytes=64, name="x_codes")
            x_planes[r] = stage.tile([P, PASSES, ROUND], U8, align_bytes=64, name="x_planes")
            nc.vector.quantize_mx(
                out=x_codes[r][:].rearrange("p g r -> p (g r)").bitcast(FP8X4),
                scales=x_planes[r][:].rearrange("p g r -> p (g r)"),
                in_=grouped[r][:].rearrange("p g r t -> p (g r t)"),
            )

        def project_features_first(w, r):
            for a in range(PAIRS):
                product[w, r, a] = psum_in.tile([P, 2, ROUND], F32, name="bank")
                for i in range(2):
                    h = 2 * a + i
                    for g in range(PASSES):
                        nc.tensor.matmul_mx(
                            out=product[w, r, a][:, i, :],
                            lhsT=w_codes[:, w, g, h * D : (h + 1) * D].bitcast(FP8X4),
                            lhsT_scale=w_planes[:, w, g, h * D : (h + 1) * D],
                            rhs=x_codes[r][:, g, :].bitcast(FP8X4),
                            rhs_scale=x_planes[r][:, g, :],
                            start=(g == 0), stop=(g == PASSES - 1),
                        )

        def project_tokens_first(r):
            for j in range(TILES):
                product[K, r, j] = psum_in.tile([P, HEADS, D], F32, name="bank")
                for g in range(PASSES):
                    nc.tensor.matmul_mx(
                        out=product[K, r, j][:].rearrange("p h d -> p (h d)"),
                        lhsT=x_codes[r][:, g, j * P : (j + 1) * P].bitcast(FP8X4),
                        lhsT_scale=x_planes[r][:, g, j * P : (j + 1) * P],
                        rhs=w_codes[:, K, g, :].bitcast(FP8X4),
                        rhs_scale=w_planes[:, K, g, :],
                        start=(g == 0), stop=(g == PASSES - 1),
                    )

        def affine(w, r, a):
            if a == 0:
                u_t[w, r] = u_pool.tile([P, HEADS, ROUND], F32, name="u_t")
            nc.scalar.activation(
                out=u_t[w, r][:, 2 * a : 2 * a + 2, :], in_=product[w, r, a][:],
                func=ACT.Identity, bias=gb_column[:, 1:2], scale=gb_column[:, 0:1],
            )

        def transpose_back(w, r):
            pool, name = (psum_back, "back") if w == Q else (psum_in, "bank")
            for j in range(TILES):
                back[w, r, j] = pool.tile([P, HEADS, D], F32, name=name)
                for h in range(HEADS):
                    nc.tensor.transpose(back[w, r, j][:, h, :], u_t[w, r][:, h, j * P : (j + 1) * P], ident[:])

        def times_gamma(r, j):
            if j == 0:
                scaled[r] = k_pool.tile([P, TILES, HEADS, D], F32, name="scaled")
            nc.vector.tensor_tensor(out=scaled[r][:, j], in0=product[K, r, j][:], in1=for_all_heads(0), op=ALU.mult)

        def plus_beta(r, j):
            if j == 0:
                shifted[r] = k_pool.tile([P, TILES, HEADS, D], F32, name="shifted")
            nc.gpsimd.tensor_tensor(out=shifted[r][:, j], in0=scaled[r][:, j], in1=for_all_heads(1), op=ALU.add)

        def affined(w, r, j):
            return shifted[r][:, j] if (w, r, j) not in back else back[w, r, j][:]

        def epoch(w, r):
            return r if w == Q else r + 1

        def moments(w, r):
            e = epoch(w, r)
            if e not in stats:
                stats[e] = small.tile([P, 2, TILES, PAIRS, 6], F32, name="stats")
            for j in range(TILES):
                for a in range(PAIRS):
                    nc.vector.bn_stats(
                        out=stats[e][:, w, j, a, :], in_=affined(w, r, j)[:, 2 * a : 2 * a + 2, :].rearrange("p h d -> p d h")
                    )

        def by_block(e):
            return stats[e][:].rearrange("p w j a (h s) -> p w (j a h) s", s=3)

        def one_over_std(w, r):
            e = epoch(w, r)
            if e not in rstd:
                rstd[e] = small.tile([P, 2, TILES * HEADS], F32, name="rstd")
            nc.scalar.activation(
                out=rstd[e][:, w, :], in_=by_block(e)[:, w, :, 2], func=ACT.Abs_reciprocal_sqrt,
                bias=eps[:, w : w + 1], scale=(1.0 if w == Q else 1.0 / D),
            )

        def minus_mean_over_std(e, ws):
            if e not in shift:
                shift[e] = small.tile([P, 2, TILES * HEADS], F32, name="shift")
            nc.vector.scalar_tensor_tensor(
                out=shift[e][:, ws, :], in0=by_block(e)[:, ws, :, 1], scalar=-1.0, in1=rstd[e][:, ws, :],
                op0=ALU.mult, op1=ALU.mult,
            )

        def normalise(w, r, j, h):
            if (w, r, j) not in feat:
                feat[w, r, j] = feat_pool.tile([P, HEADS, D], F32, name="feat")
            e, b = epoch(w, r), j * HEADS + h
            out, value = feat[w, r, j][:, h, :], affined(w, r, j)[:, h, :]
            engine = normaliser(w, r, j, h)
            if engine == "scalar":
                nc.scalar.activation(
                    out=out, in_=value, func=ACT.Identity, bias=shift[e][:, w, b : b + 1], scale=rstd[e][:, w, b : b + 1]
                )
            elif engine == "gpsimd":
                nc.gpsimd.tensor_scalar(
                    out=out, in0=value, scalar1=rstd[e][:, w, b : b + 1], scalar2=shift[e][:, w, b : b + 1],
                    op0=ALU.mult, op1=ALU.add,
                )
            else:
                nc.vector.tensor_scalar(
                    out=out, in0=value, scalar1=by_block(e)[:, w, b, 1:2], scalar2=rstd[e][:, w, b : b + 1],
                    op0=ALU.subtract, op1=ALU.mult,
                )

        def normalise_on(engine, w, r):
            for j in range(TILES):
                for h in range(HEADS):
                    if normaliser(w, r, j, h) == engine:
                        normalise(w, r, j, h)
                        finished[w, r, j] = finished.get((w, r, j), 0) + 1
                        if finished[w, r, j] == HEADS:
                            t = r * TILES + j
                            nc.sync.dma_start(
                                out=out_rows[w][t * P : (t + 1) * P, :], in_=feat[w, r, j][:].rearrange("p h d -> p (h d)")
                            )

        load_x(0)
        load_scales(Q, Wq_scales)
        load_x(1)
        load_codes(Q, Wq_words)
        load_gamma_beta()
        load_codes(K, Wk_words)
        load_scales(K, Wk_scales)
        for r in range(2, LOAD_LEAD):
            load_x(r)

        with tc.manual_schedule():
            for r in range(-X_LEAD, N_ROUNDS - 1):
                old, older, ahead = r - 1, r - 2, r + X_LEAD
                if r >= 0:
                    project_features_first(Q, r)
                    project_tokens_first(r)
                    affine(Q, r, 0)
                if old >= 0:
                    one_over_std(Q, old)
                if older >= 0:
                    one_over_std(K, older)
                if r >= 0:
                    affine(Q, r, 1)
                if r + 1 >= 0:
                    quantise_x(r + 1)
                if old >= 0:
                    minus_mean_over_std(old, slice(0, 2 if older >= 0 else 1))
                    normalise_on("vector", Q, old)
                if older >= 0:
                    normalise_on("gpsimd", K, older)
                if older >= 0:
                    normalise_on("scalar", K, older)
                if old >= 0:
                    normalise_on("scalar", Q, old)
                if r >= 0:
                    transpose_back(Q, r)
                    if r + LOAD_LEAD < N_ROUNDS:
                        load_x(r + LOAD_LEAD)
                    for j in range(TILES):
                        times_gamma(r, j)
                        plus_beta(r, j)
                if old >= 0:
                    moments(K, old)
                if r >= 0:
                    moments(Q, r)
                if r < 0:
                    keep_busy(WARM_UP[ahead])
                if ahead < N_ROUNDS:
                    transpose_x(ahead, 0)
                    copy_x(ahead, 0)
                    transpose_x(ahead, 1)
                if r == -1:
                    spread_gamma_beta()
                if ahead < N_ROUNDS:
                    copy_x(ahead, 1)

            last, old, older = N_ROUNDS - 1, N_ROUNDS - 2, N_ROUNDS - 3
            for w in (Q, K):
                project_features_first(w, last)
                for a in range(PAIRS):
                    affine(w, last, a)
            moments(K, old)
            one_over_std(Q, old)
            one_over_std(K, older)
            one_over_std(K, old)
            minus_mean_over_std(old, slice(0, 2))
            minus_mean_over_std(last, slice(1, 2))
            normalise_on("vector", Q, old)
            normalise_on("gpsimd", K, older)
            normalise_on("scalar", Q, old)
            transpose_back(Q, last)
            transpose_back(K, last)
            moments(Q, last)
            normalise_on("scalar", K, older)
            normalise_on("gpsimd", K, old)
            one_over_std(Q, last)
            moments(K, last)
            minus_mean_over_std(last, slice(0, 1))
            normalise_on("scalar", K, old)
            one_over_std(K, last)
            minus_mean_over_std(last + 1, slice(1, 2))
            normalise_on("scalar", Q, last)
            normalise_on("vector", K, last)
            normalise_on("scalar", K, last)
